import numpy as np
import ml_dtypes


def mxq(x, axis, fmt="e4m3"):
    dtype, down = {"e4m3": (ml_dtypes.float8_e4m3fn, 7), "e5m2": (ml_dtypes.float8_e5m2, 14)}[fmt]
    v = np.moveaxis(np.asarray(x, np.float32).astype(ml_dtypes.bfloat16).astype(np.float64), axis, -1)
    blocks = v.reshape(v.shape[:-1] + (-1, 32))
    amax = np.abs(blocks).max(-1, keepdims=True)
    byte = np.maximum(np.where(amax > 0, np.frexp(amax)[1] - 1 + 127, 0) - down, 1)
    scale = np.exp2(byte - 127.0)
    codes = (blocks / scale).astype(np.float32).astype(dtype).astype(np.float64)
    return np.moveaxis((codes * scale).reshape(v.shape), -1, axis)


WIDE = False


def mx_kscale(k):
    if not WIDE:
        return np.ones(k)
    levels = np.array([10, -10, 5, -5, 0])
    if k % 512:
        return np.exp2(np.random.permutation(np.resize(levels, k // 32))).repeat(32)
    a = np.empty((k // 512, 16))
    for p in range(k // 512):
        a[p, :8] = np.random.permutation(np.resize(levels, 8))
        for g in range(8):
            far = levels[np.abs(levels - a[p, g]) >= 10]
            a[p, g + 8] = far[np.random.randint(len(far))]
    return np.exp2(a.ravel()).repeat(32)


BF16 = ml_dtypes.bfloat16


def bf(x):
    return np.asarray(x, np.float32).astype(BF16)


def f64(x):
    return np.asarray(x).astype(np.float64)


B, N, D, F, M1, M2 = 4, 128, 512, 2048, 3, 5
D2 = D + D


def silu(v):
    return v / (1.0 + np.exp(-v))


def draw0():
    s, t = mx_kscale(D), mx_kscale(D2)
    return {"h": bf(np.random.standard_normal((B, N, D)) * t[:D]),
            "x1": bf(np.random.standard_normal((B, N, D, M1)) * s[:, None]),
            "pre1": bf(np.random.standard_normal((D, D)) / np.sqrt(D) / s[:, None] * t[D:]),
            "w1_0": bf(np.random.standard_normal((D2, F)) / np.sqrt(D2) / t[:, None]),
            "b1_0": bf(np.random.standard_normal(F) * 0.2)}


def core(h, x1, pre1, w1_0, b1_0):
    xt = f64(x1).swapaxes(-1, -2).reshape(B * N * M1, D)
    pm = (mxq(xt, 1, "e4m3") @ mxq(f64(pre1), 0, "e4m3")).reshape(B, N, M1, D)
    inv = np.sqrt(np.sum(pm * pm, axis=-2))
    mlp_in = np.concatenate([f64(h), inv], axis=-1)
    return silu((mxq(mlp_in, 2, "e4m3") @ mxq(f64(w1_0), 0, "e4m3")) + f64(b1_0))


def e4m3fn_bytes(y):
    return np.clip(np.asarray(y, np.float64), -448.0, 448.0).astype(np.float32).astype(ml_dtypes.float8_e4m3fn).view(np.uint8)


def e4m3fn_values(b):
    return np.asarray(b, np.uint8).view(ml_dtypes.float8_e4m3fn).astype(np.float64)


def setup_inputs():
    d = draw0()
    x0 = np.asarray(d['w1_0']).astype(np.float64)
    s = (np.max(np.abs(x0), axis=(1,), keepdims=True) / 448.0).astype(np.float32)
    out = {}
    for k, v in d.items():
        if k == 'w1_0':
            out['w1_0_bytes'] = e4m3fn_bytes(x0 / s.astype(np.float64))
            out['w1_0_scale'] = s
        else:
            out[k] = v
    return out


def reference(h, x1, pre1, w1_0_bytes, w1_0_scale, b1_0):
    return core(h, x1, pre1, e4m3fn_values(w1_0_bytes) * w1_0_scale.astype(np.float64), b1_0)

@@ -1,0 +1,289 @@
+from contextlib import ExitStack
+
+import concourse.mybir as mybir
+from concourse.masks import make_identity
+
+F32 = mybir.dt.float32
+BF16 = mybir.dt.bfloat16
+U8 = mybir.dt.uint8
+U32 = mybir.dt.uint32
+FP8 = mybir.dt.float8_e4m3fn
+FP8X4 = mybir.dt.float8_e4m3fn_x4
+ACT = mybir.ActivationFunctionType
+ALU = mybir.AluOpType
+
+P = 128
+TOK = 512
+D = 512
+M1 = 3
+FF = 2048
+NT = TOK // P
+FQ = 512
+NQ = FF // FQ
+
+FLOPS = 2 * TOK * M1 * D * D + 2 * TOK * 2 * D * FF
+
+
+ORDER = """
+dx.0.1 dx.1.0 pi.1 x.0.0.0 dx.3.1 dx.2.0 x.0.1.1 pq w.0.2.1.0 x.0.2.1 xq.0.0 w.0.0.1.0
+w.1.1.1.0 xq.0.1 w.1.0.1.1 x.1.2.1 x.1.0.1 w.1.1.0.0 xq.0.2 xq.1.0 x.1.1.1 xq.1.1 w.0.1.0.0 w.0.3.0.1
+w.1.0.0.1 mm.0.1 w.0.0.0.0 w.1.3.0.0 mm.1.3 xq.1.2 mm.0.3 w.1.2.0.0 mm.1.2 mm.0.2 mm.2.2 w.0.3.1.0
+mm.1.0 w.0.2.0.0 w.1.3.1.0 mm.0.0 ad.1.1.0 mm.2.1 h.0.0 mm.1.1 mm.2.3 iv.1.0.0 it.0.1 mm.2.0
+ad.1.0.1 ad.2.1.1 ad.2.0.0 w.1.2.1.1 wq.0.1 wq.1.0 it.0.0 rt.0 iv.1.1.0 w.0.1.1.0 it.1.2 wq.1.1
+aq.0 wq.0.0 h.1.1 hq.0 wq.1.2 hq.1 rt.1 aq.1 b.0.1 iv.0.2.1 b.1.0 iv.1.3.0
+b.1.1 b.3.0 f.0.1 wq.0.2 it.0.3 wq.1.3 b.3.1 f.3.0 b.0.2 f.1.1 b.2.1 b.0.0
+f.1.0 f.0.2 wq.0.3 f.3.1 b.2.2 f.2.1 b.2.0 b.0.3 f.0.0 b.3.2 f.2.2 f.2.0
+f.0.3 b.2.3 b.1.2 f.3.2 f.2.3 b.1.3 b.3.3 f.1.2 f.1.3 f.3.3
+"""
+
+
+def tile_equivariantfeedforward_pa_kernel(tc, h, x1, pre1, w1_0_bytes, w1_0_scale, b1_0, out):
+    nc = tc.nc
+    with ExitStack() as ctx:
+        keep = ctx.enter_context(tc.tile_pool(name="keep", bufs=1))
+        work = ctx.enter_context(tc.tile_pool(name="work", bufs=3))
+        outs = ctx.enter_context(tc.tile_pool(name="outs", bufs=12))
+        psum_tr = ctx.enter_context(tc.psum_pool(name="psum_tr", bufs=3))
+        psum_mm = ctx.enter_context(tc.psum_pool(name="psum_mm", bufs=5))
+
+        w_view = w1_0_bytes.rearrange("(g p t) n -> g t p n", p=P, t=4)
+        wb = {}
+        for g in range(2):
+            for t in range(4):
+                wb[g, t] = keep.tile([P, FF], U8, name=f"wb{g}{t}", align_bytes=64)
+        xs = [keep.tile([P, D * M1], BF16, name=f"xs{i}", align_bytes=64) for i in range(NT)]
+        hs = keep.tile([P, NT, D], BF16, name="hs", align_bytes=64)
+        pre_raw = keep.tile([P, 4, D], BF16, name="pre_raw", align_bytes=64)
+        ws = keep.tile([P, 2, 4], F32, name="ws", align_bytes=64)
+        bias = keep.tile([P, FF], BF16, name="bias", align_bytes=64)
+
+        def load_w(g, t):
+            nc.sync.dma_start(out=wb[g, t][:], in_=w_view[g][t])
+
+        def load_x(i):
+            nc.sync.dma_start(out=xs[i][:], in_=x1[i].rearrange("n d m -> n (d m)"))
+
+        nc.scalar.dma_start(out=ws[:], in_=w1_0_scale.rearrange("(g p t) o -> p g (t o)", p=P, t=4))
+        load_x(0)
+        load_x(1)
+        nc.sync.dma_start(out=pre_raw[:], in_=pre1.rearrange("(p j) e -> p j e", j=4))
+        load_x(3)
+        load_x(2)
+        load_w(1, 0)
+        load_w(0, 2)
+        load_w(0, 0)
+        load_w(1, 1)
+        load_w(1, 2)
+        load_w(0, 3)
+        load_w(0, 1)
+        load_w(1, 3)
+        nc.sync.dma_start(out=bias[:], in_=b1_0.partition_broadcast(P))
+        nc.sync.dma_start(out=hs[:], in_=h.rearrange("b n d -> n b d"))
+
+        ident_bf = keep.tile([P, P], BF16, name="ident_bf", align_bytes=64)
+        make_identity(nc, ident_bf[:])
+        ident_f = keep.tile([P, P], F32, name="ident_f", align_bytes=64)
+        make_identity(nc, ident_f[:])
+
+        warm = keep.tile([P, 1], F32, name="warm")
+        nc.vector.memset(warm[:], 1.0)
+        nc.scalar.activation(out=warm[:], in_=warm[:], func=ACT.Sqrt)
+
+        planes = [keep.tile([P, 4, FF], BF16, name=f"planes{g}", align_bytes=64) for g in range(2)]
+        w_codes = [keep.tile([P, FF], U32, name=f"w_codes{g}", align_bytes=64) for g in range(2)]
+        w_scales = [keep.tile([P, FF], U8, name=f"w_scales{g}", align_bytes=64) for g in range(2)]
+        x_m = [keep.tile([P, M1, D], BF16, name=f"x_m{i}", align_bytes=64) for i in range(NT)]
+        x_int = [keep.tile([P, TOK, 4], BF16, name=f"x_int{m}", align_bytes=64) for m in range(M1)]
+        x_codes = [keep.tile([P, TOK], U32, name=f"x_codes{m}", align_bytes=64) for m in range(M1)]
+        x_scales = [keep.tile([P, TOK], U8, name=f"x_scales{m}", align_bytes=64) for m in range(M1)]
+        pre_int = keep.tile([P, 4 * P, 4], BF16, name="pre_int", align_bytes=64)
+        pre_codes = keep.tile([P, D], U32, name="pre_codes", align_bytes=64)
+        pre_scales = keep.tile([P, D], U8, name="pre_scales", align_bytes=64)
+        a_int = [keep.tile([P, TOK, 4], BF16, name=f"a_int{g}", align_bytes=64) for g in range(2)]
+        a_codes = [keep.tile([P, TOK], U32, name=f"a_codes{g}", align_bytes=64) for g in range(2)]
+        a_scales = [keep.tile([P, TOK], U8, name=f"a_scales{g}", align_bytes=64) for g in range(2)]
+        sq = [keep.tile([P, 4, TOK], F32, name=f"sq{m}", align_bytes=64) for m in range(M1)]
+
+        def widen_v(g, t, c0, c1):
+            nc.vector.tensor_scalar(
+                out=planes[g][:, t, c0:c1], in0=wb[g, t][:, c0:c1].bitcast(FP8),
+                scalar1=ws[:, g, t : t + 1], scalar2=None, op0=ALU.mult)
+
+        def widen_s(g, t, c0, c1):
+            nc.scalar.activation(
+                out=planes[g][:, t, c0:c1], in_=wb[g, t][:, c0:c1].bitcast(FP8),
+                func=ACT.Copy, scale=ws[:, g, t : t + 1])
+
+        def inter_w(g, q, engine):
+            w_int = work.tile([P, FQ, 4], BF16, name="w_int", align_bytes=64)
+            src = planes[g][:, :, q * FQ : (q + 1) * FQ].rearrange("p t n -> p n t")
+            if engine == 2:
+                for k in range(2):
+                    c = slice(k * 256, k * 256 + 256)
+                    nc.gpsimd.tensor_scalar(out=w_int[:, c, :], in0=src[:, c, :], scalar1=1.0, scalar2=0.0,
+                                            op0=ALU.mult, op1=ALU.add)
+            elif engine == 1:
+                nc.scalar.copy(out=w_int[:], in_=src)
+            else:
+                nc.vector.tensor_copy(out=w_int[:], in_=src)
+            return w_int
+
+        def inter_w_tensor(g, q):
+            w_int = work.tile([P, FQ, 4], BF16, name="w_int", align_bytes=64)
+            for k in range(2):
+                tr = psum_tr.tile([P, 2, P, 4], BF16, name="tr")
+                for j in range(2):
+                    c0 = q * FQ + (2 * k + j) * P
+                    nc.tensor.matmul(tr[:, j, :, :].rearrange("p n t -> p (n t)"), lhsT=ident_bf[:],
+                                     rhs=planes[g][:, :, c0 : c0 + P].rearrange("p t n -> p n t"), start=True, stop=True)
+                nc.scalar.copy(out=w_int[:, 2 * k * P : 2 * (k + 1) * P, :].rearrange("p n t -> p (n t)"),
+                               in_=tr[:].rearrange("p j n t -> p (j n t)"))
+            return w_int
+
+        def quant_w(g, q, w_int):
+            c = slice(q * FQ, (q + 1) * FQ)
+            nc.vector.quantize_mx(out=w_codes[g][:, c].bitcast(FP8X4), scales=w_scales[g][:, c],
+                                  in_=w_int[:].rearrange("p n t -> p (n t)"))
+
+        def split_x(i, engine):
+            src = xs[i][:].rearrange("p (d m) -> p m d", m=M1)
+            if engine == 2:
+                for k in range(2):
+                    c = slice(k * 256, k * 256 + 256)
+                    nc.gpsimd.tensor_scalar(out=x_m[i][:, :, c], in0=src[:, :, c], scalar1=1.0, scalar2=0.0,
+                                            op0=ALU.mult, op1=ALU.add)
+            elif engine == 1:
+                nc.scalar.copy(out=x_m[i][:], in_=src)
+            else:
+                nc.vector.tensor_copy(out=x_m[i][:], in_=src)
+
+        def x_tiles(half, m, on_scalar):
+            tr = psum_tr.tile([P, 2, 2, P], F32, name="tr")
+            for i in range(2):
+                words = x_m[2 * half + i][:].rearrange("p m d -> p (m d)").bitcast(F32)
+                for u in range(2):
+                    w0 = m * (D // 2)
+                    nc.tensor.transpose(tr[:, i, u, :], words[:, w0 + u : w0 + D // 2 : 2], ident_f[:])
+            dst = x_int[m][:].rearrange("p n t -> p (n t)").bitcast(F32)
+            dst = dst[:, half * 512 : (half + 1) * 512].rearrange("p (i n u) -> p i n u", i=2, u=2)
+            copy = nc.scalar.copy if on_scalar else nc.vector.tensor_copy
+            copy(out=dst, in_=tr[:].rearrange("p i u n -> p i n u"))
+
+        def x_quant(half, m):
+            c = slice(half * 256, half * 256 + 256)
+            nc.vector.quantize_mx(out=x_codes[m][:, c].bitcast(FP8X4), scales=x_scales[m][:, c],
+                                  in_=x_int[m][:, c, :].rearrange("p n t -> p (n t)"))
+
+        def pre_inter(engine):
+            dst = pre_int[:].rearrange("p (t m) j -> p t m j", t=4)
+            src = pre_raw[:].rearrange("p j (m t) -> p t m j", t=4)
+            if engine == 2:
+                for t in range(4):
+                    nc.gpsimd.tensor_scalar(out=dst[:, t], in0=src[:, t], scalar1=1.0, scalar2=0.0,
+                                            op0=ALU.mult, op1=ALU.add)
+            else:
+                nc.vector.tensor_copy(out=dst, in_=src)
+
+        def pre_quant():
+            nc.vector.quantize_mx(out=pre_codes[:].bitcast(FP8X4), scales=pre_scales[:],
+                                  in_=pre_int[:].rearrange("p n j -> p (n j)"))
+
+        def h_tiles(k, on_scalar):
+            i0 = 2 * k
+            words = hs[:].rearrange("p i d -> p (i d)").bitcast(F32)
+            tr = psum_tr.tile([P, 2, 2, P], F32, name="tr")
+            for i in range(2):
+                w0 = (i0 + i) * (D // 2)
+                for u in range(2):
+                    nc.tensor.transpose(tr[:, i, u, :], words[:, w0 + u : w0 + D // 2 : 2], ident_f[:])
+            dst = a_int[0][:].rearrange("p n t -> p (n t)").bitcast(F32)
+            dst = dst[:, i0 * 256 : (i0 + 2) * 256].rearrange("p (i n u) -> p i n u", i=2, u=2)
+            copy = nc.scalar.copy if on_scalar else nc.vector.tensor_copy
+            copy(out=dst, in_=tr[:].rearrange("p i u n -> p i n u"))
+
+        def quant_a(g, half):
+            c = slice(half * 256, half * 256 + 256)
+            nc.vector.quantize_mx(out=a_codes[g][:, c].bitcast(FP8X4), scales=a_scales[g][:, c],
+                                  in_=a_int[g][:, c, :].rearrange("p n t -> p (n t)"))
+
+        def mm1(m, t):
+            acc = psum_mm.tile([P, TOK], F32, name="acc")
+            c = slice(t * P, (t + 1) * P)
+            nc.tensor.matmul_mx(out=acc[:], lhsT=pre_codes[:, c].bitcast(FP8X4), lhsT_scale=pre_scales[:, c],
+                                rhs=x_codes[m][:].bitcast(FP8X4), rhs_scale=x_scales[m][:], start=True, stop=True)
+            nc.scalar.activation(out=sq[m][:, t, :], in_=acc[:], func=ACT.Square)
+
+        def add(m, t0, engine):
+            if engine == 2:
+                for t in (t0, t0 + 1):
+                    nc.gpsimd.tensor_tensor(out=sq[0][:, t, :], in0=sq[0][:, t, :], in1=sq[m][:, t, :], op=ALU.add)
+            else:
+                nc.vector.tensor_tensor(out=sq[0][:, t0 : t0 + 2, :], in0=sq[0][:, t0 : t0 + 2, :],
+                                        in1=sq[m][:, t0 : t0 + 2, :], op=ALU.add)
+
+        def root(half):
+            c = slice(half * 256, half * 256 + 256)
+            nc.scalar.activation(out=a_int[1][:, c, :], in_=sq[0][:, :, c].rearrange("p t n -> p n t"), func=ACT.Sqrt)
+
+        def mm2(i, q):
+            acc = psum_mm.tile([P, FQ], F32, name="acc")
+            r = slice(i * P, (i + 1) * P)
+            c = slice(q * FQ, (q + 1) * FQ)
+            for g in range(2):
+                nc.tensor.matmul_mx(out=acc[:], lhsT=a_codes[g][:, r].bitcast(FP8X4), lhsT_scale=a_scales[g][:, r],
+                                    rhs=w_codes[g][:, c].bitcast(FP8X4), rhs_scale=w_scales[g][:, c],
+                                    start=(g == 0), stop=(g == 1))
+            o = outs.tile([P, FQ], F32, name="o", align_bytes=64)
+            nc.vector.tensor_tensor(out=o[:], in0=acc[:], in1=bias[:, c], op=ALU.add)
+            return o
+
+        def finish(i, q, o):
+            nc.scalar.activation(out=o[:], in_=o[:], func=ACT.Silu)
+            nc.sync.dma_start(out=out[i][:, q * FQ : (q + 1) * FQ], in_=o[:])
+
+        w_int = {}
+        o = {}
+
+        def widen(g, t, half, on_scalar):
+            (widen_s if on_scalar else widen_v)(g, t, half * 1024, half * 1024 + 1024)
+
+        def step(kind, a):
+            if kind == "w":
+                widen(a[0], a[1], a[2], a[3])
+            elif kind == "x":
+                x_tiles(a[0], a[1], a[2])
+            elif kind == "dx":
+                split_x(a[0], a[1])
+            elif kind == "xq":
+                x_quant(a[0], a[1])
+            elif kind == "pi":
+                pre_inter(a[0])
+            elif kind == "pq":
+                pre_quant()
+            elif kind == "h":
+                h_tiles(a[0], a[1])
+            elif kind == "hq":
+                quant_a(0, a[0])
+            elif kind == "mm":
+                mm1(a[0], a[1])
+            elif kind == "ad":
+                add(a[0], 2 * a[1], a[2])
+            elif kind == "rt":
+                root(a[0])
+            elif kind == "aq":
+                quant_a(1, a[0])
+            elif kind == "iv":
+                w_int[a[0], a[1]] = inter_w(a[0], a[1], a[2])
+            elif kind == "it":
+                w_int[a[0], a[1]] = inter_w_tensor(a[0], a[1])
+            elif kind == "wq":
+                quant_w(a[0], a[1], w_int[a[0], a[1]])
+            elif kind == "b":
+                o[a[0], a[1]] = mm2(a[0], a[1])
+            elif kind == "f":
+                finish(a[0], a[1], o[a[0], a[1]])
+
+        with tc.manual_schedule():
+            for word in ORDER.split():
+                parts = word.split(".")
+                step(parts[0], [int(v) for v in parts[1:]])

@@ -13,277 +13,274 @@ ACT = mybir.ActivationFunctionType
 ALU = mybir.AluOpType
 
 P = 128
-TOK = 512
+PACK = 4
 D = 512
 M1 = 3
 FF = 2048
-NT = TOK // P
-FQ = 512
-NQ = FF // FQ
+NT = 4
+BANK = 512
+HALF = FF // 2
+NQ = FF // BANK
 
-FLOPS = 2 * TOK * M1 * D * D + 2 * TOK * 2 * D * FF
-
-
-ORDER = """
-dx.0.1 dx.1.0 pi.1 x.0.0.0 dx.3.1 dx.2.0 x.0.1.1 pq w.0.2.1.0 x.0.2.1 xq.0.0 w.0.0.1.0
-w.1.1.1.0 xq.0.1 w.1.0.1.1 x.1.2.1 x.1.0.1 w.1.1.0.0 xq.0.2 xq.1.0 x.1.1.1 xq.1.1 w.0.1.0.0 w.0.3.0.1
-w.1.0.0.1 mm.0.1 w.0.0.0.0 w.1.3.0.0 mm.1.3 xq.1.2 mm.0.3 w.1.2.0.0 mm.1.2 mm.0.2 mm.2.2 w.0.3.1.0
-mm.1.0 w.0.2.0.0 w.1.3.1.0 mm.0.0 ad.1.1.0 mm.2.1 h.0.0 mm.1.1 mm.2.3 iv.1.0.0 it.0.1 mm.2.0
-ad.1.0.1 ad.2.1.1 ad.2.0.0 w.1.2.1.1 wq.0.1 wq.1.0 it.0.0 rt.0 iv.1.1.0 w.0.1.1.0 it.1.2 wq.1.1
-aq.0 wq.0.0 h.1.1 hq.0 wq.1.2 hq.1 rt.1 aq.1 b.0.1 iv.0.2.1 b.1.0 iv.1.3.0
-b.1.1 b.3.0 f.0.1 wq.0.2 it.0.3 wq.1.3 b.3.1 f.3.0 b.0.2 f.1.1 b.2.1 b.0.0
-f.1.0 f.0.2 wq.0.3 f.3.1 b.2.2 f.2.1 b.2.0 b.0.3 f.0.0 b.3.2 f.2.2 f.2.0
-f.0.3 b.2.3 b.1.2 f.3.2 f.2.3 b.1.3 b.3.3 f.1.2 f.1.3 f.3.3
-"""
+FLOPS = 2 * NT * P * M1 * D * D + 2 * NT * P * 2 * D * FF
+PSUM_BANKS = 8
 
 
 def tile_equivariantfeedforward_pa_kernel(tc, h, x1, pre1, w1_0_bytes, w1_0_scale, b1_0, out):
     nc = tc.nc
     with ExitStack() as ctx:
         keep = ctx.enter_context(tc.tile_pool(name="keep", bufs=1))
-        work = ctx.enter_context(tc.tile_pool(name="work", bufs=3))
-        outs = ctx.enter_context(tc.tile_pool(name="outs", bufs=12))
-        psum_tr = ctx.enter_context(tc.psum_pool(name="psum_tr", bufs=3))
-        psum_mm = ctx.enter_context(tc.psum_pool(name="psum_mm", bufs=5))
+        psum = ctx.enter_context(tc.psum_pool(name="psum", bufs=1))
 
-        w_view = w1_0_bytes.rearrange("(g p t) n -> g t p n", p=P, t=4)
-        wb = {}
-        for g in range(2):
-            for t in range(4):
-                wb[g, t] = keep.tile([P, FF], U8, name=f"wb{g}{t}", align_bytes=64)
-        xs = [keep.tile([P, D * M1], BF16, name=f"xs{i}", align_bytes=64) for i in range(NT)]
-        hs = keep.tile([P, NT, D], BF16, name="hs", align_bytes=64)
-        pre_raw = keep.tile([P, 4, D], BF16, name="pre_raw", align_bytes=64)
-        ws = keep.tile([P, 2, 4], F32, name="ws", align_bytes=64)
-        bias = keep.tile([P, FF], BF16, name="bias", align_bytes=64)
+        def sbuf(name, shape, dtype):
+            return keep.tile([P] + shape, dtype, name=name, align_bytes=64)
 
-        def load_w(g, t):
-            nc.sync.dma_start(out=wb[g, t][:], in_=w_view[g][t])
+        banks_taken = []
+
+        def bank(shape, dtype):
+            n = len(banks_taken) % PSUM_BANKS
+            banks_taken.append(n)
+            return psum.tile([P] + shape, dtype, name=f"bank{n}")
+
+        tiles = range(NT)
+        w_rows = w1_0_bytes.rearrange("(g p t) n -> g p t n", p=P, t=PACK)
+        w_bytes = {}
+        x_raw = [sbuf(f"x_raw{i}", [D * M1], BF16) for i in tiles]
+        h_raw = [sbuf(f"h_raw{i}", [D], BF16) for i in tiles]
+        pre_raw = sbuf("pre_raw", [PACK, D], BF16)
+        w_scale = sbuf("w_scale", [2, PACK], F32)
+        bias = sbuf("bias", [FF], BF16)
+
+        def load_w(g, half, t0, t1):
+            raw = sbuf(f"w_bytes{g}{half}{t0}", [t1 - t0, HALF], U8)
+            nc.sync.dma_start(out=raw[:], in_=w_rows[g][:, t0:t1, half * HALF : (half + 1) * HALF])
+            for t in range(t0, t1):
+                w_bytes[g, half, t] = raw[:, t - t0, :]
 
         def load_x(i):
-            nc.sync.dma_start(out=xs[i][:], in_=x1[i].rearrange("n d m -> n (d m)"))
+            nc.sync.dma_start(out=x_raw[i][:], in_=x1[i].rearrange("n d m -> n (d m)"))
 
-        nc.scalar.dma_start(out=ws[:], in_=w1_0_scale.rearrange("(g p t) o -> p g (t o)", p=P, t=4))
-        load_x(0)
-        load_x(1)
-        nc.sync.dma_start(out=pre_raw[:], in_=pre1.rearrange("(p j) e -> p j e", j=4))
-        load_x(3)
-        load_x(2)
-        load_w(1, 0)
-        load_w(0, 2)
-        load_w(0, 0)
-        load_w(1, 1)
-        load_w(1, 2)
-        load_w(0, 3)
-        load_w(0, 1)
-        load_w(1, 3)
-        nc.sync.dma_start(out=bias[:], in_=b1_0.partition_broadcast(P))
-        nc.sync.dma_start(out=hs[:], in_=h.rearrange("b n d -> n b d"))
+        def load_h(i):
+            nc.sync.dma_start(out=h_raw[i][:], in_=h[i])
 
-        ident_bf = keep.tile([P, P], BF16, name="ident_bf", align_bytes=64)
-        make_identity(nc, ident_bf[:])
-        ident_f = keep.tile([P, P], F32, name="ident_f", align_bytes=64)
-        make_identity(nc, ident_f[:])
+        ident_f32 = sbuf("ident_f32", [P], F32)
+        ident_bf16 = sbuf("ident_bf16", [P], BF16)
 
-        warm = keep.tile([P, 1], F32, name="warm")
-        nc.vector.memset(warm[:], 1.0)
-        nc.scalar.activation(out=warm[:], in_=warm[:], func=ACT.Sqrt)
+        w_wide = {(g, half): sbuf(f"w_wide{g}{half}", [PACK, HALF], BF16) for g in range(2) for half in range(2)}
+        w_words = {(g, half): sbuf(f"w_words{g}{half}", [HALF * PACK], BF16) for g in range(2) for half in range(2)}
+        w_codes = {(g, half): sbuf(f"w_codes{g}{half}", [HALF], U32) for g in range(2) for half in range(2)}
+        w_scales = {(g, half): sbuf(f"w_scales{g}{half}", [HALF], U8) for g in range(2) for half in range(2)}
+        pre_words = sbuf("pre_words", [D, PACK], BF16)
+        pre_codes = sbuf("pre_codes", [D], U32)
+        pre_scales = sbuf("pre_scales", [D], U8)
+        x_split = [sbuf(f"x_split{i}", [M1, D], BF16) for i in tiles]
+        xh_words = [sbuf(f"xh_words{i}", [(M1 + 1) * P * PACK], BF16) for i in tiles]
+        xh_codes = [sbuf(f"xh_codes{i}", [(M1 + 1) * P], U32) for i in tiles]
+        xh_scales = [sbuf(f"xh_scales{i}", [(M1 + 1) * P], U8) for i in tiles]
+        squares = {(i, m): sbuf(f"squares{i}{m}", [PACK, P], F32) for i in tiles for m in range(M1)}
+        inv_words = [sbuf(f"inv_words{i}", [P, PACK], BF16) for i in tiles]
+        inv_codes = [sbuf(f"inv_codes{i}", [P], U32) for i in tiles]
+        inv_scales = [sbuf(f"inv_scales{i}", [P], U8) for i in tiles]
+        rows = [sbuf(f"rows{q}", [NT * BANK], F32) for q in range(NQ)]
+        held = {}
 
-        planes = [keep.tile([P, 4, FF], BF16, name=f"planes{g}", align_bytes=64) for g in range(2)]
-        w_codes = [keep.tile([P, FF], U32, name=f"w_codes{g}", align_bytes=64) for g in range(2)]
-        w_scales = [keep.tile([P, FF], U8, name=f"w_scales{g}", align_bytes=64) for g in range(2)]
-        x_m = [keep.tile([P, M1, D], BF16, name=f"x_m{i}", align_bytes=64) for i in range(NT)]
-        x_int = [keep.tile([P, TOK, 4], BF16, name=f"x_int{m}", align_bytes=64) for m in range(M1)]
-        x_codes = [keep.tile([P, TOK], U32, name=f"x_codes{m}", align_bytes=64) for m in range(M1)]
-        x_scales = [keep.tile([P, TOK], U8, name=f"x_scales{m}", align_bytes=64) for m in range(M1)]
-        pre_int = keep.tile([P, 4 * P, 4], BF16, name="pre_int", align_bytes=64)
-        pre_codes = keep.tile([P, D], U32, name="pre_codes", align_bytes=64)
-        pre_scales = keep.tile([P, D], U8, name="pre_scales", align_bytes=64)
-        a_int = [keep.tile([P, TOK, 4], BF16, name=f"a_int{g}", align_bytes=64) for g in range(2)]
-        a_codes = [keep.tile([P, TOK], U32, name=f"a_codes{g}", align_bytes=64) for g in range(2)]
-        a_scales = [keep.tile([P, TOK], U8, name=f"a_scales{g}", align_bytes=64) for g in range(2)]
-        sq = [keep.tile([P, 4, TOK], F32, name=f"sq{m}", align_bytes=64) for m in range(M1)]
+        def quantise(codes, scales, words):
+            nc.vector.quantize_mx(out=codes.bitcast(FP8X4), scales=scales, in_=words)
 
-        def widen_v(g, t, c0, c1):
-            nc.vector.tensor_scalar(
-                out=planes[g][:, t, c0:c1], in0=wb[g, t][:, c0:c1].bitcast(FP8),
-                scalar1=ws[:, g, t : t + 1], scalar2=None, op0=ALU.mult)
+        def widen_on_vector(g, half, t):
+            nc.vector.tensor_scalar(out=w_wide[g, half][:, t, :], in0=w_bytes[g, half, t].bitcast(FP8),
+                                    scalar1=w_scale[:, g, t : t + 1], scalar2=None, op0=ALU.mult)
 
-        def widen_s(g, t, c0, c1):
-            nc.scalar.activation(
-                out=planes[g][:, t, c0:c1], in_=wb[g, t][:, c0:c1].bitcast(FP8),
-                func=ACT.Copy, scale=ws[:, g, t : t + 1])
+        def widen_on_scalar(g, half, t):
+            nc.scalar.activation(out=w_wide[g, half][:, t, :], in_=w_bytes[g, half, t].bitcast(FP8),
+                                 func=ACT.Copy, scale=w_scale[:, g, t : t + 1])
 
-        def inter_w(g, q, engine):
-            w_int = work.tile([P, FQ, 4], BF16, name="w_int", align_bytes=64)
-            src = planes[g][:, :, q * FQ : (q + 1) * FQ].rearrange("p t n -> p n t")
-            if engine == 2:
-                for k in range(2):
-                    c = slice(k * 256, k * 256 + 256)
-                    nc.gpsimd.tensor_scalar(out=w_int[:, c, :], in0=src[:, c, :], scalar1=1.0, scalar2=0.0,
-                                            op0=ALU.mult, op1=ALU.add)
-            elif engine == 1:
-                nc.scalar.copy(out=w_int[:], in_=src)
-            else:
-                nc.vector.tensor_copy(out=w_int[:], in_=src)
-            return w_int
+        def w_columns(g, c0, c1):
+            half = c0 // HALF
+            return w_wide[g, half][:, :, c0 - half * HALF : c1 - half * HALF].rearrange("p t n -> p n t")
 
-        def inter_w_tensor(g, q):
-            w_int = work.tile([P, FQ, 4], BF16, name="w_int", align_bytes=64)
-            for k in range(2):
-                tr = psum_tr.tile([P, 2, P, 4], BF16, name="tr")
-                for j in range(2):
-                    c0 = q * FQ + (2 * k + j) * P
-                    nc.tensor.matmul(tr[:, j, :, :].rearrange("p n t -> p (n t)"), lhsT=ident_bf[:],
-                                     rhs=planes[g][:, :, c0 : c0 + P].rearrange("p t n -> p n t"), start=True, stop=True)
-                nc.scalar.copy(out=w_int[:, 2 * k * P : 2 * (k + 1) * P, :].rearrange("p n t -> p (n t)"),
-                               in_=tr[:].rearrange("p j n t -> p (j n t)"))
-            return w_int
+        def w_part(parts, g, c0, c1, width):
+            half = c0 // HALF
+            return parts[g, half][:, (c0 - half * HALF) * width : (c1 - half * HALF) * width]
 
-        def quant_w(g, q, w_int):
-            c = slice(q * FQ, (q + 1) * FQ)
-            nc.vector.quantize_mx(out=w_codes[g][:, c].bitcast(FP8X4), scales=w_scales[g][:, c],
-                                  in_=w_int[:].rearrange("p n t -> p (n t)"))
+        def interleave_w(g, q):
+            c0, c1 = q * BANK, (q + 1) * BANK
+            nc.vector.tensor_copy(out=w_part(w_words, g, c0, c1, PACK).rearrange("p (n t) -> p n t", t=PACK),
+                                  in_=w_columns(g, c0, c1))
 
-        def split_x(i, engine):
-            src = xs[i][:].rearrange("p (d m) -> p m d", m=M1)
-            if engine == 2:
-                for k in range(2):
-                    c = slice(k * 256, k * 256 + 256)
-                    nc.gpsimd.tensor_scalar(out=x_m[i][:, :, c], in0=src[:, :, c], scalar1=1.0, scalar2=0.0,
-                                            op0=ALU.mult, op1=ALU.add)
-            elif engine == 1:
-                nc.scalar.copy(out=x_m[i][:], in_=src)
-            else:
-                nc.vector.tensor_copy(out=x_m[i][:], in_=src)
+        def lay_w(g, q, k):
+            laid = bank([2, P * PACK], BF16)
+            for j in range(2):
+                c0 = q * BANK + (2 * k + j) * P
+                nc.tensor.matmul(laid[:, j, :], lhsT=ident_bf16[:], rhs=w_columns(g, c0, c0 + P), start=True, stop=True)
+            held["w", g, q, k] = laid
 
-        def x_tiles(half, m, on_scalar):
-            tr = psum_tr.tile([P, 2, 2, P], F32, name="tr")
-            for i in range(2):
-                words = x_m[2 * half + i][:].rearrange("p m d -> p (m d)").bitcast(F32)
+        def fetch_w(g, q, k):
+            c0 = q * BANK + 2 * k * P
+            nc.scalar.copy(out=w_part(w_words, g, c0, c0 + 2 * P, PACK),
+                           in_=held["w", g, q, k][:].rearrange("p j c -> p (j c)"))
+
+        def quantise_w(g, q0, q1):
+            c0, c1 = q0 * BANK, q1 * BANK
+            quantise(w_part(w_codes, g, c0, c1, 1), w_part(w_scales, g, c0, c1, 1), w_part(w_words, g, c0, c1, PACK))
+
+        def interleave_pre():
+            nc.vector.tensor_copy(out=pre_words[:], in_=pre_raw[:].rearrange("p t e -> p e t"))
+
+        def quantise_pre():
+            quantise(pre_codes[:], pre_scales[:], pre_words[:].rearrange("p e t -> p (e t)"))
+
+        def split_x(i):
+            nc.vector.tensor_copy(out=x_split[i][:].rearrange("p m (a d) -> p a m d", a=2),
+                                  in_=x_raw[i][:].rearrange("p (a d m) -> p a m d", a=2, m=M1))
+
+        def turn_xh(i, b):
+            turned = bank([2, 2, P], F32)
+            for j in range(2):
+                m = 2 * b + j
+                words = (x_split[i][:, m, :] if m < M1 else h_raw[i][:]).bitcast(F32)
                 for u in range(2):
-                    w0 = m * (D // 2)
-                    nc.tensor.transpose(tr[:, i, u, :], words[:, w0 + u : w0 + D // 2 : 2], ident_f[:])
-            dst = x_int[m][:].rearrange("p n t -> p (n t)").bitcast(F32)
-            dst = dst[:, half * 512 : (half + 1) * 512].rearrange("p (i n u) -> p i n u", i=2, u=2)
-            copy = nc.scalar.copy if on_scalar else nc.vector.tensor_copy
-            copy(out=dst, in_=tr[:].rearrange("p i u n -> p i n u"))
+                    nc.tensor.transpose(turned[:, j, u, :], words[:, u : D // 2 : 2], ident_f32[:])
+            held["xh", i, b] = turned
 
-        def x_quant(half, m):
-            c = slice(half * 256, half * 256 + 256)
-            nc.vector.quantize_mx(out=x_codes[m][:, c].bitcast(FP8X4), scales=x_scales[m][:, c],
-                                  in_=x_int[m][:, c, :].rearrange("p n t -> p (n t)"))
+        def fetch_xh(i, b):
+            dst = xh_words[i][:, b * 2 * P * PACK : (b + 1) * 2 * P * PACK].bitcast(F32)
+            nc.scalar.copy(out=dst.rearrange("p (j n u) -> p j n u", j=2, u=2),
+                           in_=held["xh", i, b][:].rearrange("p j u n -> p j n u"))
 
-        def pre_inter(engine):
-            dst = pre_int[:].rearrange("p (t m) j -> p t m j", t=4)
-            src = pre_raw[:].rearrange("p j (m t) -> p t m j", t=4)
-            if engine == 2:
-                for t in range(4):
-                    nc.gpsimd.tensor_scalar(out=dst[:, t], in0=src[:, t], scalar1=1.0, scalar2=0.0,
-                                            op0=ALU.mult, op1=ALU.add)
-            else:
-                nc.vector.tensor_copy(out=dst, in_=src)
+        def quantise_xh(i, b0, b1):
+            c = slice(b0 * 2 * P, b1 * 2 * P)
+            quantise(xh_codes[i][:, c], xh_scales[i][:, c], xh_words[i][:, b0 * 2 * P * PACK : b1 * 2 * P * PACK])
 
-        def pre_quant():
-            nc.vector.quantize_mx(out=pre_codes[:].bitcast(FP8X4), scales=pre_scales[:],
-                                  in_=pre_int[:].rearrange("p n j -> p (n j)"))
+        def xh_operand(i, m):
+            c = slice(m * P, (m + 1) * P)
+            return xh_codes[i][:, c].bitcast(FP8X4), xh_scales[i][:, c]
 
-        def h_tiles(k, on_scalar):
-            i0 = 2 * k
-            words = hs[:].rearrange("p i d -> p (i d)").bitcast(F32)
-            tr = psum_tr.tile([P, 2, 2, P], F32, name="tr")
-            for i in range(2):
-                w0 = (i0 + i) * (D // 2)
-                for u in range(2):
-                    nc.tensor.transpose(tr[:, i, u, :], words[:, w0 + u : w0 + D // 2 : 2], ident_f[:])
-            dst = a_int[0][:].rearrange("p n t -> p (n t)").bitcast(F32)
-            dst = dst[:, i0 * 256 : (i0 + 2) * 256].rearrange("p (i n u) -> p i n u", i=2, u=2)
-            copy = nc.scalar.copy if on_scalar else nc.vector.tensor_copy
-            copy(out=dst, in_=tr[:].rearrange("p i u n -> p i n u"))
+        def project(i, m):
+            pm = bank([BANK], F32)
+            codes, scales = xh_operand(i, m)
+            nc.tensor.matmul_mx(out=pm[:], lhsT=codes, lhsT_scale=scales, rhs=pre_codes[:].bitcast(FP8X4),
+                                rhs_scale=pre_scales[:], start=True, stop=True)
+            held["pm", i, m] = pm
 
-        def quant_a(g, half):
-            c = slice(half * 256, half * 256 + 256)
-            nc.vector.quantize_mx(out=a_codes[g][:, c].bitcast(FP8X4), scales=a_scales[g][:, c],
-                                  in_=a_int[g][:, c, :].rearrange("p n t -> p (n t)"))
+        def square(i, m):
+            nc.scalar.activation(out=squares[i, m][:], in_=held["pm", i, m][:].rearrange("p (c t) -> p t c", t=PACK),
+                                 func=ACT.Square)
 
-        def mm1(m, t):
-            acc = psum_mm.tile([P, TOK], F32, name="acc")
-            c = slice(t * P, (t + 1) * P)
-            nc.tensor.matmul_mx(out=acc[:], lhsT=pre_codes[:, c].bitcast(FP8X4), lhsT_scale=pre_scales[:, c],
-                                rhs=x_codes[m][:].bitcast(FP8X4), rhs_scale=x_scales[m][:], start=True, stop=True)
-            nc.scalar.activation(out=sq[m][:, t, :], in_=acc[:], func=ACT.Square)
+        def sum_squares(i):
+            total = bank([PACK, P], F32)
+            for t in range(PACK):
+                for m in range(M1):
+                    nc.tensor.matmul(total[:, t, :], lhsT=squares[i, m][:, t, :], rhs=ident_f32[:],
+                                     start=(m == 0), stop=(m == M1 - 1), is_transpose=True)
+            held["sum", i] = total
 
-        def add(m, t0, engine):
-            if engine == 2:
-                for t in (t0, t0 + 1):
-                    nc.gpsimd.tensor_tensor(out=sq[0][:, t, :], in0=sq[0][:, t, :], in1=sq[m][:, t, :], op=ALU.add)
-            else:
-                nc.vector.tensor_tensor(out=sq[0][:, t0 : t0 + 2, :], in0=sq[0][:, t0 : t0 + 2, :],
-                                        in1=sq[m][:, t0 : t0 + 2, :], op=ALU.add)
+        def root(i):
+            nc.scalar.activation(out=inv_words[i][:], in_=held["sum", i][:].rearrange("p t n -> p n t"), func=ACT.Sqrt)
 
-        def root(half):
-            c = slice(half * 256, half * 256 + 256)
-            nc.scalar.activation(out=a_int[1][:, c, :], in_=sq[0][:, :, c].rearrange("p t n -> p n t"), func=ACT.Sqrt)
+        def quantise_inv(i):
+            quantise(inv_codes[i][:], inv_scales[i][:], inv_words[i][:].rearrange("p n t -> p (n t)"))
 
-        def mm2(i, q):
-            acc = psum_mm.tile([P, FQ], F32, name="acc")
-            r = slice(i * P, (i + 1) * P)
-            c = slice(q * FQ, (q + 1) * FQ)
+        def multiply(i, q):
+            acc = bank([BANK], F32)
+            h_codes, h_scales = xh_operand(i, M1)
+            sides = [(h_codes, h_scales), (inv_codes[i][:].bitcast(FP8X4), inv_scales[i][:])]
             for g in range(2):
-                nc.tensor.matmul_mx(out=acc[:], lhsT=a_codes[g][:, r].bitcast(FP8X4), lhsT_scale=a_scales[g][:, r],
-                                    rhs=w_codes[g][:, c].bitcast(FP8X4), rhs_scale=w_scales[g][:, c],
+                nc.tensor.matmul_mx(out=acc[:], lhsT=sides[g][0], lhsT_scale=sides[g][1],
+                                    rhs=w_part(w_codes, g, q * BANK, (q + 1) * BANK, 1).bitcast(FP8X4),
+                                    rhs_scale=w_part(w_scales, g, q * BANK, (q + 1) * BANK, 1),
                                     start=(g == 0), stop=(g == 1))
-            o = outs.tile([P, FQ], F32, name="o", align_bytes=64)
-            nc.vector.tensor_tensor(out=o[:], in0=acc[:], in1=bias[:, c], op=ALU.add)
-            return o
+            held["acc", i, q] = acc
 
-        def finish(i, q, o):
-            nc.scalar.activation(out=o[:], in_=o[:], func=ACT.Silu)
-            nc.sync.dma_start(out=out[i][:, q * FQ : (q + 1) * FQ], in_=o[:])
+        def add_bias(i, q):
+            nc.vector.tensor_tensor(out=rows[q][:, i * BANK : (i + 1) * BANK], in0=held["acc", i, q][:],
+                                    in1=bias[:, q * BANK : (q + 1) * BANK], op=ALU.add)
 
-        w_int = {}
-        o = {}
+        def finish(i0, i1, q):
+            part = rows[q][:, i0 * BANK : i1 * BANK]
+            nc.scalar.activation(out=part, in_=part, func=ACT.Silu)
+            nc.sync.dma_start(out=out[i0:i1, :, q * BANK : (q + 1) * BANK].rearrange("i n c -> n i c"),
+                              in_=part.rearrange("p (i c) -> p i c", c=BANK))
 
-        def widen(g, t, half, on_scalar):
-            (widen_s if on_scalar else widen_v)(g, t, half * 1024, half * 1024 + 1024)
+        def start_loads():
+            nc.scalar.dma_start(out=w_scale[:], in_=w1_0_scale.rearrange("(g p t) o -> p g (t o)", p=P, t=PACK))
+            load_x(0)
+            load_w(0, 0, 0, 2)
+            nc.sync.dma_start(out=pre_raw[:], in_=pre1.rearrange("(p t) e -> p t e", t=PACK))
+            load_h(0)
+            load_x(1)
+            load_w(0, 0, 2, 4)
+            load_h(1)
+            load_x(2)
+            load_h(2)
+            load_w(1, 0, 0, 4)
+            load_x(3)
+            load_h(3)
+            load_w(0, 1, 0, 4)
+            load_w(1, 1, 0, 4)
+            nc.sync.dma_start(out=bias[:], in_=b1_0.partition_broadcast(P))
+            make_identity(nc, ident_f32[:])
+            make_identity(nc, ident_bf16[:])
 
-        def step(kind, a):
-            if kind == "w":
-                widen(a[0], a[1], a[2], a[3])
-            elif kind == "x":
-                x_tiles(a[0], a[1], a[2])
-            elif kind == "dx":
-                split_x(a[0], a[1])
-            elif kind == "xq":
-                x_quant(a[0], a[1])
-            elif kind == "pi":
-                pre_inter(a[0])
-            elif kind == "pq":
-                pre_quant()
-            elif kind == "h":
-                h_tiles(a[0], a[1])
-            elif kind == "hq":
-                quant_a(0, a[0])
-            elif kind == "mm":
-                mm1(a[0], a[1])
-            elif kind == "ad":
-                add(a[0], 2 * a[1], a[2])
-            elif kind == "rt":
-                root(a[0])
-            elif kind == "aq":
-                quant_a(1, a[0])
-            elif kind == "iv":
-                w_int[a[0], a[1]] = inter_w(a[0], a[1], a[2])
-            elif kind == "it":
-                w_int[a[0], a[1]] = inter_w_tensor(a[0], a[1])
-            elif kind == "wq":
-                quant_w(a[0], a[1], w_int[a[0], a[1]])
-            elif kind == "b":
-                o[a[0], a[1]] = mm2(a[0], a[1])
-            elif kind == "f":
-                finish(a[0], a[1], o[a[0], a[1]])
+        tensor_steps = [(turn_xh, 0, 0,), (turn_xh, 0, 1,), (turn_xh, 1, 0,), (turn_xh, 1, 1,), (project, 0, 0,), (project, 0, 1,), (project, 0, 2,), (turn_xh, 2, 0,), (turn_xh, 2, 1,), (project, 1, 0,), (project, 1, 1,), (project, 1, 2,), (sum_squares, 0,), (turn_xh, 3, 0,), (turn_xh, 3, 1,), (lay_w, 0, 0, 0,), (lay_w, 0, 0, 1,), (project, 2, 0,), (project, 2, 1,), (project, 2, 2,), (sum_squares, 1,), (project, 3, 0,), (project, 3, 1,), (project, 3, 2,), (sum_squares, 2,), (lay_w, 0, 1, 0,), (lay_w, 0, 1, 1,), (multiply, 0, 0,), (sum_squares, 3,), (multiply, 1, 0,), (lay_w, 0, 2, 0,), (lay_w, 0, 2, 1,), (multiply, 2, 0,), (multiply, 3, 0,), (multiply, 0, 1,), (multiply, 1, 1,), (lay_w, 0, 3, 0,), (lay_w, 0, 3, 1,), (multiply, 2, 1,), (multiply, 3, 1,), (multiply, 0, 2,), (multiply, 1, 2,), (multiply, 2, 2,), (multiply, 3, 2,), (multiply, 0, 3,), (multiply, 1, 3,), (multiply, 2, 3,), (multiply, 3, 3,)]
+        scalar_steps = [(widen_on_scalar, 0, 0, 0,), (fetch_xh, 0, 0,), (fetch_xh, 0, 1,), (widen_on_scalar, 0, 0, 2,), (fetch_xh, 1, 0,), (fetch_xh, 1, 1,), (square, 0, 0,), (square, 0, 1,), (square, 0, 2,), (widen_on_scalar, 0, 0, 3,), (fetch_xh, 2, 0,), (fetch_xh, 2, 1,), (square, 1, 0,), (square, 1, 1,), (square, 1, 2,), (fetch_xh, 3, 0,), (fetch_xh, 3, 1,), (root, 0,), (square, 2, 0,), (square, 2, 1,), (square, 2, 2,), (fetch_w, 0, 0, 0,), (fetch_w, 0, 0, 1,), (root, 1,), (square, 3, 0,), (square, 3, 1,), (square, 3, 2,), (root, 2,), (fetch_w, 0, 1, 0,), (fetch_w, 0, 1, 1,), (widen_on_scalar, 0, 1, 3,), (root, 3,), (fetch_w, 0, 2, 0,), (fetch_w, 0, 2, 1,), (finish, 0, 2, 0,), (fetch_w, 0, 3, 0,), (fetch_w, 0, 3, 1,), (finish, 2, 4, 0,), (finish, 0, 2, 1,), (finish, 2, 4, 1,), (finish, 0, 2, 2,), (finish, 2, 4, 2,), (finish, 0, 1, 3,), (finish, 1, 2, 3,), (finish, 2, 3, 3,), (finish, 3, 4, 3,)]
+        vector_steps = [(split_x, 0,), (widen_on_vector, 0, 0, 1,), (interleave_pre,), (split_x, 1,), (quantise_pre,), (quantise_xh, 0, 0, 1,), (quantise_xh, 0, 1, 2,), (split_x, 2,), (widen_on_vector, 1, 0, 0,), (quantise_xh, 1, 0, 2,), (split_x, 3,), (widen_on_vector, 1, 0, 1,), (widen_on_vector, 1, 0, 2,), (widen_on_vector, 1, 0, 3,), (quantise_xh, 2, 0, 2,), (interleave_w, 1, 0,), (widen_on_vector, 0, 1, 0,), (widen_on_vector, 0, 1, 1,), (quantise_xh, 3, 0, 2,), (interleave_w, 1, 1,), (quantise_inv, 0,), (quantise_w, 1, 0, 1,), (widen_on_vector, 0, 1, 2,), (widen_on_vector, 1, 1, 0,), (quantise_w, 0, 0, 1,), (quantise_inv, 1,), (widen_on_vector, 1, 1, 1,), (widen_on_vector, 1, 1, 2,), (widen_on_vector, 1, 1, 3,), (quantise_w, 1, 1, 2,), (quantise_inv, 2,), (add_bias, 0, 0,), (quantise_w, 0, 1, 2,), (add_bias, 1, 0,), (quantise_inv, 3,), (interleave_w, 1, 2,), (add_bias, 2, 0,), (quantise_w, 1, 2, 3,), (add_bias, 3, 0,), (quantise_w, 0, 2, 3,), (add_bias, 0, 1,), (interleave_w, 1, 3,), (add_bias, 1, 1,), (quantise_w, 1, 3, 4,), (add_bias, 2, 1,), (quantise_w, 0, 3, 4,), (add_bias, 3, 1,), (add_bias, 0, 2,), (add_bias, 1, 2,), (add_bias, 2, 2,), (add_bias, 3, 2,), (add_bias, 0, 3,), (add_bias, 1, 3,), (add_bias, 2, 3,), (add_bias, 3, 3,)]
 
+        def inputs_of(work, *a):
+            if work is turn_xh:
+                return [(split_x, a[0])]
+            if work is fetch_xh:
+                return [(turn_xh, *a)]
+            if work is quantise_xh:
+                return [(fetch_xh, a[0], b) for b in range(a[1], a[2])]
+            if work is quantise_pre:
+                return [(interleave_pre,)]
+            if work is project:
+                return [(quantise_pre,), covering(quantise_xh, a[0], a[1] // 2)]
+            if work is square:
+                return [(project, *a)]
+            if work is sum_squares:
+                return [(square, a[0], m) for m in range(M1)]
+            if work is root:
+                return [(sum_squares, *a)]
+            if work is quantise_inv:
+                return [(root, *a)]
+            if work in (lay_w, interleave_w):
+                return [s for s in steps if s[0] in (widen_on_vector, widen_on_scalar) and s[1:3] == (a[0], a[1] // 2)]
+            if work is fetch_w:
+                return [(lay_w, *a)]
+            if work is quantise_w:
+                return [s for s in steps if s[0] in (fetch_w, interleave_w) and s[1] == a[0] and a[1] <= s[2] < a[2]]
+            if work is multiply:
+                return [(quantise_inv, a[0]), covering(quantise_xh, a[0], 1)] + [covering(quantise_w, g, a[1]) for g in range(2)]
+            if work is add_bias:
+                return [(multiply, *a)]
+            if work is finish:
+                return [(add_bias, i, a[2]) for i in range(a[0], a[1])]
+            return []
+
+        def covering(work, which, part):
+            return [s for s in steps if s[0] is work and s[1] == which and s[2] <= part < s[3]][0]
+
+        emptied_by = {turn_xh: fetch_xh, project: square, sum_squares: root, lay_w: fetch_w, multiply: add_bias}
+        queues = [tensor_steps, scalar_steps, vector_steps]
+        steps = tensor_steps + scalar_steps + vector_steps
+        written = set()
+        at = [0, 0, 0]
         with tc.manual_schedule():
-            for word in ORDER.split():
-                parts = word.split(".")
-                step(parts[0], [int(v) for v in parts[1:]])
+            start_loads()
+            while len(written) < len(steps):
+                before = len(written)
+                for e in range(3):
+                    if at[e] == len(queues[e]):
+                        continue
+                    s = queues[e][at[e]]
+                    needs = inputs_of(*s)
+                    if e == 0 and at[0] >= PSUM_BANKS:
+                        old = tensor_steps[at[0] - PSUM_BANKS]
+                        needs = needs + [(emptied_by[old[0]], *old[1:])]
+                    if all(n in written for n in needs):
+                        s[0](*s[1:])
+                        written.add(s)
+                        at[e] = at[e] + 1
+                assert len(written) > before

@@ -219,6 +219,9 @@ def tile_equivariantfeedforward_pa_kernel(tc, h, x1, pre1, w1_0_bytes, w1_0_scal
             load_w(0, 1, 0, 4)
             load_w(1, 1, 0, 4)
             nc.sync.dma_start(out=bias[:], in_=b1_0.partition_broadcast(P))
+            warm = sbuf("warm", [1], F32)
+            nc.vector.memset(warm[:], 1.0)
+            nc.scalar.activation(out=warm[:], in_=warm[:], func=ACT.Sqrt)
             make_identity(nc, ident_f32[:])
             make_identity(nc, ident_bf16[:])
 

@@ -24,6 +24,7 @@ NQ = FF // BANK
 
 FLOPS = 2 * NT * P * M1 * D * D + 2 * NT * P * 2 * D * FF
 PSUM_BANKS = 8
+RUN = 4
 
 
 def tile_equivariantfeedforward_pa_kernel(tc, h, x1, pre1, w1_0_bytes, w1_0_scale, b1_0, out):
@@ -105,8 +106,10 @@ def tile_equivariantfeedforward_pa_kernel(tc, h, x1, pre1, w1_0_bytes, w1_0_scal
 
         def interleave_w(g, q):
             c0, c1 = q * BANK, (q + 1) * BANK
-            nc.vector.tensor_copy(out=w_part(w_words, g, c0, c1, PACK).rearrange("p (n t) -> p n t", t=PACK),
-                                  in_=w_columns(g, c0, c1))
+            half = c0 // HALF
+            src = w_wide[g, half][:, :, c0 - half * HALF : c1 - half * HALF]
+            nc.vector.tensor_copy(out=w_part(w_words, g, c0, c1, PACK).rearrange("p (c i t) -> p c t i", i=RUN, t=PACK),
+                                  in_=src.rearrange("p t (c i) -> p c t i", i=RUN))
 
         def lay_w(g, q, k):
             laid = bank([2, P * PACK], BF16)
@@ -125,7 +128,8 @@ def tile_equivariantfeedforward_pa_kernel(tc, h, x1, pre1, w1_0_bytes, w1_0_scal
             quantise(w_part(w_codes, g, c0, c1, 1), w_part(w_scales, g, c0, c1, 1), w_part(w_words, g, c0, c1, PACK))
 
         def interleave_pre():
-            nc.vector.tensor_copy(out=pre_words[:], in_=pre_raw[:].rearrange("p t e -> p e t"))
+            nc.vector.tensor_copy(out=pre_words[:].rearrange("p (c i) t -> p c t i", i=RUN),
+                                  in_=pre_raw[:].rearrange("p t (c i) -> p c t i", i=RUN))
 
         def quantise_pre():
             quantise(pre_codes[:], pre_scales[:], pre_words[:].rearrange("p e t -> p (e t)"))
@@ -204,12 +208,13 @@ def tile_equivariantfeedforward_pa_kernel(tc, h, x1, pre1, w1_0_bytes, w1_0_scal
 
         def start_loads():
             nc.scalar.dma_start(out=w_scale[:], in_=w1_0_scale.rearrange("(g p t) o -> p g (t o)", p=P, t=PACK))
-            load_x(0)
             load_w(0, 0, 0, 2)
+            load_x(0)
+            load_w(0, 0, 2, 3)
             nc.sync.dma_start(out=pre_raw[:], in_=pre1.rearrange("(p t) e -> p t e", t=PACK))
+            load_w(0, 0, 3, 4)
             load_h(0)
             load_x(1)
-            load_w(0, 0, 2, 4)
             load_h(1)
             load_x(2)
             load_h(2)
@@ -225,9 +230,9 @@ def tile_equivariantfeedforward_pa_kernel(tc, h, x1, pre1, w1_0_bytes, w1_0_scal
             make_identity(nc, ident_f32[:])
             make_identity(nc, ident_bf16[:])
 
-        tensor_steps = [(turn_xh, 0, 0,), (turn_xh, 0, 1,), (turn_xh, 1, 0,), (turn_xh, 1, 1,), (project, 0, 0,), (project, 0, 1,), (project, 0, 2,), (turn_xh, 2, 0,), (turn_xh, 2, 1,), (project, 1, 0,), (project, 1, 1,), (project, 1, 2,), (sum_squares, 0,), (turn_xh, 3, 0,), (turn_xh, 3, 1,), (lay_w, 0, 0, 0,), (lay_w, 0, 0, 1,), (project, 2, 0,), (project, 2, 1,), (project, 2, 2,), (sum_squares, 1,), (project, 3, 0,), (project, 3, 1,), (project, 3, 2,), (sum_squares, 2,), (lay_w, 0, 1, 0,), (lay_w, 0, 1, 1,), (multiply, 0, 0,), (sum_squares, 3,), (multiply, 1, 0,), (lay_w, 0, 2, 0,), (lay_w, 0, 2, 1,), (multiply, 2, 0,), (multiply, 3, 0,), (multiply, 0, 1,), (multiply, 1, 1,), (lay_w, 0, 3, 0,), (lay_w, 0, 3, 1,), (multiply, 2, 1,), (multiply, 3, 1,), (multiply, 0, 2,), (multiply, 1, 2,), (multiply, 2, 2,), (multiply, 3, 2,), (multiply, 0, 3,), (multiply, 1, 3,), (multiply, 2, 3,), (multiply, 3, 3,)]
-        scalar_steps = [(widen_on_scalar, 0, 0, 0,), (fetch_xh, 0, 0,), (fetch_xh, 0, 1,), (widen_on_scalar, 0, 0, 2,), (fetch_xh, 1, 0,), (fetch_xh, 1, 1,), (square, 0, 0,), (square, 0, 1,), (square, 0, 2,), (widen_on_scalar, 0, 0, 3,), (fetch_xh, 2, 0,), (fetch_xh, 2, 1,), (square, 1, 0,), (square, 1, 1,), (square, 1, 2,), (fetch_xh, 3, 0,), (fetch_xh, 3, 1,), (root, 0,), (square, 2, 0,), (square, 2, 1,), (square, 2, 2,), (fetch_w, 0, 0, 0,), (fetch_w, 0, 0, 1,), (root, 1,), (square, 3, 0,), (square, 3, 1,), (square, 3, 2,), (root, 2,), (fetch_w, 0, 1, 0,), (fetch_w, 0, 1, 1,), (widen_on_scalar, 0, 1, 3,), (root, 3,), (fetch_w, 0, 2, 0,), (fetch_w, 0, 2, 1,), (finish, 0, 2, 0,), (fetch_w, 0, 3, 0,), (fetch_w, 0, 3, 1,), (finish, 2, 4, 0,), (finish, 0, 2, 1,), (finish, 2, 4, 1,), (finish, 0, 2, 2,), (finish, 2, 4, 2,), (finish, 0, 1, 3,), (finish, 1, 2, 3,), (finish, 2, 3, 3,), (finish, 3, 4, 3,)]
-        vector_steps = [(split_x, 0,), (widen_on_vector, 0, 0, 1,), (interleave_pre,), (split_x, 1,), (quantise_pre,), (quantise_xh, 0, 0, 1,), (quantise_xh, 0, 1, 2,), (split_x, 2,), (widen_on_vector, 1, 0, 0,), (quantise_xh, 1, 0, 2,), (split_x, 3,), (widen_on_vector, 1, 0, 1,), (widen_on_vector, 1, 0, 2,), (widen_on_vector, 1, 0, 3,), (quantise_xh, 2, 0, 2,), (interleave_w, 1, 0,), (widen_on_vector, 0, 1, 0,), (widen_on_vector, 0, 1, 1,), (quantise_xh, 3, 0, 2,), (interleave_w, 1, 1,), (quantise_inv, 0,), (quantise_w, 1, 0, 1,), (widen_on_vector, 0, 1, 2,), (widen_on_vector, 1, 1, 0,), (quantise_w, 0, 0, 1,), (quantise_inv, 1,), (widen_on_vector, 1, 1, 1,), (widen_on_vector, 1, 1, 2,), (widen_on_vector, 1, 1, 3,), (quantise_w, 1, 1, 2,), (quantise_inv, 2,), (add_bias, 0, 0,), (quantise_w, 0, 1, 2,), (add_bias, 1, 0,), (quantise_inv, 3,), (interleave_w, 1, 2,), (add_bias, 2, 0,), (quantise_w, 1, 2, 3,), (add_bias, 3, 0,), (quantise_w, 0, 2, 3,), (add_bias, 0, 1,), (interleave_w, 1, 3,), (add_bias, 1, 1,), (quantise_w, 1, 3, 4,), (add_bias, 2, 1,), (quantise_w, 0, 3, 4,), (add_bias, 3, 1,), (add_bias, 0, 2,), (add_bias, 1, 2,), (add_bias, 2, 2,), (add_bias, 3, 2,), (add_bias, 0, 3,), (add_bias, 1, 3,), (add_bias, 2, 3,), (add_bias, 3, 3,)]
+        tensor_steps = [(turn_xh, 0, 0,), (turn_xh, 0, 1,), (lay_w, 0, 0, 0,), (turn_xh, 1, 0,), (turn_xh, 1, 1,), (project, 0, 0,), (project, 0, 1,), (project, 0, 2,), (lay_w, 0, 0, 1,), (turn_xh, 2, 0,), (turn_xh, 2, 1,), (project, 1, 0,), (project, 1, 1,), (project, 1, 2,), (sum_squares, 0,), (turn_xh, 3, 0,), (turn_xh, 3, 1,), (lay_w, 0, 1, 0,), (project, 2, 0,), (project, 2, 1,), (project, 2, 2,), (sum_squares, 1,), (lay_w, 0, 1, 1,), (project, 3, 0,), (project, 3, 1,), (project, 3, 2,), (sum_squares, 2,), (multiply, 0, 0,), (lay_w, 0, 2, 0,), (multiply, 1, 0,), (sum_squares, 3,), (lay_w, 0, 2, 1,), (multiply, 2, 0,), (multiply, 3, 0,), (multiply, 0, 1,), (multiply, 1, 1,), (lay_w, 0, 3, 0,), (lay_w, 0, 3, 1,), (multiply, 2, 1,), (multiply, 3, 1,), (multiply, 0, 2,), (multiply, 1, 2,), (multiply, 2, 2,), (multiply, 3, 2,), (multiply, 0, 3,), (multiply, 1, 3,), (multiply, 2, 3,), (multiply, 3, 3,)]
+        scalar_steps = [(widen_on_scalar, 0, 0, 0,), (widen_on_scalar, 0, 0, 2,), (widen_on_scalar, 0, 0, 3,), (fetch_xh, 0, 0,), (fetch_xh, 0, 1,), (fetch_w, 0, 0, 0,), (fetch_xh, 1, 0,), (fetch_xh, 1, 1,), (square, 0, 0,), (square, 0, 1,), (square, 0, 2,), (fetch_w, 0, 0, 1,), (fetch_xh, 2, 0,), (fetch_xh, 2, 1,), (square, 1, 0,), (square, 1, 1,), (square, 1, 2,), (fetch_xh, 3, 0,), (fetch_xh, 3, 1,), (root, 0,), (fetch_w, 0, 1, 0,), (square, 2, 0,), (square, 2, 1,), (square, 2, 2,), (root, 1,), (fetch_w, 0, 1, 1,), (widen_on_scalar, 0, 1, 3,), (square, 3, 0,), (square, 3, 1,), (square, 3, 2,), (root, 2,), (widen_on_scalar, 1, 1, 3,), (root, 3,), (fetch_w, 0, 2, 0,), (fetch_w, 0, 2, 1,), (finish, 0, 2, 0,), (fetch_w, 0, 3, 0,), (fetch_w, 0, 3, 1,), (finish, 2, 4, 0,), (finish, 0, 2, 1,), (finish, 2, 4, 1,), (finish, 0, 2, 2,), (finish, 2, 3, 2,), (finish, 3, 4, 2,), (finish, 0, 1, 3,), (finish, 1, 2, 3,), (finish, 2, 3, 3,), (finish, 3, 4, 3,)]
+        vector_steps = [(widen_on_vector, 0, 0, 1,), (split_x, 0,), (interleave_pre,), (split_x, 1,), (quantise_pre,), (quantise_xh, 0, 0, 1,), (quantise_xh, 0, 1, 2,), (split_x, 2,), (widen_on_vector, 1, 0, 0,), (quantise_xh, 1, 0, 2,), (split_x, 3,), (widen_on_vector, 1, 0, 1,), (widen_on_vector, 1, 0, 2,), (widen_on_vector, 1, 0, 3,), (quantise_xh, 2, 0, 2,), (interleave_w, 1, 0,), (widen_on_vector, 0, 1, 0,), (widen_on_vector, 0, 1, 1,), (quantise_xh, 3, 0, 2,), (widen_on_vector, 0, 1, 2,), (quantise_inv, 0,), (quantise_w, 1, 0, 1,), (interleave_w, 1, 1,), (quantise_w, 0, 0, 1,), (quantise_inv, 1,), (widen_on_vector, 1, 1, 0,), (widen_on_vector, 1, 1, 1,), (widen_on_vector, 1, 1, 2,), (quantise_w, 1, 1, 2,), (add_bias, 0, 0,), (quantise_w, 0, 1, 2,), (quantise_inv, 2,), (add_bias, 1, 0,), (interleave_w, 1, 2,), (quantise_inv, 3,), (add_bias, 2, 0,), (quantise_w, 1, 2, 3,), (add_bias, 3, 0,), (quantise_w, 0, 2, 3,), (add_bias, 0, 1,), (add_bias, 1, 1,), (add_bias, 2, 1,), (add_bias, 3, 1,), (add_bias, 0, 2,), (interleave_w, 1, 3,), (add_bias, 1, 2,), (quantise_w, 1, 3, 4,), (quantise_w, 0, 3, 4,), (add_bias, 2, 2,), (add_bias, 3, 2,), (add_bias, 0, 3,), (add_bias, 1, 3,), (add_bias, 2, 3,), (add_bias, 3, 3,)]
 
         def inputs_of(work, *a):
             if work is turn_xh:

@@ -24,7 +24,6 @@ NQ = FF // BANK
 
 FLOPS = 2 * NT * P * M1 * D * D + 2 * NT * P * 2 * D * FF
 PSUM_BANKS = 8
-RUN = 4
 
 
 def tile_equivariantfeedforward_pa_kernel(tc, h, x1, pre1, w1_0_bytes, w1_0_scale, b1_0, out):
@@ -106,10 +105,8 @@ def tile_equivariantfeedforward_pa_kernel(tc, h, x1, pre1, w1_0_bytes, w1_0_scal
 
         def interleave_w(g, q):
             c0, c1 = q * BANK, (q + 1) * BANK
-            half = c0 // HALF
-            src = w_wide[g, half][:, :, c0 - half * HALF : c1 - half * HALF]
-            nc.vector.tensor_copy(out=w_part(w_words, g, c0, c1, PACK).rearrange("p (c i t) -> p c t i", i=RUN, t=PACK),
-                                  in_=src.rearrange("p t (c i) -> p c t i", i=RUN))
+            nc.vector.tensor_copy(out=w_part(w_words, g, c0, c1, PACK).rearrange("p (n t) -> p n t", t=PACK),
+                                  in_=w_columns(g, c0, c1))
 
         def lay_w(g, q, k):
             laid = bank([2, P * PACK], BF16)
@@ -128,8 +125,7 @@ def tile_equivariantfeedforward_pa_kernel(tc, h, x1, pre1, w1_0_bytes, w1_0_scal
             quantise(w_part(w_codes, g, c0, c1, 1), w_part(w_scales, g, c0, c1, 1), w_part(w_words, g, c0, c1, PACK))
 
         def interleave_pre():
-            nc.vector.tensor_copy(out=pre_words[:].rearrange("p (c i) t -> p c t i", i=RUN),
-                                  in_=pre_raw[:].rearrange("p t (c i) -> p c t i", i=RUN))
+            nc.vector.tensor_copy(out=pre_words[:], in_=pre_raw[:].rearrange("p t e -> p e t"))
 
         def quantise_pre():
             quantise(pre_codes[:], pre_scales[:], pre_words[:].rearrange("p e t -> p (e t)"))

@@ -24,6 +24,7 @@ NQ = FF // BANK
 
 FLOPS = 2 * NT * P * M1 * D * D + 2 * NT * P * 2 * D * FF
 PSUM_BANKS = 8
+STAGE2_BANKS = 4
 
 
 def tile_equivariantfeedforward_pa_kernel(tc, h, x1, pre1, w1_0_bytes, w1_0_scale, b1_0, out):
@@ -38,7 +39,7 @@ def tile_equivariantfeedforward_pa_kernel(tc, h, x1, pre1, w1_0_bytes, w1_0_scal
         banks_taken = []
 
         def bank(shape, dtype):
-            n = len(banks_taken) % PSUM_BANKS
+            n = bank_of[len(banks_taken)]
             banks_taken.append(n)
             return psum.tile([P] + shape, dtype, name=f"bank{n}")
 
@@ -67,7 +68,6 @@ def tile_equivariantfeedforward_pa_kernel(tc, h, x1, pre1, w1_0_bytes, w1_0_scal
         ident_bf16 = sbuf("ident_bf16", [P], BF16)
 
         w_wide = {(g, half): sbuf(f"w_wide{g}{half}", [PACK, HALF], BF16) for g in range(2) for half in range(2)}
-        w_words = {(g, half): sbuf(f"w_words{g}{half}", [HALF * PACK], BF16) for g in range(2) for half in range(2)}
         w_codes = {(g, half): sbuf(f"w_codes{g}{half}", [HALF], U32) for g in range(2) for half in range(2)}
         w_scales = {(g, half): sbuf(f"w_scales{g}{half}", [HALF], U8) for g in range(2) for half in range(2)}
         pre_words = sbuf("pre_words", [D, PACK], BF16)
@@ -103,10 +103,19 @@ def tile_equivariantfeedforward_pa_kernel(tc, h, x1, pre1, w1_0_bytes, w1_0_scal
             half = c0 // HALF
             return parts[g, half][:, (c0 - half * HALF) * width : (c1 - half * HALF) * width]
 
+        def words_tile(g, q):
+            words = sbuf(f"w_words{words_slot[g, q]}", [BANK * PACK], BF16)
+            held["words", g, q] = words
+            return words
+
         def interleave_w(g, q):
-            c0, c1 = q * BANK, (q + 1) * BANK
-            nc.vector.tensor_copy(out=w_part(w_words, g, c0, c1, PACK).rearrange("p (n t) -> p n t", t=PACK),
-                                  in_=w_columns(g, c0, c1))
+            nc.vector.tensor_copy(out=words_tile(g, q)[:].rearrange("p (n t) -> p n t", t=PACK),
+                                  in_=w_columns(g, q * BANK, (q + 1) * BANK))
+
+        def interleave_w_on_gpsimd(g, q):
+            nc.gpsimd.tensor_scalar(out=words_tile(g, q)[:].rearrange("p (n t) -> p n t", t=PACK),
+                                    in0=w_columns(g, q * BANK, (q + 1) * BANK),
+                                    scalar1=1.0, scalar2=0.0, op0=ALU.mult, op1=ALU.add)
 
         def lay_w(g, q, k):
             laid = bank([2, P * PACK], BF16)
@@ -116,16 +125,17 @@ def tile_equivariantfeedforward_pa_kernel(tc, h, x1, pre1, w1_0_bytes, w1_0_scal
             held["w", g, q, k] = laid
 
         def fetch_w(g, q, k):
-            c0 = q * BANK + 2 * k * P
-            nc.scalar.copy(out=w_part(w_words, g, c0, c0 + 2 * P, PACK),
+            words = words_tile(g, q) if k == 0 else held["words", g, q]
+            nc.scalar.copy(out=words[:, k * 2 * P * PACK : (k + 1) * 2 * P * PACK],
                            in_=held["w", g, q, k][:].rearrange("p j c -> p (j c)"))
 
-        def quantise_w(g, q0, q1):
-            c0, c1 = q0 * BANK, q1 * BANK
-            quantise(w_part(w_codes, g, c0, c1, 1), w_part(w_scales, g, c0, c1, 1), w_part(w_words, g, c0, c1, PACK))
+        def quantise_w(g, q, q1):
+            c0, c1 = q * BANK, q1 * BANK
+            quantise(w_part(w_codes, g, c0, c1, 1), w_part(w_scales, g, c0, c1, 1), held["words", g, q][:])
 
         def interleave_pre():
-            nc.vector.tensor_copy(out=pre_words[:], in_=pre_raw[:].rearrange("p t e -> p e t"))
+            nc.vector.tensor_copy(out=pre_words[:].rearrange("p (r c) t -> p r c t", r=PACK),
+                                  in_=pre_raw[:].rearrange("p t (c r) -> p r c t", r=PACK))
 
         def quantise_pre():
             quantise(pre_codes[:], pre_scales[:], pre_words[:].rearrange("p e t -> p (e t)"))
@@ -164,8 +174,7 @@ def tile_equivariantfeedforward_pa_kernel(tc, h, x1, pre1, w1_0_bytes, w1_0_scal
             held["pm", i, m] = pm
 
         def square(i, m):
-            nc.scalar.activation(out=squares[i, m][:], in_=held["pm", i, m][:].rearrange("p (c t) -> p t c", t=PACK),
-                                 func=ACT.Square)
+            nc.scalar.activation(out=squares[i, m][:].rearrange("p t c -> p (t c)"), in_=held["pm", i, m][:], func=ACT.Square)
 
         def sum_squares(i):
             total = bank([PACK, P], F32)
@@ -226,9 +235,12 @@ def tile_equivariantfeedforward_pa_kernel(tc, h, x1, pre1, w1_0_bytes, w1_0_scal
             make_identity(nc, ident_f32[:])
             make_identity(nc, ident_bf16[:])
 
-        tensor_steps = [(turn_xh, 0, 0,), (turn_xh, 0, 1,), (lay_w, 0, 0, 0,), (turn_xh, 1, 0,), (turn_xh, 1, 1,), (project, 0, 0,), (project, 0, 1,), (project, 0, 2,), (lay_w, 0, 0, 1,), (turn_xh, 2, 0,), (turn_xh, 2, 1,), (project, 1, 0,), (project, 1, 1,), (project, 1, 2,), (sum_squares, 0,), (turn_xh, 3, 0,), (turn_xh, 3, 1,), (lay_w, 0, 1, 0,), (project, 2, 0,), (project, 2, 1,), (project, 2, 2,), (sum_squares, 1,), (lay_w, 0, 1, 1,), (project, 3, 0,), (project, 3, 1,), (project, 3, 2,), (sum_squares, 2,), (multiply, 0, 0,), (lay_w, 0, 2, 0,), (multiply, 1, 0,), (sum_squares, 3,), (lay_w, 0, 2, 1,), (multiply, 2, 0,), (multiply, 3, 0,), (multiply, 0, 1,), (multiply, 1, 1,), (lay_w, 0, 3, 0,), (lay_w, 0, 3, 1,), (multiply, 2, 1,), (multiply, 3, 1,), (multiply, 0, 2,), (multiply, 1, 2,), (multiply, 2, 2,), (multiply, 3, 2,), (multiply, 0, 3,), (multiply, 1, 3,), (multiply, 2, 3,), (multiply, 3, 3,)]
-        scalar_steps = [(widen_on_scalar, 0, 0, 0,), (widen_on_scalar, 0, 0, 2,), (widen_on_scalar, 0, 0, 3,), (fetch_xh, 0, 0,), (fetch_xh, 0, 1,), (fetch_w, 0, 0, 0,), (fetch_xh, 1, 0,), (fetch_xh, 1, 1,), (square, 0, 0,), (square, 0, 1,), (square, 0, 2,), (fetch_w, 0, 0, 1,), (fetch_xh, 2, 0,), (fetch_xh, 2, 1,), (square, 1, 0,), (square, 1, 1,), (square, 1, 2,), (fetch_xh, 3, 0,), (fetch_xh, 3, 1,), (root, 0,), (fetch_w, 0, 1, 0,), (square, 2, 0,), (square, 2, 1,), (square, 2, 2,), (root, 1,), (fetch_w, 0, 1, 1,), (widen_on_scalar, 0, 1, 3,), (square, 3, 0,), (square, 3, 1,), (square, 3, 2,), (root, 2,), (widen_on_scalar, 1, 1, 3,), (root, 3,), (fetch_w, 0, 2, 0,), (fetch_w, 0, 2, 1,), (finish, 0, 2, 0,), (fetch_w, 0, 3, 0,), (fetch_w, 0, 3, 1,), (finish, 2, 4, 0,), (finish, 0, 2, 1,), (finish, 2, 4, 1,), (finish, 0, 2, 2,), (finish, 2, 3, 2,), (finish, 3, 4, 2,), (finish, 0, 1, 3,), (finish, 1, 2, 3,), (finish, 2, 3, 3,), (finish, 3, 4, 3,)]
-        vector_steps = [(widen_on_vector, 0, 0, 1,), (split_x, 0,), (interleave_pre,), (split_x, 1,), (quantise_pre,), (quantise_xh, 0, 0, 1,), (quantise_xh, 0, 1, 2,), (split_x, 2,), (widen_on_vector, 1, 0, 0,), (quantise_xh, 1, 0, 2,), (split_x, 3,), (widen_on_vector, 1, 0, 1,), (widen_on_vector, 1, 0, 2,), (widen_on_vector, 1, 0, 3,), (quantise_xh, 2, 0, 2,), (interleave_w, 1, 0,), (widen_on_vector, 0, 1, 0,), (widen_on_vector, 0, 1, 1,), (quantise_xh, 3, 0, 2,), (widen_on_vector, 0, 1, 2,), (quantise_inv, 0,), (quantise_w, 1, 0, 1,), (interleave_w, 1, 1,), (quantise_w, 0, 0, 1,), (quantise_inv, 1,), (widen_on_vector, 1, 1, 0,), (widen_on_vector, 1, 1, 1,), (widen_on_vector, 1, 1, 2,), (quantise_w, 1, 1, 2,), (add_bias, 0, 0,), (quantise_w, 0, 1, 2,), (quantise_inv, 2,), (add_bias, 1, 0,), (interleave_w, 1, 2,), (quantise_inv, 3,), (add_bias, 2, 0,), (quantise_w, 1, 2, 3,), (add_bias, 3, 0,), (quantise_w, 0, 2, 3,), (add_bias, 0, 1,), (add_bias, 1, 1,), (add_bias, 2, 1,), (add_bias, 3, 1,), (add_bias, 0, 2,), (interleave_w, 1, 3,), (add_bias, 1, 2,), (quantise_w, 1, 3, 4,), (quantise_w, 0, 3, 4,), (add_bias, 2, 2,), (add_bias, 3, 2,), (add_bias, 0, 3,), (add_bias, 1, 3,), (add_bias, 2, 3,), (add_bias, 3, 3,)]
+        tensor_steps = [(turn_xh, 0, 0,), (turn_xh, 0, 1,), (lay_w, 0, 0, 0,), (turn_xh, 1, 0,), (turn_xh, 1, 1,), (project, 0, 0,), (project, 0, 1,), (project, 0, 2,), (lay_w, 0, 0, 1,), (turn_xh, 2, 0,), (turn_xh, 2, 1,), (project, 1, 0,), (project, 1, 1,), (project, 1, 2,), (sum_squares, 0,), (turn_xh, 3, 0,), (turn_xh, 3, 1,), (lay_w, 0, 1, 0,), (project, 2, 0,), (project, 2, 1,), (project, 2, 2,), (sum_squares, 1,), (lay_w, 0, 1, 1,), (project, 3, 0,), (project, 3, 1,), (project, 3, 2,), (sum_squares, 2,), (lay_w, 0, 2, 0,), (multiply, 0, 0,), (lay_w, 0, 2, 1,), (multiply, 1, 0,), (sum_squares, 3,), (multiply, 2, 0,), (multiply, 0, 1,), (lay_w, 0, 3, 0,), (multiply, 3, 0,), (lay_w, 0, 3, 1,), (multiply, 1, 1,), (multiply, 2, 1,), (multiply, 3, 1,), (multiply, 0, 2,), (multiply, 1, 2,), (multiply, 2, 2,), (multiply, 3, 2,), (multiply, 0, 3,), (multiply, 1, 3,), (multiply, 2, 3,), (multiply, 3, 3,)]
+        scalar_steps = [(widen_on_scalar, 0, 0, 0,), (widen_on_scalar, 0, 0, 2,), (widen_on_scalar, 0, 0, 3,), (fetch_xh, 0, 0,), (fetch_xh, 0, 1,), (fetch_w, 0, 0, 0,), (fetch_xh, 1, 0,), (fetch_xh, 1, 1,), (square, 0, 0,), (square, 0, 1,), (square, 0, 2,), (fetch_w, 0, 0, 1,), (fetch_xh, 2, 0,), (fetch_xh, 2, 1,), (square, 1, 0,), (square, 1, 1,), (square, 1, 2,), (fetch_xh, 3, 0,), (fetch_xh, 3, 1,), (root, 0,), (fetch_w, 0, 1, 0,), (square, 2, 0,), (square, 2, 1,), (square, 2, 2,), (root, 1,), (fetch_w, 0, 1, 1,), (square, 3, 0,), (square, 3, 1,), (square, 3, 2,), (root, 2,), (fetch_w, 0, 2, 0,), (fetch_w, 0, 2, 1,), (root, 3,), (finish, 0, 2, 0,), (fetch_w, 0, 3, 0,), (fetch_w, 0, 3, 1,), (finish, 2, 4, 0,), (finish, 0, 2, 1,), (finish, 2, 4, 1,), (finish, 0, 2, 2,), (finish, 2, 3, 2,), (finish, 3, 4, 2,), (finish, 0, 1, 3,), (finish, 1, 2, 3,), (finish, 2, 3, 3,), (finish, 3, 4, 3,)]
+        vector_steps = [(widen_on_vector, 0, 0, 1,), (split_x, 0,), (interleave_pre,), (split_x, 1,), (quantise_pre,), (quantise_xh, 0, 0, 1,), (quantise_xh, 0, 1, 2,), (split_x, 2,), (widen_on_vector, 1, 0, 0,), (quantise_xh, 1, 0, 2,), (split_x, 3,), (widen_on_vector, 1, 0, 1,), (widen_on_vector, 1, 0, 2,), (widen_on_vector, 1, 0, 3,), (quantise_xh, 2, 0, 2,), (interleave_w, 1, 0,), (widen_on_vector, 0, 1, 0,), (quantise_w, 0, 0, 1,), (quantise_xh, 3, 0, 2,), (quantise_w, 1, 0, 1,), (widen_on_vector, 0, 1, 1,), (quantise_inv, 0,), (widen_on_vector, 0, 1, 2,), (widen_on_vector, 0, 1, 3,), (interleave_w, 1, 1,), (quantise_inv, 1,), (widen_on_vector, 1, 1, 0,), (widen_on_vector, 1, 1, 1,), (quantise_w, 1, 1, 2,), (widen_on_vector, 1, 1, 2,), (quantise_inv, 2,), (quantise_w, 0, 1, 2,), (quantise_w, 0, 2, 3,), (quantise_inv, 3,), (widen_on_vector, 1, 1, 3,), (add_bias, 0, 0,), (add_bias, 1, 0,), (add_bias, 2, 0,), (add_bias, 0, 1,), (add_bias, 3, 0,), (quantise_w, 1, 2, 3,), (add_bias, 1, 1,), (add_bias, 2, 1,), (add_bias, 3, 1,), (add_bias, 0, 2,), (add_bias, 1, 2,), (quantise_w, 0, 3, 4,), (quantise_w, 1, 3, 4,), (add_bias, 2, 2,), (add_bias, 3, 2,), (add_bias, 0, 3,), (add_bias, 1, 3,), (add_bias, 2, 3,), (add_bias, 3, 3,)]
+        gpsimd_steps = [(interleave_w_on_gpsimd, 1, 2,), (interleave_w_on_gpsimd, 1, 3,)]
+
+        gate = {(1, 3): (1, 2)}
 
         def inputs_of(work, *a):
             if work is turn_xh:
@@ -249,12 +261,12 @@ def tile_equivariantfeedforward_pa_kernel(tc, h, x1, pre1, w1_0_bytes, w1_0_scal
                 return [(sum_squares, *a)]
             if work is quantise_inv:
                 return [(root, *a)]
-            if work in (lay_w, interleave_w):
+            if work in (lay_w, interleave_w, interleave_w_on_gpsimd):
                 return [s for s in steps if s[0] in (widen_on_vector, widen_on_scalar) and s[1:3] == (a[0], a[1] // 2)]
             if work is fetch_w:
                 return [(lay_w, *a)]
             if work is quantise_w:
-                return [s for s in steps if s[0] in (fetch_w, interleave_w) and s[1] == a[0] and a[1] <= s[2] < a[2]]
+                return [s for s in steps if s[0] in (fetch_w, interleave_w, interleave_w_on_gpsimd) and s[1] == a[0] and a[1] <= s[2] < a[2]]
             if work is multiply:
                 return [(quantise_inv, a[0]), covering(quantise_xh, a[0], 1)] + [covering(quantise_w, g, a[1]) for g in range(2)]
             if work is add_bias:
@@ -267,22 +279,36 @@ def tile_equivariantfeedforward_pa_kernel(tc, h, x1, pre1, w1_0_bytes, w1_0_scal
             return [s for s in steps if s[0] is work and s[1] == which and s[2] <= part < s[3]][0]
 
         emptied_by = {turn_xh: fetch_xh, project: square, sum_squares: root, lay_w: fetch_w, multiply: add_bias}
-        queues = [tensor_steps, scalar_steps, vector_steps]
-        steps = tensor_steps + scalar_steps + vector_steps
+        queues = [tensor_steps, scalar_steps, vector_steps, gpsimd_steps]
+        steps = tensor_steps + scalar_steps + vector_steps + gpsimd_steps
+        bank_of = []
+        for s in tensor_steps:
+            if s[0] is multiply:
+                allowed = range(PSUM_BANKS - STAGE2_BANKS, PSUM_BANKS)
+            elif any(r[0] is multiply for r in tensor_steps[: len(bank_of)]):
+                allowed = range(PSUM_BANKS - STAGE2_BANKS)
+            else:
+                allowed = range(PSUM_BANKS)
+            bank_of.append(min(allowed, key=lambda n: max([-1] + [k for k in range(len(bank_of)) if bank_of[k] == n])))
+        words_slot = {(g, q): f"{g}{q}" for g in range(2) for q in range(NQ)}
+        for late in gate:
+            words_slot[late] = words_slot[gate[late]]
         written = set()
-        at = [0, 0, 0]
+        at = [0, 0, 0, 0]
         with tc.manual_schedule():
             start_loads()
             while len(written) < len(steps):
                 before = len(written)
-                for e in range(3):
+                for e in range(4):
                     if at[e] == len(queues[e]):
                         continue
                     s = queues[e][at[e]]
                     needs = inputs_of(*s)
-                    if e == 0 and at[0] >= PSUM_BANKS:
-                        old = tensor_steps[at[0] - PSUM_BANKS]
+                    if e == 0 and bank_of[at[0]] in bank_of[: at[0]]:
+                        old = [tensor_steps[n] for n in range(at[0]) if bank_of[n] == bank_of[at[0]]][-1]
                         needs = needs + [(emptied_by[old[0]], *old[1:])]
+                    if s[1:] in gate and s[0] is interleave_w_on_gpsimd:
+                        needs = needs + [covering(quantise_w, *gate[s[1:]])]
                     if all(n in written for n in needs):
                         s[0](*s[1:])
                         written.add(s)

@@ -21,10 +21,12 @@ NT = 4
 BANK = 512
 HALF = FF // 2
 NQ = FF // BANK
+UNITS = M1 + 1
+PSUM_BANKS = 8
+PRODUCT_BANKS = 4
+BIAS_RUN = 5
 
 FLOPS = 2 * NT * P * M1 * D * D + 2 * NT * P * 2 * D * FF
-PSUM_BANKS = 8
-STAGE2_BANKS = 4
 
 
 def tile_equivariantfeedforward_pa_kernel(tc, h, x1, pre1, w1_0_bytes, w1_0_scale, b1_0, out):
@@ -36,14 +38,23 @@ def tile_equivariantfeedforward_pa_kernel(tc, h, x1, pre1, w1_0_bytes, w1_0_scal
         def sbuf(name, shape, dtype):
             return keep.tile([P] + shape, dtype, name=name, align_bytes=64)
 
-        banks_taken = []
+        taken = {"stage 1": 0, "products": 0, "beside products": 0}
 
-        def bank(shape, dtype):
-            n = bank_of[len(banks_taken)]
-            banks_taken.append(n)
+        def bank(shape, dtype, product=False):
+            others = PSUM_BANKS - PRODUCT_BANKS
+            if product:
+                n = others + taken["products"] % PRODUCT_BANKS
+                taken["products"] += 1
+            elif taken["products"]:
+                n = taken["beside products"] % others
+                taken["beside products"] += 1
+            else:
+                n = taken["stage 1"] % PSUM_BANKS
+                taken["stage 1"] += 1
             return psum.tile([P] + shape, dtype, name=f"bank{n}")
 
         tiles = range(NT)
+        halves = [(g, half) for g in range(2) for half in range(2)]
         w_rows = w1_0_bytes.rearrange("(g p t) n -> g p t n", p=P, t=PACK)
         w_bytes = {}
         x_raw = [sbuf(f"x_raw{i}", [D * M1], BF16) for i in tiles]
@@ -51,6 +62,25 @@ def tile_equivariantfeedforward_pa_kernel(tc, h, x1, pre1, w1_0_bytes, w1_0_scal
         pre_raw = sbuf("pre_raw", [PACK, D], BF16)
         w_scale = sbuf("w_scale", [2, PACK], F32)
         bias = sbuf("bias", [FF], BF16)
+        ident_f32 = sbuf("ident_f32", [P], F32)
+        ident_bf16 = sbuf("ident_bf16", [P], BF16)
+        w_wide = {gh: sbuf(f"w_wide{gh[0]}{gh[1]}", [PACK, HALF], BF16) for gh in halves}
+        w_words = {}
+        w_codes = [sbuf(f"w_codes{q}", [2 * BANK], U32) for q in range(NQ)]
+        w_scales = [sbuf(f"w_scales{q}", [2 * BANK], U8) for q in range(NQ)]
+        pre_words = sbuf("pre_words", [D, PACK], BF16)
+        pre_codes = sbuf("pre_codes", [D], U32)
+        pre_scales = sbuf("pre_scales", [D], U8)
+        x_split = [sbuf(f"x_split{i}", [M1, D], BF16) for i in tiles]
+        xh_words = [sbuf(f"xh_words{i}", [UNITS * P * PACK], BF16) for i in tiles]
+        xh_codes = [sbuf(f"xh_codes{i}", [UNITS * P], U32) for i in tiles]
+        xh_scales = [sbuf(f"xh_scales{i}", [UNITS * P], U8) for i in tiles]
+        squares = {(i, m): sbuf(f"squares{i}{m}", [PACK, P], F32) for i in tiles for m in range(M1)}
+        inv_words = [sbuf(f"inv_words{i}", [P, PACK], BF16) for i in tiles]
+        inv_codes = [sbuf(f"inv_codes{i}", [P], U32) for i in tiles]
+        inv_scales = [sbuf(f"inv_scales{i}", [P], U8) for i in tiles]
+        rows = [sbuf(f"rows{q}", [NT * BANK], F32) for q in range(NQ)]
+        held = {}
 
         def load_w(g, half, t0, t1):
             raw = sbuf(f"w_bytes{g}{half}{t0}", [t1 - t0, HALF], U8)
@@ -63,26 +93,6 @@ def tile_equivariantfeedforward_pa_kernel(tc, h, x1, pre1, w1_0_bytes, w1_0_scal
 
         def load_h(i):
             nc.sync.dma_start(out=h_raw[i][:], in_=h[i])
-
-        ident_f32 = sbuf("ident_f32", [P], F32)
-        ident_bf16 = sbuf("ident_bf16", [P], BF16)
-
-        w_wide = {(g, half): sbuf(f"w_wide{g}{half}", [PACK, HALF], BF16) for g in range(2) for half in range(2)}
-        w_codes = {(g, half): sbuf(f"w_codes{g}{half}", [HALF], U32) for g in range(2) for half in range(2)}
-        w_scales = {(g, half): sbuf(f"w_scales{g}{half}", [HALF], U8) for g in range(2) for half in range(2)}
-        pre_words = sbuf("pre_words", [D, PACK], BF16)
-        pre_codes = sbuf("pre_codes", [D], U32)
-        pre_scales = sbuf("pre_scales", [D], U8)
-        x_split = [sbuf(f"x_split{i}", [M1, D], BF16) for i in tiles]
-        xh_words = [sbuf(f"xh_words{i}", [(M1 + 1) * P * PACK], BF16) for i in tiles]
-        xh_codes = [sbuf(f"xh_codes{i}", [(M1 + 1) * P], U32) for i in tiles]
-        xh_scales = [sbuf(f"xh_scales{i}", [(M1 + 1) * P], U8) for i in tiles]
-        squares = {(i, m): sbuf(f"squares{i}{m}", [PACK, P], F32) for i in tiles for m in range(M1)}
-        inv_words = [sbuf(f"inv_words{i}", [P, PACK], BF16) for i in tiles]
-        inv_codes = [sbuf(f"inv_codes{i}", [P], U32) for i in tiles]
-        inv_scales = [sbuf(f"inv_scales{i}", [P], U8) for i in tiles]
-        rows = [sbuf(f"rows{q}", [NT * BANK], F32) for q in range(NQ)]
-        held = {}
 
         def quantise(codes, scales, words):
             nc.vector.quantize_mx(out=codes.bitcast(FP8X4), scales=scales, in_=words)
@@ -99,39 +109,40 @@ def tile_equivariantfeedforward_pa_kernel(tc, h, x1, pre1, w1_0_bytes, w1_0_scal
             half = c0 // HALF
             return w_wide[g, half][:, :, c0 - half * HALF : c1 - half * HALF].rearrange("p t n -> p n t")
 
-        def w_part(parts, g, c0, c1, width):
-            half = c0 // HALF
-            return parts[g, half][:, (c0 - half * HALF) * width : (c1 - half * HALF) * width]
+        def words_of(g, q):
+            if (g, q) not in w_words:
+                w_words[g, q] = sbuf(f"w_words{g}{min(q, NQ - 1 - g)}", [BANK * PACK], BF16)
+            return w_words[g, q][:]
 
-        def words_tile(g, q):
-            words = sbuf(f"w_words{words_slot[g, q]}", [BANK * PACK], BF16)
-            held["words", g, q] = words
-            return words
+        def interleave_w_on_vector(q):
+            nc.vector.tensor_copy(out=words_of(1, q).rearrange("p (n t) -> p n t", t=PACK),
+                                  in_=w_columns(1, q * BANK, (q + 1) * BANK))
 
-        def interleave_w(g, q):
-            nc.vector.tensor_copy(out=words_tile(g, q)[:].rearrange("p (n t) -> p n t", t=PACK),
-                                  in_=w_columns(g, q * BANK, (q + 1) * BANK))
-
-        def interleave_w_on_gpsimd(g, q):
-            nc.gpsimd.tensor_scalar(out=words_tile(g, q)[:].rearrange("p (n t) -> p n t", t=PACK),
-                                    in0=w_columns(g, q * BANK, (q + 1) * BANK),
+        def interleave_w_on_gpsimd(q):
+            nc.gpsimd.tensor_scalar(out=words_of(1, q).rearrange("p (n t) -> p n t", t=PACK),
+                                    in0=w_columns(1, q * BANK, (q + 1) * BANK),
                                     scalar1=1.0, scalar2=0.0, op0=ALU.mult, op1=ALU.add)
 
-        def lay_w(g, q, k):
+        def lay_w(n):
             laid = bank([2, P * PACK], BF16)
             for j in range(2):
-                c0 = q * BANK + (2 * k + j) * P
-                nc.tensor.matmul(laid[:, j, :], lhsT=ident_bf16[:], rhs=w_columns(g, c0, c0 + P), start=True, stop=True)
-            held["w", g, q, k] = laid
+                c0 = (2 * n + j) * P
+                nc.tensor.matmul(laid[:, j, :], lhsT=ident_bf16[:], rhs=w_columns(0, c0, c0 + P), start=True, stop=True)
+            held["w", n] = laid
 
-        def fetch_w(g, q, k):
-            words = words_tile(g, q) if k == 0 else held["words", g, q]
-            nc.scalar.copy(out=words[:, k * 2 * P * PACK : (k + 1) * 2 * P * PACK],
-                           in_=held["w", g, q, k][:].rearrange("p j c -> p (j c)"))
+        def fetch_w(n, on_vector=False):
+            width = 2 * P * PACK
+            dst = words_of(0, n // 2)[:, n % 2 * width : (n % 2 + 1) * width]
+            src = held["w", n][:].rearrange("p j c -> p (j c)")
+            if on_vector:
+                nc.vector.tensor_copy(out=dst, in_=src)
+            else:
+                nc.scalar.copy(out=dst, in_=src)
 
-        def quantise_w(g, q, q1):
-            c0, c1 = q * BANK, q1 * BANK
-            quantise(w_part(w_codes, g, c0, c1, 1), w_part(w_scales, g, c0, c1, 1), held["words", g, q][:])
+        def quantise_w(q):
+            for g in range(2):
+                c = slice(g * BANK, (g + 1) * BANK)
+                quantise(w_codes[q][:, c], w_scales[q][:, c], w_words[g, q][:])
 
         def interleave_pre():
             nc.vector.tensor_copy(out=pre_words[:].rearrange("p (r c) t -> p r c t", r=PACK),
@@ -144,60 +155,63 @@ def tile_equivariantfeedforward_pa_kernel(tc, h, x1, pre1, w1_0_bytes, w1_0_scal
             nc.vector.tensor_copy(out=x_split[i][:].rearrange("p m (a d) -> p a m d", a=2),
                                   in_=x_raw[i][:].rearrange("p (a d m) -> p a m d", a=2, m=M1))
 
-        def turn_xh(i, b):
-            turned = bank([2, 2, P], F32)
-            for j in range(2):
-                m = 2 * b + j
-                words = (x_split[i][:, m, :] if m < M1 else h_raw[i][:]).bitcast(F32)
-                for u in range(2):
-                    nc.tensor.transpose(turned[:, j, u, :], words[:, u : D // 2 : 2], ident_f32[:])
-            held["xh", i, b] = turned
+        def turn_xh(i):
+            for b in range(2):
+                turned = bank([2, 2, P], F32)
+                for j in range(2):
+                    m = 2 * b + j
+                    words = (x_split[i][:, m, :] if m < M1 else h_raw[i][:]).bitcast(F32)
+                    for u in range(2):
+                        nc.tensor.transpose(turned[:, j, u, :], words[:, u : D // 2 : 2], ident_f32[:])
+                held["xh", i, b] = turned
 
-        def fetch_xh(i, b):
-            dst = xh_words[i][:, b * 2 * P * PACK : (b + 1) * 2 * P * PACK].bitcast(F32)
-            nc.scalar.copy(out=dst.rearrange("p (j n u) -> p j n u", j=2, u=2),
-                           in_=held["xh", i, b][:].rearrange("p j u n -> p j n u"))
+        def fetch_xh(i):
+            for b in range(2):
+                dst = xh_words[i][:, b * 2 * P * PACK : (b + 1) * 2 * P * PACK].bitcast(F32)
+                nc.scalar.copy(out=dst.rearrange("p (j n u) -> p j n u", j=2, u=2),
+                               in_=held["xh", i, b][:].rearrange("p j u n -> p j n u"))
 
-        def quantise_xh(i, b0, b1):
-            c = slice(b0 * 2 * P, b1 * 2 * P)
-            quantise(xh_codes[i][:, c], xh_scales[i][:, c], xh_words[i][:, b0 * 2 * P * PACK : b1 * 2 * P * PACK])
+        def quantise_xh(i):
+            quantise(xh_codes[i][:], xh_scales[i][:], xh_words[i][:])
 
         def xh_operand(i, m):
             c = slice(m * P, (m + 1) * P)
             return xh_codes[i][:, c].bitcast(FP8X4), xh_scales[i][:, c]
 
-        def project(i, m):
-            pm = bank([BANK], F32)
-            codes, scales = xh_operand(i, m)
-            nc.tensor.matmul_mx(out=pm[:], lhsT=codes, lhsT_scale=scales, rhs=pre_codes[:].bitcast(FP8X4),
-                                rhs_scale=pre_scales[:], start=True, stop=True)
-            held["pm", i, m] = pm
+        def project(i):
+            for m in range(M1):
+                pm = bank([BANK], F32)
+                codes, scales = xh_operand(i, m)
+                nc.tensor.matmul_mx(out=pm[:], lhsT=codes, lhsT_scale=scales, rhs=pre_codes[:].bitcast(FP8X4),
+                                    rhs_scale=pre_scales[:], start=True, stop=True)
+                held["pm", i, m] = pm
 
-        def square(i, m):
-            nc.scalar.activation(out=squares[i, m][:].rearrange("p t c -> p (t c)"), in_=held["pm", i, m][:], func=ACT.Square)
+        def square(i):
+            for m in range(M1):
+                nc.scalar.activation(out=squares[i, m][:].rearrange("p r c -> p (r c)"), in_=held["pm", i, m][:],
+                                     func=ACT.Square)
 
         def sum_squares(i):
             total = bank([PACK, P], F32)
-            for t in range(PACK):
+            for r in range(PACK):
                 for m in range(M1):
-                    nc.tensor.matmul(total[:, t, :], lhsT=squares[i, m][:, t, :], rhs=ident_f32[:],
+                    nc.tensor.matmul(total[:, r, :], lhsT=squares[i, m][:, r, :], rhs=ident_f32[:],
                                      start=(m == 0), stop=(m == M1 - 1), is_transpose=True)
             held["sum", i] = total
 
         def root(i):
-            nc.scalar.activation(out=inv_words[i][:], in_=held["sum", i][:].rearrange("p t n -> p n t"), func=ACT.Sqrt)
+            nc.scalar.activation(out=inv_words[i][:], in_=held["sum", i][:].rearrange("p r n -> p n r"), func=ACT.Sqrt)
 
         def quantise_inv(i):
-            quantise(inv_codes[i][:], inv_scales[i][:], inv_words[i][:].rearrange("p n t -> p (n t)"))
+            quantise(inv_codes[i][:], inv_scales[i][:], inv_words[i][:].rearrange("p n r -> p (n r)"))
 
         def multiply(i, q):
-            acc = bank([BANK], F32)
-            h_codes, h_scales = xh_operand(i, M1)
-            sides = [(h_codes, h_scales), (inv_codes[i][:].bitcast(FP8X4), inv_scales[i][:])]
+            acc = bank([BANK], F32, product=True)
+            sides = [xh_operand(i, M1), (inv_codes[i][:].bitcast(FP8X4), inv_scales[i][:])]
             for g in range(2):
+                c = slice(g * BANK, (g + 1) * BANK)
                 nc.tensor.matmul_mx(out=acc[:], lhsT=sides[g][0], lhsT_scale=sides[g][1],
-                                    rhs=w_part(w_codes, g, q * BANK, (q + 1) * BANK, 1).bitcast(FP8X4),
-                                    rhs_scale=w_part(w_scales, g, q * BANK, (q + 1) * BANK, 1),
+                                    rhs=w_codes[q][:, c].bitcast(FP8X4), rhs_scale=w_scales[q][:, c],
                                     start=(g == 0), stop=(g == 1))
             held["acc", i, q] = acc
 
@@ -211,7 +225,17 @@ def tile_equivariantfeedforward_pa_kernel(tc, h, x1, pre1, w1_0_bytes, w1_0_scal
             nc.sync.dma_start(out=out[i0:i1, :, q * BANK : (q + 1) * BANK].rearrange("i n c -> n i c"),
                               in_=part.rearrange("p (i c) -> p i c", c=BANK))
 
-        def start_loads():
+        def widen_half(g, half, planes=range(PACK)):
+            return [(widen_on_vector, g, half, t) for t in planes]
+
+        w_work = [
+            widen_half(1, 0, range(1, PACK)),
+            widen_half(0, 1) + [(interleave_w_on_vector, 0)],
+            [(interleave_w_on_vector, 1), (quantise_w, 0)],
+            widen_half(1, 1, range(PACK - 1)) + [(quantise_w, 1)],
+        ]
+
+        with tc.manual_schedule():
             nc.scalar.dma_start(out=w_scale[:], in_=w1_0_scale.rearrange("(g p t) o -> p g (t o)", p=P, t=PACK))
             load_w(0, 0, 0, 2)
             load_x(0)
@@ -219,15 +243,15 @@ def tile_equivariantfeedforward_pa_kernel(tc, h, x1, pre1, w1_0_bytes, w1_0_scal
             nc.sync.dma_start(out=pre_raw[:], in_=pre1.rearrange("(p t) e -> p t e", t=PACK))
             load_w(0, 0, 3, 4)
             load_h(0)
-            load_x(1)
-            load_h(1)
-            load_x(2)
-            load_h(2)
-            load_w(1, 0, 0, 4)
-            load_x(3)
-            load_h(3)
-            load_w(0, 1, 0, 4)
-            load_w(1, 1, 0, 4)
+            for i in range(1, NT):
+                load_x(i)
+                if i == 1:
+                    load_w(1, 0, 0, 1)
+                load_h(i)
+                if i == 2:
+                    load_w(1, 0, 1, PACK)
+            load_w(0, 1, 0, PACK)
+            load_w(1, 1, 0, PACK)
             nc.sync.dma_start(out=bias[:], in_=b1_0.partition_broadcast(P))
             warm = sbuf("warm", [1], F32)
             nc.vector.memset(warm[:], 1.0)
@@ -235,82 +259,85 @@ def tile_equivariantfeedforward_pa_kernel(tc, h, x1, pre1, w1_0_bytes, w1_0_scal
             make_identity(nc, ident_f32[:])
             make_identity(nc, ident_bf16[:])
 
-        tensor_steps = [(turn_xh, 0, 0,), (turn_xh, 0, 1,), (lay_w, 0, 0, 0,), (turn_xh, 1, 0,), (turn_xh, 1, 1,), (project, 0, 0,), (project, 0, 1,), (project, 0, 2,), (lay_w, 0, 0, 1,), (turn_xh, 2, 0,), (turn_xh, 2, 1,), (project, 1, 0,), (project, 1, 1,), (project, 1, 2,), (sum_squares, 0,), (turn_xh, 3, 0,), (turn_xh, 3, 1,), (lay_w, 0, 1, 0,), (project, 2, 0,), (project, 2, 1,), (project, 2, 2,), (sum_squares, 1,), (lay_w, 0, 1, 1,), (project, 3, 0,), (project, 3, 1,), (project, 3, 2,), (sum_squares, 2,), (lay_w, 0, 2, 0,), (multiply, 0, 0,), (lay_w, 0, 2, 1,), (multiply, 1, 0,), (sum_squares, 3,), (multiply, 2, 0,), (multiply, 0, 1,), (lay_w, 0, 3, 0,), (multiply, 3, 0,), (lay_w, 0, 3, 1,), (multiply, 1, 1,), (multiply, 2, 1,), (multiply, 3, 1,), (multiply, 0, 2,), (multiply, 1, 2,), (multiply, 2, 2,), (multiply, 3, 2,), (multiply, 0, 3,), (multiply, 1, 3,), (multiply, 2, 3,), (multiply, 3, 3,)]
-        scalar_steps = [(widen_on_scalar, 0, 0, 0,), (widen_on_scalar, 0, 0, 2,), (widen_on_scalar, 0, 0, 3,), (fetch_xh, 0, 0,), (fetch_xh, 0, 1,), (fetch_w, 0, 0, 0,), (fetch_xh, 1, 0,), (fetch_xh, 1, 1,), (square, 0, 0,), (square, 0, 1,), (square, 0, 2,), (fetch_w, 0, 0, 1,), (fetch_xh, 2, 0,), (fetch_xh, 2, 1,), (square, 1, 0,), (square, 1, 1,), (square, 1, 2,), (fetch_xh, 3, 0,), (fetch_xh, 3, 1,), (root, 0,), (fetch_w, 0, 1, 0,), (square, 2, 0,), (square, 2, 1,), (square, 2, 2,), (root, 1,), (fetch_w, 0, 1, 1,), (square, 3, 0,), (square, 3, 1,), (square, 3, 2,), (root, 2,), (fetch_w, 0, 2, 0,), (fetch_w, 0, 2, 1,), (root, 3,), (finish, 0, 2, 0,), (fetch_w, 0, 3, 0,), (fetch_w, 0, 3, 1,), (finish, 2, 4, 0,), (finish, 0, 2, 1,), (finish, 2, 4, 1,), (finish, 0, 2, 2,), (finish, 2, 3, 2,), (finish, 3, 4, 2,), (finish, 0, 1, 3,), (finish, 1, 2, 3,), (finish, 2, 3, 3,), (finish, 3, 4, 3,)]
-        vector_steps = [(widen_on_vector, 0, 0, 1,), (split_x, 0,), (interleave_pre,), (split_x, 1,), (quantise_pre,), (quantise_xh, 0, 0, 1,), (quantise_xh, 0, 1, 2,), (split_x, 2,), (widen_on_vector, 1, 0, 0,), (quantise_xh, 1, 0, 2,), (split_x, 3,), (widen_on_vector, 1, 0, 1,), (widen_on_vector, 1, 0, 2,), (widen_on_vector, 1, 0, 3,), (quantise_xh, 2, 0, 2,), (interleave_w, 1, 0,), (widen_on_vector, 0, 1, 0,), (quantise_w, 0, 0, 1,), (quantise_xh, 3, 0, 2,), (quantise_w, 1, 0, 1,), (widen_on_vector, 0, 1, 1,), (quantise_inv, 0,), (widen_on_vector, 0, 1, 2,), (widen_on_vector, 0, 1, 3,), (interleave_w, 1, 1,), (quantise_inv, 1,), (widen_on_vector, 1, 1, 0,), (widen_on_vector, 1, 1, 1,), (quantise_w, 1, 1, 2,), (widen_on_vector, 1, 1, 2,), (quantise_inv, 2,), (quantise_w, 0, 1, 2,), (quantise_w, 0, 2, 3,), (quantise_inv, 3,), (widen_on_vector, 1, 1, 3,), (add_bias, 0, 0,), (add_bias, 1, 0,), (add_bias, 2, 0,), (add_bias, 0, 1,), (add_bias, 3, 0,), (quantise_w, 1, 2, 3,), (add_bias, 1, 1,), (add_bias, 2, 1,), (add_bias, 3, 1,), (add_bias, 0, 2,), (add_bias, 1, 2,), (quantise_w, 0, 3, 4,), (quantise_w, 1, 3, 4,), (add_bias, 2, 2,), (add_bias, 3, 2,), (add_bias, 0, 3,), (add_bias, 1, 3,), (add_bias, 2, 3,), (add_bias, 3, 3,)]
-        gpsimd_steps = [(interleave_w_on_gpsimd, 1, 2,), (interleave_w_on_gpsimd, 1, 3,)]
+            widen_on_vector(0, 0, 1)
+            for t in (0, 2, 3):
+                widen_on_scalar(0, 0, t)
+            split_x(0)
+            turn_xh(0)
+            fetch_xh(0)
+            widen_on_scalar(1, 0, 0)
+            lay_w(0)
+            fetch_w(0)
+            interleave_pre()
+            split_x(1)
+            turn_xh(1)
+            fetch_xh(1)
+            quantise_pre()
+            quantise_xh(0)
+            split_x(2)
 
-        gate = {(1, 3): (1, 2)}
+            for s in tiles:
+                project(s)
+                first, *rest = w_work[s]
+                first[0](*first[1:])
+                if s + 1 < NT:
+                    quantise_xh(s + 1)
+                if s + 3 < NT:
+                    split_x(s + 3)
+                square(s)
+                if s >= 1:
+                    sum_squares(s - 1)
+                    root(s - 1)
+                lay_w(s + 1)
+                fetch_w(s + 1)
+                if s + 2 < NT:
+                    turn_xh(s + 2)
+                    fetch_xh(s + 2)
+                for work in rest:
+                    work[0](*work[1:])
+                if s >= 1:
+                    quantise_inv(s - 1)
 
-        def inputs_of(work, *a):
-            if work is turn_xh:
-                return [(split_x, a[0])]
-            if work is fetch_xh:
-                return [(turn_xh, *a)]
-            if work is quantise_xh:
-                return [(fetch_xh, a[0], b) for b in range(a[1], a[2])]
-            if work is quantise_pre:
-                return [(interleave_pre,)]
-            if work is project:
-                return [(quantise_pre,), covering(quantise_xh, a[0], a[1] // 2)]
-            if work is square:
-                return [(project, *a)]
-            if work is sum_squares:
-                return [(square, a[0], m) for m in range(M1)]
-            if work is root:
-                return [(sum_squares, *a)]
-            if work is quantise_inv:
-                return [(root, *a)]
-            if work in (lay_w, interleave_w, interleave_w_on_gpsimd):
-                return [s for s in steps if s[0] in (widen_on_vector, widen_on_scalar) and s[1:3] == (a[0], a[1] // 2)]
-            if work is fetch_w:
-                return [(lay_w, *a)]
-            if work is quantise_w:
-                return [s for s in steps if s[0] in (fetch_w, interleave_w, interleave_w_on_gpsimd) and s[1] == a[0] and a[1] <= s[2] < a[2]]
-            if work is multiply:
-                return [(quantise_inv, a[0]), covering(quantise_xh, a[0], 1)] + [covering(quantise_w, g, a[1]) for g in range(2)]
-            if work is add_bias:
-                return [(multiply, *a)]
-            if work is finish:
-                return [(add_bias, i, a[2]) for i in range(a[0], a[1])]
-            return []
+            last = NT - 1
+            products = [(i, q) for q in range(NQ) for i in tiles]
+            products.remove((last, 0))
+            products.insert(products.index((last, 1)), (last, 0))
+            multiplied = []
 
-        def covering(work, which, part):
-            return [s for s in steps if s[0] is work and s[1] == which and s[2] <= part < s[3]][0]
+            def multiply_up_to(n, tiles_ready, quarters_ready):
+                for i, q in products[len(multiplied) : n]:
+                    if i >= tiles_ready or q >= quarters_ready:
+                        return
+                    multiply(i, q)
+                    multiplied.append((i, q))
 
-        emptied_by = {turn_xh: fetch_xh, project: square, sum_squares: root, lay_w: fetch_w, multiply: add_bias}
-        queues = [tensor_steps, scalar_steps, vector_steps, gpsimd_steps]
-        steps = tensor_steps + scalar_steps + vector_steps + gpsimd_steps
-        bank_of = []
-        for s in tensor_steps:
-            if s[0] is multiply:
-                allowed = range(PSUM_BANKS - STAGE2_BANKS, PSUM_BANKS)
-            elif any(r[0] is multiply for r in tensor_steps[: len(bank_of)]):
-                allowed = range(PSUM_BANKS - STAGE2_BANKS)
-            else:
-                allowed = range(PSUM_BANKS)
-            bank_of.append(min(allowed, key=lambda n: max([-1] + [k for k in range(len(bank_of)) if bank_of[k] == n])))
-        words_slot = {(g, q): f"{g}{q}" for g in range(2) for q in range(NQ)}
-        for late in gate:
-            words_slot[late] = words_slot[gate[late]]
-        written = set()
-        at = [0, 0, 0, 0]
-        with tc.manual_schedule():
-            start_loads()
-            while len(written) < len(steps):
-                before = len(written)
-                for e in range(4):
-                    if at[e] == len(queues[e]):
-                        continue
-                    s = queues[e][at[e]]
-                    needs = inputs_of(*s)
-                    if e == 0 and bank_of[at[0]] in bank_of[: at[0]]:
-                        old = [tensor_steps[n] for n in range(at[0]) if bank_of[n] == bank_of[at[0]]][-1]
-                        needs = needs + [(emptied_by[old[0]], *old[1:])]
-                    if s[1:] in gate and s[0] is interleave_w_on_gpsimd:
-                        needs = needs + [covering(quantise_w, *gate[s[1:]])]
-                    if all(n in written for n in needs):
-                        s[0](*s[1:])
-                        written.add(s)
-                        at[e] = at[e] + 1
-                assert len(written) > before
+            widen_on_vector(1, 1, PACK - 1)
+            interleave_w_on_gpsimd(NQ - 2)
+            multiply_up_to(2, last, NQ - 2)
+            sum_squares(last)
+            root(last)
+            multiply_up_to(PRODUCT_BANKS, last, NQ - 2)
+            lay_w(NT + 1)
+            for n, (i, q) in enumerate(products):
+                add_bias(i, q)
+                if n >= 2 * BIAS_RUN:
+                    finish(i, i + 1, q)
+                elif (i ^ 1, q) in products[:n]:
+                    finish(i - i % 2, i - i % 2 + 2, q)
+                if n == BIAS_RUN - 2:
+                    fetch_w(NT + 1, on_vector=True)
+                if n == 2 * BIAS_RUN - 2:
+                    fetch_w(NT + 3, on_vector=True)
+                if n == BIAS_RUN - 1:
+                    quantise_inv(last)
+                    quantise_w(NQ - 2)
+                    interleave_w_on_gpsimd(NQ - 1)
+                if n == 2 * BIAS_RUN - 1:
+                    quantise_w(NQ - 1)
+                runs_done = (n + 1) // BIAS_RUN
+                multiply_up_to(n + 1 + PRODUCT_BANKS, NT if runs_done else last, NQ - 2 + runs_done)
+                if n == 1:
+                    lay_w(NT + 2)
+                    fetch_w(NT + 2)
+                if n == BIAS_RUN - 1:
+                    lay_w(NT + 3)

@@ -54,7 +54,6 @@ def tile_equivariantfeedforward_pa_kernel(tc, h, x1, pre1, w1_0_bytes, w1_0_scal
             return psum.tile([P] + shape, dtype, name=f"bank{n}")
 
         tiles = range(NT)
-        halves = [(g, half) for g in range(2) for half in range(2)]
         w_rows = w1_0_bytes.rearrange("(g p t) n -> g p t n", p=P, t=PACK)
         w_bytes = {}
         x_raw = [sbuf(f"x_raw{i}", [D * M1], BF16) for i in tiles]
@@ -64,7 +63,8 @@ def tile_equivariantfeedforward_pa_kernel(tc, h, x1, pre1, w1_0_bytes, w1_0_scal
         bias = sbuf("bias", [FF], BF16)
         ident_f32 = sbuf("ident_f32", [P], F32)
         ident_bf16 = sbuf("ident_bf16", [P], BF16)
-        w_wide = {gh: sbuf(f"w_wide{gh[0]}{gh[1]}", [PACK, HALF], BF16) for gh in halves}
+        spans = [(0, 0, 2), (0, 2, 4), (1, 0, 2), (1, 2, 3), (1, 3, 4)]
+        w_wide = {(g, q0): sbuf(f"w_wide{g}{q0}", [PACK, (q1 - q0) * BANK], BF16) for g, q0, q1 in spans}
         w_words = {}
         w_codes = [sbuf(f"w_codes{q}", [2 * BANK], U32) for q in range(NQ)]
         w_scales = [sbuf(f"w_scales{q}", [2 * BANK], U8) for q in range(NQ)]
@@ -97,26 +97,30 @@ def tile_equivariantfeedforward_pa_kernel(tc, h, x1, pre1, w1_0_bytes, w1_0_scal
         def quantise(codes, scales, words):
             nc.vector.quantize_mx(out=codes.bitcast(FP8X4), scales=scales, in_=words)
 
-        def widen_on_vector(g, half, t):
-            nc.vector.tensor_scalar(out=w_wide[g, half][:, t, :], in0=w_bytes[g, half, t].bitcast(FP8),
-                                    scalar1=w_scale[:, g, t : t + 1], scalar2=None, op0=ALU.mult)
+        def widen_operands(g, q0, q1, t):
+            raw = w_bytes[g, q0 // 2, t][:, q0 % 2 * BANK : (q1 - q0 // 2 * 2) * BANK]
+            return w_wide[g, q0][:, t, :], raw.bitcast(FP8), w_scale[:, g, t : t + 1]
 
-        def widen_on_scalar(g, half, t):
-            nc.scalar.activation(out=w_wide[g, half][:, t, :], in_=w_bytes[g, half, t].bitcast(FP8),
-                                 func=ACT.Copy, scale=w_scale[:, g, t : t + 1])
+        def widen_on_vector(g, q0, q1, t):
+            dst, src, scale = widen_operands(g, q0, q1, t)
+            nc.vector.tensor_scalar(out=dst, in0=src, scalar1=scale, scalar2=None, op0=ALU.mult)
+
+        def widen_on_scalar(g, q0, q1, t):
+            dst, src, scale = widen_operands(g, q0, q1, t)
+            nc.scalar.activation(out=dst, in_=src, func=ACT.Copy, scale=scale)
 
         def w_columns(g, c0, c1):
-            half = c0 // HALF
-            return w_wide[g, half][:, :, c0 - half * HALF : c1 - half * HALF].rearrange("p t n -> p n t")
+            q0 = max(a for k, a, b in spans if k == g and a * BANK <= c0)
+            return w_wide[g, q0][:, :, c0 - q0 * BANK : c1 - q0 * BANK].rearrange("p t n -> p n t")
 
         def words_of(g, q):
             if (g, q) not in w_words:
                 w_words[g, q] = sbuf(f"w_words{g}{min(q, NQ - 1 - g)}", [BANK * PACK], BF16)
             return w_words[g, q][:]
 
-        def interleave_w_on_vector(q):
-            nc.vector.tensor_copy(out=words_of(1, q).rearrange("p (n t) -> p n t", t=PACK),
-                                  in_=w_columns(1, q * BANK, (q + 1) * BANK))
+        def interleave_w_on_vector(q, g=1):
+            nc.vector.tensor_copy(out=words_of(g, q).rearrange("p (n t) -> p n t", t=PACK),
+                                  in_=w_columns(g, q * BANK, (q + 1) * BANK))
 
         def interleave_w_on_gpsimd(q):
             nc.gpsimd.tensor_scalar(out=words_of(1, q).rearrange("p (n t) -> p n t", t=PACK),
@@ -225,14 +229,14 @@ def tile_equivariantfeedforward_pa_kernel(tc, h, x1, pre1, w1_0_bytes, w1_0_scal
             nc.sync.dma_start(out=out[i0:i1, :, q * BANK : (q + 1) * BANK].rearrange("i n c -> n i c"),
                               in_=part.rearrange("p (i c) -> p i c", c=BANK))
 
-        def widen_half(g, half, planes=range(PACK)):
-            return [(widen_on_vector, g, half, t) for t in planes]
+        def widen_span(g, q0, q1, planes=range(PACK)):
+            return [(widen_on_vector, g, q0, q1, t) for t in planes]
 
         w_work = [
-            widen_half(1, 0, range(1, PACK)),
-            widen_half(0, 1) + [(interleave_w_on_vector, 0)],
+            widen_span(1, 0, 2, range(1, PACK)),
+            widen_span(0, 2, 4) + [(interleave_w_on_vector, 0)],
             [(interleave_w_on_vector, 1), (quantise_w, 0)],
-            widen_half(1, 1, range(PACK - 1)) + [(quantise_w, 1)],
+            widen_span(1, 2, 3, range(PACK - 1)) + [(quantise_w, 1), (interleave_w_on_vector, 2, 0)],
         ]
 
         with tc.manual_schedule():
@@ -259,13 +263,13 @@ def tile_equivariantfeedforward_pa_kernel(tc, h, x1, pre1, w1_0_bytes, w1_0_scal
             make_identity(nc, ident_f32[:])
             make_identity(nc, ident_bf16[:])
 
-            widen_on_vector(0, 0, 1)
+            widen_on_vector(0, 0, 2, 1)
             for t in (0, 2, 3):
-                widen_on_scalar(0, 0, t)
+                widen_on_scalar(0, 0, 2, t)
             split_x(0)
             turn_xh(0)
             fetch_xh(0)
-            widen_on_scalar(1, 0, 0)
+            widen_on_scalar(1, 0, 2, 0)
             lay_w(0)
             fetch_w(0)
             interleave_pre()
@@ -288,11 +292,12 @@ def tile_equivariantfeedforward_pa_kernel(tc, h, x1, pre1, w1_0_bytes, w1_0_scal
                 if s >= 1:
                     sum_squares(s - 1)
                     root(s - 1)
-                lay_w(s + 1)
-                fetch_w(s + 1)
                 if s + 2 < NT:
                     turn_xh(s + 2)
                     fetch_xh(s + 2)
+                if s + 1 < NT:
+                    lay_w(s + 1)
+                    fetch_w(s + 1)
                 for work in rest:
                     work[0](*work[1:])
                 if s >= 1:
@@ -311,21 +316,20 @@ def tile_equivariantfeedforward_pa_kernel(tc, h, x1, pre1, w1_0_bytes, w1_0_scal
                     multiply(i, q)
                     multiplied.append((i, q))
 
-            widen_on_vector(1, 1, PACK - 1)
+            widen_on_vector(1, 2, 3, PACK - 1)
             interleave_w_on_gpsimd(NQ - 2)
             multiply_up_to(2, last, NQ - 2)
+            for t in range(PACK):
+                widen_on_scalar(1, 3, 4, t)
             sum_squares(last)
             root(last)
             multiply_up_to(PRODUCT_BANKS, last, NQ - 2)
-            lay_w(NT + 1)
             for n, (i, q) in enumerate(products):
                 add_bias(i, q)
                 if n >= 2 * BIAS_RUN:
                     finish(i, i + 1, q)
                 elif (i ^ 1, q) in products[:n]:
                     finish(i - i % 2, i - i % 2 + 2, q)
-                if n == BIAS_RUN - 2:
-                    fetch_w(NT + 1, on_vector=True)
                 if n == 2 * BIAS_RUN - 2:
                     fetch_w(NT + 3, on_vector=True)
                 if n == BIAS_RUN - 1:

@@ -25,6 +25,7 @@ UNITS = M1 + 1
 PSUM_BANKS = 8
 PRODUCT_BANKS = 4
 BIAS_RUN = 5
+RUN = 4
 
 FLOPS = 2 * NT * P * M1 * D * D + 2 * NT * P * 2 * D * FF
 
@@ -119,8 +120,8 @@ def tile_equivariantfeedforward_pa_kernel(tc, h, x1, pre1, w1_0_bytes, w1_0_scal
             return w_words[g, q][:]
 
         def interleave_w_on_vector(q, g=1):
-            nc.vector.tensor_copy(out=words_of(g, q).rearrange("p (n t) -> p n t", t=PACK),
-                                  in_=w_columns(g, q * BANK, (q + 1) * BANK))
+            nc.vector.tensor_copy(out=words_of(g, q).rearrange("p (c i t) -> p c t i", i=RUN, t=PACK),
+                                  in_=w_columns(g, q * BANK, (q + 1) * BANK).rearrange("p (c i) t -> p c t i", i=RUN))
 
         def interleave_w_on_gpsimd(q):
             nc.gpsimd.tensor_scalar(out=words_of(1, q).rearrange("p (n t) -> p n t", t=PACK),

@@ -157,17 +157,22 @@ def tile_equivariantfeedforward_pa_kernel(tc, h, x1, pre1, w1_0_bytes, w1_0_scal
             quantise(pre_codes[:], pre_scales[:], pre_words[:].rearrange("p e t -> p (e t)"))
 
         def split_x(i):
-            nc.vector.tensor_copy(out=x_split[i][:].rearrange("p m (a d) -> p a m d", a=2),
-                                  in_=x_raw[i][:].rearrange("p (a d m) -> p a m d", a=2, m=M1))
+            dst = x_split[i][:].rearrange("p m (u c e) -> p c m u e", u=2, e=2)
+            src = x_raw[i][:].rearrange("p (c u e m) -> p c m u e", u=2, e=2, m=M1)
+            for m0, m1 in ((0, 2), (2, M1)):
+                nc.vector.tensor_copy(out=dst[:, :, m0:m1], in_=src[:, :, m0:m1])
 
         def turn_xh(i):
             for b in range(2):
                 turned = bank([2, 2, P], F32)
                 for j in range(2):
                     m = 2 * b + j
-                    words = (x_split[i][:, m, :] if m < M1 else h_raw[i][:]).bitcast(F32)
                     for u in range(2):
-                        nc.tensor.transpose(turned[:, j, u, :], words[:, u : D // 2 : 2], ident_f32[:])
+                        if m < M1:
+                            words = x_split[i][:, m, :].bitcast(F32)[:, u * P : (u + 1) * P]
+                        else:
+                            words = h_raw[i][:].bitcast(F32)[:, u : D // 2 : 2]
+                        nc.tensor.transpose(turned[:, j, u, :], words, ident_f32[:])
                 held["xh", i, b] = turned
 
         def fetch_xh(i):

@@ -39,20 +39,19 @@ def tile_equivariantfeedforward_pa_kernel(tc, h, x1, pre1, w1_0_bytes, w1_0_scal
         def sbuf(name, shape, dtype):
             return keep.tile([P] + shape, dtype, name=name, align_bytes=64)
 
-        taken = {"stage 1": 0, "products": 0, "beside products": 0}
+        free_banks = list(range(PSUM_BANKS))
+        held = {}
 
-        def bank(shape, dtype, product=False):
-            others = PSUM_BANKS - PRODUCT_BANKS
-            if product:
-                n = others + taken["products"] % PRODUCT_BANKS
-                taken["products"] += 1
-            elif taken["products"]:
-                n = taken["beside products"] % others
-                taken["beside products"] += 1
-            else:
-                n = taken["stage 1"] % PSUM_BANKS
-                taken["stage 1"] += 1
-            return psum.tile([P] + shape, dtype, name=f"bank{n}")
+        def take_bank(key, shape, dtype):
+            n = free_banks[0]
+            free_banks.remove(n)
+            held[key] = (psum.tile([P] + shape, dtype, name=f"bank{n}"), n)
+            return held[key][0]
+
+        def empty_bank(key):
+            tile, n = held[key]
+            free_banks.append(n)
+            return tile
 
         tiles = range(NT)
         w_rows = w1_0_bytes.rearrange("(g p t) n -> g p t n", p=P, t=PACK)
@@ -80,8 +79,7 @@ def tile_equivariantfeedforward_pa_kernel(tc, h, x1, pre1, w1_0_bytes, w1_0_scal
         inv_words = [sbuf(f"inv_words{i}", [P, PACK], BF16) for i in tiles]
         inv_codes = [sbuf(f"inv_codes{i}", [P], U32) for i in tiles]
         inv_scales = [sbuf(f"inv_scales{i}", [P], U8) for i in tiles]
-        rows = [sbuf(f"rows{q}", [NT * BANK], F32) for q in range(NQ)]
-        held = {}
+        rows = [sbuf(f"rows{i}", [FF], F32) for i in tiles]
 
         def load_w(g, half, t0, t1):
             raw = sbuf(f"w_bytes{g}{half}{t0}", [t1 - t0, HALF], U8)
@@ -129,25 +127,23 @@ def tile_equivariantfeedforward_pa_kernel(tc, h, x1, pre1, w1_0_bytes, w1_0_scal
                                     scalar1=1.0, scalar2=0.0, op0=ALU.mult, op1=ALU.add)
 
         def lay_w(n):
-            laid = bank([2, P * PACK], BF16)
+            laid = take_bank(("w", n), [2, P * PACK], BF16)
             for j in range(2):
                 c0 = (2 * n + j) * P
                 nc.tensor.matmul(laid[:, j, :], lhsT=ident_bf16[:], rhs=w_columns(0, c0, c0 + P), start=True, stop=True)
-            held["w", n] = laid
 
         def fetch_w(n, on_vector=False):
             width = 2 * P * PACK
             dst = words_of(0, n // 2)[:, n % 2 * width : (n % 2 + 1) * width]
-            src = held["w", n][:].rearrange("p j c -> p (j c)")
+            src = empty_bank(("w", n))[:].rearrange("p j c -> p (j c)")
             if on_vector:
                 nc.vector.tensor_copy(out=dst, in_=src)
             else:
                 nc.scalar.copy(out=dst, in_=src)
 
-        def quantise_w(q):
-            for g in range(2):
-                c = slice(g * BANK, (g + 1) * BANK)
-                quantise(w_codes[q][:, c], w_scales[q][:, c], w_words[g, q][:])
+        def quantise_w(g, q):
+            c = slice(g * BANK, (g + 1) * BANK)
+            quantise(w_codes[q][:, c], w_scales[q][:, c], w_words[g, q][:])
 
         def interleave_pre():
             nc.vector.tensor_copy(out=pre_words[:].rearrange("p (r c) t -> p r c t", r=PACK),
@@ -159,12 +155,15 @@ def tile_equivariantfeedforward_pa_kernel(tc, h, x1, pre1, w1_0_bytes, w1_0_scal
         def split_x(i):
             dst = x_split[i][:].rearrange("p m (u c e) -> p c m u e", u=2, e=2)
             src = x_raw[i][:].rearrange("p (c u e m) -> p c m u e", u=2, e=2, m=M1)
-            for m0, m1 in ((0, 2), (2, M1)):
-                nc.vector.tensor_copy(out=dst[:, :, m0:m1], in_=src[:, :, m0:m1])
+            nc.vector.tensor_copy(out=dst[:, :, :2], in_=src[:, :, :2])
+            if i == 0:
+                nc.scalar.copy(out=dst[:, :, 2:], in_=src[:, :, 2:])
+            else:
+                nc.vector.tensor_copy(out=dst[:, :, 2:], in_=src[:, :, 2:])
 
         def turn_xh(i):
             for b in range(2):
-                turned = bank([2, 2, P], F32)
+                turned = take_bank(("xh", i, b), [2, 2, P], F32)
                 for j in range(2):
                     m = 2 * b + j
                     for u in range(2):
@@ -173,13 +172,12 @@ def tile_equivariantfeedforward_pa_kernel(tc, h, x1, pre1, w1_0_bytes, w1_0_scal
                         else:
                             words = h_raw[i][:].bitcast(F32)[:, u : D // 2 : 2]
                         nc.tensor.transpose(turned[:, j, u, :], words, ident_f32[:])
-                held["xh", i, b] = turned
 
         def fetch_xh(i):
             for b in range(2):
                 dst = xh_words[i][:, b * 2 * P * PACK : (b + 1) * 2 * P * PACK].bitcast(F32)
                 nc.scalar.copy(out=dst.rearrange("p (j n u) -> p j n u", j=2, u=2),
-                               in_=held["xh", i, b][:].rearrange("p j u n -> p j n u"))
+                               in_=empty_bank(("xh", i, b))[:].rearrange("p j u n -> p j n u"))
 
         def quantise_xh(i):
             quantise(xh_codes[i][:], xh_scales[i][:], xh_words[i][:])
@@ -190,76 +188,59 @@ def tile_equivariantfeedforward_pa_kernel(tc, h, x1, pre1, w1_0_bytes, w1_0_scal
 
         def project(i):
             for m in range(M1):
-                pm = bank([BANK], F32)
+                pm = take_bank(("pm", i, m), [BANK], F32)
                 codes, scales = xh_operand(i, m)
                 nc.tensor.matmul_mx(out=pm[:], lhsT=codes, lhsT_scale=scales, rhs=pre_codes[:].bitcast(FP8X4),
                                     rhs_scale=pre_scales[:], start=True, stop=True)
-                held["pm", i, m] = pm
 
-        def square(i):
-            for m in range(M1):
-                nc.scalar.activation(out=squares[i, m][:].rearrange("p r c -> p (r c)"), in_=held["pm", i, m][:],
+        def square(i, components=range(M1)):
+            for m in components:
+                nc.scalar.activation(out=squares[i, m][:].rearrange("p r c -> p (r c)"), in_=empty_bank(("pm", i, m))[:],
                                      func=ACT.Square)
 
         def sum_squares(i):
-            total = bank([PACK, P], F32)
-            for r in range(PACK):
-                for m in range(M1):
+            total = take_bank(("sum", i), [PACK, P], F32)
+            for m in range(M1):
+                for r in range(PACK):
                     nc.tensor.matmul(total[:, r, :], lhsT=squares[i, m][:, r, :], rhs=ident_f32[:],
-                                     start=(m == 0), stop=(m == M1 - 1), is_transpose=True)
-            held["sum", i] = total
+                                     start=(m, r) == (0, 0), stop=(m, r) == (M1 - 1, PACK - 1), is_transpose=True)
 
         def root(i):
-            nc.scalar.activation(out=inv_words[i][:], in_=held["sum", i][:].rearrange("p r n -> p n r"), func=ACT.Sqrt)
+            nc.scalar.activation(out=inv_words[i][:], in_=empty_bank(("sum", i))[:].rearrange("p r n -> p n r"), func=ACT.Sqrt)
 
         def quantise_inv(i):
             quantise(inv_codes[i][:], inv_scales[i][:], inv_words[i][:].rearrange("p n r -> p (n r)"))
 
         def multiply(i, q):
-            acc = bank([BANK], F32, product=True)
+            acc = take_bank(("acc", i, q), [BANK], F32)
             sides = [xh_operand(i, M1), (inv_codes[i][:].bitcast(FP8X4), inv_scales[i][:])]
             for g in range(2):
                 c = slice(g * BANK, (g + 1) * BANK)
                 nc.tensor.matmul_mx(out=acc[:], lhsT=sides[g][0], lhsT_scale=sides[g][1],
                                     rhs=w_codes[q][:, c].bitcast(FP8X4), rhs_scale=w_scales[q][:, c],
                                     start=(g == 0), stop=(g == 1))
-            held["acc", i, q] = acc
 
         def add_bias(i, q):
-            nc.vector.tensor_tensor(out=rows[q][:, i * BANK : (i + 1) * BANK], in0=held["acc", i, q][:],
+            nc.vector.tensor_tensor(out=rows[i][:, q * BANK : (q + 1) * BANK], in0=empty_bank(("acc", i, q))[:],
                                     in1=bias[:, q * BANK : (q + 1) * BANK], op=ALU.add)
 
-        def finish(i0, i1, q):
-            part = rows[q][:, i0 * BANK : i1 * BANK]
+        def finish(i, c0, c1):
+            part = rows[i][:, c0:c1]
             nc.scalar.activation(out=part, in_=part, func=ACT.Silu)
-            nc.sync.dma_start(out=out[i0:i1, :, q * BANK : (q + 1) * BANK].rearrange("i n c -> n i c"),
-                              in_=part.rearrange("p (i c) -> p i c", c=BANK))
-
-        def widen_span(g, q0, q1, planes=range(PACK)):
-            return [(widen_on_vector, g, q0, q1, t) for t in planes]
-
-        w_work = [
-            widen_span(1, 0, 2, range(1, PACK)),
-            widen_span(0, 2, 4) + [(interleave_w_on_vector, 0)],
-            [(interleave_w_on_vector, 1), (quantise_w, 0)],
-            widen_span(1, 2, 3, range(PACK - 1)) + [(quantise_w, 1), (interleave_w_on_vector, 2, 0)],
-        ]
+            nc.sync.dma_start(out=out[i, :, c0:c1], in_=part)
 
         with tc.manual_schedule():
             nc.scalar.dma_start(out=w_scale[:], in_=w1_0_scale.rearrange("(g p t) o -> p g (t o)", p=P, t=PACK))
-            load_w(0, 0, 0, 2)
             load_x(0)
-            load_w(0, 0, 2, 3)
-            nc.sync.dma_start(out=pre_raw[:], in_=pre1.rearrange("(p t) e -> p t e", t=PACK))
-            load_w(0, 0, 3, 4)
+            load_w(0, 0, 0, 2)
+            load_w(0, 0, 2, 4)
             load_h(0)
+            nc.sync.dma_start(out=pre_raw[:], in_=pre1.rearrange("(p t) e -> p t e", t=PACK))
+            load_w(1, 0, 0, 3)
             for i in range(1, NT):
                 load_x(i)
-                if i == 1:
-                    load_w(1, 0, 0, 1)
                 load_h(i)
-                if i == 2:
-                    load_w(1, 0, 1, PACK)
+            load_w(1, 0, 3, 4)
             load_w(0, 1, 0, PACK)
             load_w(1, 1, 0, PACK)
             nc.sync.dma_start(out=bias[:], in_=b1_0.partition_broadcast(P))
@@ -269,85 +250,110 @@ def tile_equivariantfeedforward_pa_kernel(tc, h, x1, pre1, w1_0_bytes, w1_0_scal
             make_identity(nc, ident_f32[:])
             make_identity(nc, ident_bf16[:])
 
-            widen_on_vector(0, 0, 2, 1)
-            for t in (0, 2, 3):
-                widen_on_scalar(0, 0, 2, t)
             split_x(0)
+            widen_on_scalar(0, 0, 2, 0)
+            for t in range(1, PACK):
+                widen_on_vector(0, 0, 2, t)
             turn_xh(0)
             fetch_xh(0)
-            widen_on_scalar(1, 0, 2, 0)
             lay_w(0)
-            fetch_w(0)
+            lay_w(1)
             interleave_pre()
+            quantise_xh(0)
             split_x(1)
+            quantise_pre()
+            widen_on_scalar(1, 0, 2, 0)
+            widen_on_scalar(1, 0, 2, 1)
+            fetch_w(0)
+            widen_on_scalar(1, 0, 2, 2)
+            fetch_w(1)
             turn_xh(1)
             fetch_xh(1)
-            quantise_pre()
-            quantise_xh(0)
             split_x(2)
-
-            for s in tiles:
-                project(s)
-                first, *rest = w_work[s]
-                first[0](*first[1:])
-                if s + 1 < NT:
-                    quantise_xh(s + 1)
-                if s + 3 < NT:
-                    split_x(s + 3)
-                square(s)
-                if s >= 1:
-                    sum_squares(s - 1)
-                    root(s - 1)
-                if s + 2 < NT:
-                    turn_xh(s + 2)
-                    fetch_xh(s + 2)
-                if s + 1 < NT:
-                    lay_w(s + 1)
-                    fetch_w(s + 1)
-                for work in rest:
-                    work[0](*work[1:])
-                if s >= 1:
-                    quantise_inv(s - 1)
+            project(0)
+            square(0)
+            split_x(3)
+            widen_on_vector(1, 0, 2, 3)
+            interleave_w_on_vector(0)
+            quantise_xh(1)
+            turn_xh(2)
+            fetch_xh(2)
+            lay_w(2)
+            fetch_w(2)
+            turn_xh(3)
+            fetch_xh(3)
+            quantise_w(0, 0)
+            for t in range(3):
+                widen_on_vector(0, 2, 4, t)
+            quantise_xh(2)
+            widen_on_vector(0, 2, 4, 3)
+            quantise_w(1, 0)
+            quantise_xh(3)
+            project(1)
+            square(1)
+            sum_squares(0)
+            root(0)
+            lay_w(3)
+            fetch_w(3)
+            interleave_w_on_vector(1)
+            quantise_inv(0)
+            quantise_w(0, 1)
+            quantise_w(1, 1)
+            interleave_w_on_vector(2, 0)
+            project(2)
+            square(2)
+            sum_squares(1)
+            root(1)
+            project(3)
+            sum_squares(2)
+            quantise_inv(1)
+            for t in range(PACK - 1):
+                widen_on_vector(1, 2, 3, t)
 
             last = NT - 1
-            products = [(i, q) for q in range(NQ) for i in tiles]
-            products.remove((last, 0))
-            products.insert(products.index((last, 1)), (last, 0))
+            products = [(i, q) for i in tiles for q in range(2)] + [(i, q) for q in range(2, NQ) for i in tiles]
             multiplied = []
 
-            def multiply_up_to(n, tiles_ready, quarters_ready):
+            def multiply_up_to(n):
                 for i, q in products[len(multiplied) : n]:
-                    if i >= tiles_ready or q >= quarters_ready:
-                        return
                     multiply(i, q)
                     multiplied.append((i, q))
 
+            def add_biases(n0, n1, ready):
+                for n in range(n0, n1):
+                    i, q = products[n]
+                    add_bias(i, q)
+                    if q >= 2 or i == 0:
+                        finish(i, q * BANK, (q + 1) * BANK)
+                    elif q == 1:
+                        finish(i, 0, HALF)
+                    multiply_up_to(min(ready, n + 1 + PRODUCT_BANKS))
+
+            square(last, range(1))
+            root(last - 1)
+            multiply_up_to(2)
+            square(last, range(1, M1))
+            multiply_up_to(4)
+            sum_squares(last)
+            for t in range(PACK - 1):
+                widen_on_scalar(1, 3, 4, t)
+            root(last)
+            widen_on_vector(1, 3, 4, PACK - 1)
+            quantise_inv(last - 1)
             widen_on_vector(1, 2, 3, PACK - 1)
             interleave_w_on_gpsimd(NQ - 2)
-            multiply_up_to(2, last, NQ - 2)
-            for t in range(PACK):
-                widen_on_scalar(1, 3, 4, t)
-            sum_squares(last)
-            root(last)
-            multiply_up_to(PRODUCT_BANKS, last, NQ - 2)
-            for n, (i, q) in enumerate(products):
-                add_bias(i, q)
-                if n >= 2 * BIAS_RUN:
-                    finish(i, i + 1, q)
-                elif (i ^ 1, q) in products[:n]:
-                    finish(i - i % 2, i - i % 2 + 2, q)
-                if n == 2 * BIAS_RUN - 2:
-                    fetch_w(NT + 3, on_vector=True)
-                if n == BIAS_RUN - 1:
-                    quantise_inv(last)
-                    quantise_w(NQ - 2)
-                    interleave_w_on_gpsimd(NQ - 1)
-                if n == 2 * BIAS_RUN - 1:
-                    quantise_w(NQ - 1)
-                runs_done = (n + 1) // BIAS_RUN
-                multiply_up_to(n + 1 + PRODUCT_BANKS, NT if runs_done else last, NQ - 2 + runs_done)
-                if n == 1:
-                    lay_w(NT + 2)
-                    fetch_w(NT + 2)
-                if n == BIAS_RUN - 1:
-                    lay_w(NT + 3)
+            add_biases(0, 2, 6)
+            lay_w(6)
+            lay_w(7)
+            add_biases(2, 6, 6)
+            quantise_inv(last)
+            quantise_w(0, NQ - 2)
+            quantise_w(1, NQ - 2)
+            interleave_w_on_gpsimd(NQ - 1)
+            multiply_up_to(10)
+            fetch_w(6, on_vector=True)
+            fetch_w(7, on_vector=True)
+            add_biases(6, 10, 12)
+            quantise_w(0, NQ - 1)
+            quantise_w(1, NQ - 1)
+            add_biases(10, 16, 16)

@@ -42,8 +42,8 @@ def tile_equivariantfeedforward_pa_kernel(tc, h, x1, pre1, w1_0_bytes, w1_0_scal
         free_banks = list(range(PSUM_BANKS))
         held = {}
 
-        def take_bank(key, shape, dtype):
-            n = free_banks[0]
+        def take_bank(key, shape, dtype, newest=False):
+            n = free_banks[-1 if newest else 0]
             free_banks.remove(n)
             held[key] = (psum.tile([P] + shape, dtype, name=f"bank{n}"), n)
             return held[key][0]
@@ -113,9 +113,10 @@ def tile_equivariantfeedforward_pa_kernel(tc, h, x1, pre1, w1_0_bytes, w1_0_scal
             return w_wide[g, q0][:, :, c0 - q0 * BANK : c1 - q0 * BANK].rearrange("p t n -> p n t")
 
         def words_of(g, q):
-            if (g, q) not in w_words:
-                w_words[g, q] = sbuf(f"w_words{g}{min(q, NQ - 1 - g)}", [BANK * PACK], BF16)
-            return w_words[g, q][:]
+            key = (g, q) if q == NQ - 1 else q
+            if key not in w_words:
+                w_words[key] = sbuf(f"w_words{q - g if q == NQ - 1 else q}", [2 * BANK * PACK], BF16)
+            return w_words[key][:, g * BANK * PACK : (g + 1) * BANK * PACK]
 
         def interleave_w_on_vector(q, g=1):
             nc.vector.tensor_copy(out=words_of(g, q).rearrange("p (c i t) -> p c t i", i=RUN, t=PACK),
@@ -141,13 +142,13 @@ def tile_equivariantfeedforward_pa_kernel(tc, h, x1, pre1, w1_0_bytes, w1_0_scal
             else:
                 nc.scalar.copy(out=dst, in_=src)
 
-        def quantise_w(g, q):
-            c = slice(g * BANK, (g + 1) * BANK)
-            quantise(w_codes[q][:, c], w_scales[q][:, c], w_words[g, q][:])
+        def quantise_w(q, g0=0, g1=2):
+            c = slice(g0 * BANK, g1 * BANK)
+            quantise(w_codes[q][:, c], w_scales[q][:, c], w_words[(g0, q) if q == NQ - 1 else q][:, g0 * BANK * PACK : g1 * BANK * PACK])
 
         def interleave_pre():
-            nc.vector.tensor_copy(out=pre_words[:].rearrange("p (r c) t -> p r c t", r=PACK),
-                                  in_=pre_raw[:].rearrange("p t (c r) -> p r c t", r=PACK))
+            nc.vector.tensor_copy(out=pre_words[:].rearrange("p (r c) t -> p c t r", r=PACK),
+                                  in_=pre_raw[:].rearrange("p t (c r) -> p c t r", r=PACK))
 
         def quantise_pre():
             quantise(pre_codes[:], pre_scales[:], pre_words[:].rearrange("p e t -> p (e t)"))
@@ -176,8 +177,8 @@ def tile_equivariantfeedforward_pa_kernel(tc, h, x1, pre1, w1_0_bytes, w1_0_scal
         def fetch_xh(i):
             for b in range(2):
                 dst = xh_words[i][:, b * 2 * P * PACK : (b + 1) * 2 * P * PACK].bitcast(F32)
-                nc.scalar.copy(out=dst.rearrange("p (j n u) -> p j n u", j=2, u=2),
-                               in_=empty_bank(("xh", i, b))[:].rearrange("p j u n -> p j n u"))
+                nc.scalar.copy(out=dst.rearrange("p (j n a u) -> p j n u a", j=2, a=2, u=2),
+                               in_=empty_bank(("xh", i, b))[:].rearrange("p j u (n a) -> p j n u a", a=2))
 
         def quantise_xh(i):
             quantise(xh_codes[i][:], xh_scales[i][:], xh_words[i][:])
@@ -206,15 +207,18 @@ def tile_equivariantfeedforward_pa_kernel(tc, h, x1, pre1, w1_0_bytes, w1_0_scal
                                      start=(m, r) == (0, 0), stop=(m, r) == (M1 - 1, PACK - 1), is_transpose=True)
 
         def root(i):
-            nc.scalar.activation(out=inv_words[i][:], in_=empty_bank(("sum", i))[:].rearrange("p r n -> p n r"), func=ACT.Sqrt)
+            nc.scalar.activation(out=inv_words[i][:].rearrange("p (n a) r -> p n r a", a=2),
+                                 in_=empty_bank(("sum", i))[:].rearrange("p r (n a) -> p n r a", a=2), func=ACT.Sqrt)
 
         def quantise_inv(i):
             quantise(inv_codes[i][:], inv_scales[i][:], inv_words[i][:].rearrange("p n r -> p (n r)"))
 
-        def multiply(i, q):
-            acc = take_bank(("acc", i, q), [BANK], F32)
+        def multiply(i, q, paced=False, passes=(0, 1)):
+            if ("acc", i, q) not in held:
+                take_bank(("acc", i, q), [BANK], F32, paced)
+            acc = held["acc", i, q][0]
             sides = [xh_operand(i, M1), (inv_codes[i][:].bitcast(FP8X4), inv_scales[i][:])]
-            for g in range(2):
+            for g in passes:
                 c = slice(g * BANK, (g + 1) * BANK)
                 nc.tensor.matmul_mx(out=acc[:], lhsT=sides[g][0], lhsT_scale=sides[g][1],
                                     rhs=w_codes[q][:, c].bitcast(FP8X4), rhs_scale=w_scales[q][:, c],
@@ -237,10 +241,13 @@ def tile_equivariantfeedforward_pa_kernel(tc, h, x1, pre1, w1_0_bytes, w1_0_scal
             load_h(0)
             nc.sync.dma_start(out=pre_raw[:], in_=pre1.rearrange("(p t) e -> p t e", t=PACK))
             load_w(1, 0, 0, 3)
-            for i in range(1, NT):
-                load_x(i)
-                load_h(i)
+            load_x(1)
+            load_h(1)
+            load_x(2)
+            load_h(2)
             load_w(1, 0, 3, 4)
+            load_x(3)
+            load_h(3)
             load_w(0, 1, 0, PACK)
             load_w(1, 1, 0, PACK)
             nc.sync.dma_start(out=bias[:], in_=b1_0.partition_broadcast(P))
@@ -272,8 +279,8 @@ def tile_equivariantfeedforward_pa_kernel(tc, h, x1, pre1, w1_0_bytes, w1_0_scal
             split_x(2)
             project(0)
             square(0)
-            split_x(3)
             widen_on_vector(1, 0, 2, 3)
+            split_x(3)
             interleave_w_on_vector(0)
             quantise_xh(1)
             turn_xh(2)
@@ -282,12 +289,11 @@ def tile_equivariantfeedforward_pa_kernel(tc, h, x1, pre1, w1_0_bytes, w1_0_scal
             fetch_w(2)
             turn_xh(3)
             fetch_xh(3)
-            quantise_w(0, 0)
             for t in range(3):
                 widen_on_vector(0, 2, 4, t)
             quantise_xh(2)
             widen_on_vector(0, 2, 4, 3)
-            quantise_w(1, 0)
+            quantise_w(0)
             quantise_xh(3)
             project(1)
             square(1)
@@ -297,8 +303,8 @@ def tile_equivariantfeedforward_pa_kernel(tc, h, x1, pre1, w1_0_bytes, w1_0_scal
             fetch_w(3)
             interleave_w_on_vector(1)
             quantise_inv(0)
-            quantise_w(0, 1)
-            quantise_w(1, 1)
+            widen_on_vector(1, 2, 3, 0)
+            quantise_w(1)
             interleave_w_on_vector(2, 0)
             project(2)
             square(2)
@@ -307,19 +313,19 @@ def tile_equivariantfeedforward_pa_kernel(tc, h, x1, pre1, w1_0_bytes, w1_0_scal
             project(3)
             sum_squares(2)
             quantise_inv(1)
-            for t in range(PACK - 1):
+            for t in range(1, PACK - 1):
                 widen_on_vector(1, 2, 3, t)
 
             last = NT - 1
             products = [(i, q) for i in tiles for q in range(2)] + [(i, q) for q in range(2, NQ) for i in tiles]
             multiplied = []
 
-            def multiply_up_to(n):
+            def multiply_up_to(n, paced=False):
                 for i, q in products[len(multiplied) : n]:
-                    multiply(i, q)
+                    multiply(i, q, paced)
                     multiplied.append((i, q))
 
-            def add_biases(n0, n1, ready):
+            def add_biases(n0, n1, ready, ahead=PRODUCT_BANKS, paced=False):
                 for n in range(n0, n1):
                     i, q = products[n]
                     add_bias(i, q)
@@ -327,18 +333,20 @@ def tile_equivariantfeedforward_pa_kernel(tc, h, x1, pre1, w1_0_bytes, w1_0_scal
                         finish(i, q * BANK, (q + 1) * BANK)
                     elif q == 1:
                         finish(i, 0, HALF)
-                    multiply_up_to(min(ready, n + 1 + PRODUCT_BANKS))
+                    multiply_up_to(min(ready, n + 1 + ahead), paced)
 
             square(last, range(1))
             root(last - 1)
             multiply_up_to(2)
             square(last, range(1, M1))
-            multiply_up_to(4)
+            multiply_up_to(3)
             sum_squares(last)
-            for t in range(PACK - 1):
+            multiply_up_to(4)
+            for t in range(2):
                 widen_on_scalar(1, 3, 4, t)
             root(last)
-            widen_on_vector(1, 3, 4, PACK - 1)
+            for t in range(2, PACK):
+                widen_on_vector(1, 3, 4, t)
             quantise_inv(last - 1)
             widen_on_vector(1, 2, 3, PACK - 1)
             interleave_w_on_gpsimd(NQ - 2)
@@ -347,13 +355,12 @@ def tile_equivariantfeedforward_pa_kernel(tc, h, x1, pre1, w1_0_bytes, w1_0_scal
             lay_w(7)
             add_biases(2, 6, 6)
             quantise_inv(last)
-            quantise_w(0, NQ - 2)
-            quantise_w(1, NQ - 2)
+            quantise_w(NQ - 2)
             interleave_w_on_gpsimd(NQ - 1)
             multiply_up_to(10)
             fetch_w(6, on_vector=True)
             fetch_w(7, on_vector=True)
-            add_biases(6, 10, 12)
-            quantise_w(0, NQ - 1)
-            quantise_w(1, NQ - 1)
+            add_biases(6, 10, 12, 3, True)
+            quantise_w(NQ - 1, 0, 1)
+            quantise_w(NQ - 1, 1, 2)
             add_biases(10, 16, 16)

@@ -147,8 +147,10 @@ def tile_equivariantfeedforward_pa_kernel(tc, h, x1, pre1, w1_0_bytes, w1_0_scal
             quantise(w_codes[q][:, c], w_scales[q][:, c], w_words[(g0, q) if q == NQ - 1 else q][:, g0 * BANK * PACK : g1 * BANK * PACK])
 
         def interleave_pre():
-            nc.vector.tensor_copy(out=pre_words[:].rearrange("p (r c) t -> p c t r", r=PACK),
-                                  in_=pre_raw[:].rearrange("p t (c r) -> p c t r", r=PACK))
+            dst = pre_words[:].rearrange("p (r c) t -> p c t r", r=PACK)
+            src = pre_raw[:].rearrange("p t (c r) -> p c t r", r=PACK)
+            nc.vector.tensor_copy(out=dst[:, :, :, : PACK - 1], in_=src[:, :, :, : PACK - 1])
+            nc.scalar.copy(out=dst[:, :, :, PACK - 1], in_=src[:, :, :, PACK - 1])
 
         def quantise_pre():
             quantise(pre_codes[:], pre_scales[:], pre_words[:].rearrange("p e t -> p (e t)"))
@@ -240,12 +242,12 @@ def tile_equivariantfeedforward_pa_kernel(tc, h, x1, pre1, w1_0_bytes, w1_0_scal
             load_w(0, 0, 2, 4)
             load_h(0)
             nc.sync.dma_start(out=pre_raw[:], in_=pre1.rearrange("(p t) e -> p t e", t=PACK))
-            load_w(1, 0, 0, 3)
+            load_w(1, 0, 0, 2)
             load_x(1)
             load_h(1)
             load_x(2)
             load_h(2)
-            load_w(1, 0, 3, 4)
+            load_w(1, 0, 2, 4)
             load_x(3)
             load_h(3)
             load_w(0, 1, 0, PACK)
@@ -272,27 +274,28 @@ def tile_equivariantfeedforward_pa_kernel(tc, h, x1, pre1, w1_0_bytes, w1_0_scal
             widen_on_scalar(1, 0, 2, 0)
             widen_on_scalar(1, 0, 2, 1)
             fetch_w(0)
-            widen_on_scalar(1, 0, 2, 2)
             fetch_w(1)
             turn_xh(1)
             fetch_xh(1)
             split_x(2)
             project(0)
             square(0)
+            widen_on_vector(1, 0, 2, 2)
             widen_on_vector(1, 0, 2, 3)
             split_x(3)
-            interleave_w_on_vector(0)
             quantise_xh(1)
+            interleave_w_on_vector(0)
             turn_xh(2)
             fetch_xh(2)
             lay_w(2)
             fetch_w(2)
             turn_xh(3)
             fetch_xh(3)
-            for t in range(3):
+            for t in range(2):
                 widen_on_vector(0, 2, 4, t)
             quantise_xh(2)
-            widen_on_vector(0, 2, 4, 3)
+            for t in range(2, PACK):
+                widen_on_vector(0, 2, 4, t)
             quantise_w(0)
             quantise_xh(3)
             project(1)
@@ -342,11 +345,10 @@ def tile_equivariantfeedforward_pa_kernel(tc, h, x1, pre1, w1_0_bytes, w1_0_scal
             multiply_up_to(3)
             sum_squares(last)
             multiply_up_to(4)
-            for t in range(2):
+            for t in range(PACK - 1):
                 widen_on_scalar(1, 3, 4, t)
             root(last)
-            for t in range(2, PACK):
-                widen_on_vector(1, 3, 4, t)
+            widen_on_vector(1, 3, 4, PACK - 1)
             quantise_inv(last - 1)
             widen_on_vector(1, 2, 3, PACK - 1)
             interleave_w_on_gpsimd(NQ - 2)

@@ -131,7 +131,8 @@ def tile_equivariantfeedforward_pa_kernel(tc, h, x1, pre1, w1_0_bytes, w1_0_scal
             laid = take_bank(("w", n), [2, P * PACK], BF16)
             for j in range(2):
                 c0 = (2 * n + j) * P
-                nc.tensor.matmul(laid[:, j, :], lhsT=ident_bf16[:], rhs=w_columns(0, c0, c0 + P), start=True, stop=True)
+                nc.tensor.matmul(laid[:, j, :].rearrange("p (n t) -> p t n", t=PACK), lhsT=ident_bf16[:],
+                                 rhs=w_columns(0, c0, c0 + P).rearrange("p n t -> p t n"), start=True, stop=True)
 
         def fetch_w(n, on_vector=False):
             width = 2 * P * PACK

@@ -23,8 +23,6 @@ HALF = FF // 2
 NQ = FF // BANK
 UNITS = M1 + 1
 PSUM_BANKS = 8
-PRODUCT_BANKS = 4
-BIAS_RUN = 5
 RUN = 4
 
 FLOPS = 2 * NT * P * M1 * D * D + 2 * NT * P * 2 * D * FF
@@ -42,7 +40,7 @@ def tile_equivariantfeedforward_pa_kernel(tc, h, x1, pre1, w1_0_bytes, w1_0_scal
         free_banks = list(range(PSUM_BANKS))
         held = {}
 
-        def take_bank(key, shape, dtype, newest=False):
+        def take_bank(key, shape, dtype, newest=0):
             n = free_banks[-1 if newest else 0]
             free_banks.remove(n)
             held[key] = (psum.tile([P] + shape, dtype, name=f"bank{n}"), n)
@@ -58,20 +56,19 @@ def tile_equivariantfeedforward_pa_kernel(tc, h, x1, pre1, w1_0_bytes, w1_0_scal
         w_bytes = {}
         x_raw = [sbuf(f"x_raw{i}", [D * M1], BF16) for i in tiles]
         h_raw = [sbuf(f"h_raw{i}", [D], BF16) for i in tiles]
+        x_split = [sbuf(f"x_split{i}", [M1, D], BF16) for i in tiles]
         pre_raw = sbuf("pre_raw", [PACK, D], BF16)
         w_scale = sbuf("w_scale", [2, PACK], F32)
         bias = sbuf("bias", [FF], BF16)
         ident_f32 = sbuf("ident_f32", [P], F32)
         ident_bf16 = sbuf("ident_bf16", [P], BF16)
-        spans = [(0, 0, 2), (0, 2, 4), (1, 0, 2), (1, 2, 3), (1, 3, 4)]
-        w_wide = {(g, q0): sbuf(f"w_wide{g}{q0}", [PACK, (q1 - q0) * BANK], BF16) for g, q0, q1 in spans}
+        w_wide = {}
         w_words = {}
         w_codes = [sbuf(f"w_codes{q}", [2 * BANK], U32) for q in range(NQ)]
         w_scales = [sbuf(f"w_scales{q}", [2 * BANK], U8) for q in range(NQ)]
         pre_words = sbuf("pre_words", [D, PACK], BF16)
         pre_codes = sbuf("pre_codes", [D], U32)
         pre_scales = sbuf("pre_scales", [D], U8)
-        x_split = [sbuf(f"x_split{i}", [M1, D], BF16) for i in tiles]
         xh_words = [sbuf(f"xh_words{i}", [UNITS * P * PACK], BF16) for i in tiles]
         xh_codes = [sbuf(f"xh_codes{i}", [UNITS * P], U32) for i in tiles]
         xh_scales = [sbuf(f"xh_scales{i}", [UNITS * P], U8) for i in tiles]
@@ -80,6 +77,12 @@ def tile_equivariantfeedforward_pa_kernel(tc, h, x1, pre1, w1_0_bytes, w1_0_scal
         inv_codes = [sbuf(f"inv_codes{i}", [P], U32) for i in tiles]
         inv_scales = [sbuf(f"inv_scales{i}", [P], U8) for i in tiles]
         rows = [sbuf(f"rows{i}", [FF], F32) for i in tiles]
+
+        def copy_on(engine, dst, src):
+            if engine == "vector":
+                nc.vector.tensor_copy(out=dst, in_=src)
+            else:
+                nc.scalar.copy(out=dst, in_=src)
 
         def load_w(g, half, t0, t1):
             raw = sbuf(f"w_bytes{g}{half}{t0}", [t1 - t0, HALF], U8)
@@ -93,24 +96,24 @@ def tile_equivariantfeedforward_pa_kernel(tc, h, x1, pre1, w1_0_bytes, w1_0_scal
         def load_h(i):
             nc.sync.dma_start(out=h_raw[i][:], in_=h[i])
 
+        def load_pre():
+            nc.sync.dma_start(out=pre_raw[:], in_=pre1.rearrange("(p t) e -> p t e", t=PACK))
+
         def quantise(codes, scales, words):
             nc.vector.quantize_mx(out=codes.bitcast(FP8X4), scales=scales, in_=words)
 
-        def widen_operands(g, q0, q1, t):
-            raw = w_bytes[g, q0 // 2, t][:, q0 % 2 * BANK : (q1 - q0 // 2 * 2) * BANK]
-            return w_wide[g, q0][:, t, :], raw.bitcast(FP8), w_scale[:, g, t : t + 1]
-
-        def widen_on_vector(g, q0, q1, t):
-            dst, src, scale = widen_operands(g, q0, q1, t)
-            nc.vector.tensor_scalar(out=dst, in0=src, scalar1=scale, scalar2=None, op0=ALU.mult)
-
-        def widen_on_scalar(g, q0, q1, t):
-            dst, src, scale = widen_operands(g, q0, q1, t)
-            nc.scalar.activation(out=dst, in_=src, func=ACT.Copy, scale=scale)
-
-        def w_columns(g, c0, c1):
-            q0 = max(a for k, a, b in spans if k == g and a * BANK <= c0)
-            return w_wide[g, q0][:, :, c0 - q0 * BANK : c1 - q0 * BANK].rearrange("p t n -> p n t")
+        def widen(engine, g, q0, q1, t):
+            if (g, q0) not in w_wide:
+                wide = sbuf(f"w_wide{g}{q0}", [PACK, (q1 - q0) * BANK], BF16)
+                for q in range(q0, q1):
+                    w_wide[g, q] = wide[:, :, (q - q0) * BANK : (q - q0 + 1) * BANK]
+                w_wide[g, q0, q1] = wide
+            raw = w_bytes[g, q0 // 2, t][:, q0 % 2 * BANK : (q1 - q0 // 2 * 2) * BANK].bitcast(FP8)
+            dst, scale = w_wide[g, q0, q1][:, t, :], w_scale[:, g, t : t + 1]
+            if engine == "vector":
+                nc.vector.tensor_scalar(out=dst, in0=raw, scalar1=scale, scalar2=None, op0=ALU.mult)
+            else:
+                nc.scalar.activation(out=dst, in_=raw, func=ACT.Copy, scale=scale)
 
         def words_of(g, q):
             key = (g, q) if q == NQ - 1 else q
@@ -118,55 +121,52 @@ def tile_equivariantfeedforward_pa_kernel(tc, h, x1, pre1, w1_0_bytes, w1_0_scal
                 w_words[key] = sbuf(f"w_words{q - g if q == NQ - 1 else q}", [2 * BANK * PACK], BF16)
             return w_words[key][:, g * BANK * PACK : (g + 1) * BANK * PACK]
 
-        def interleave_w_on_vector(q, g=1):
+        def interleave_w_on_vector(g, q):
             nc.vector.tensor_copy(out=words_of(g, q).rearrange("p (c i t) -> p c t i", i=RUN, t=PACK),
-                                  in_=w_columns(g, q * BANK, (q + 1) * BANK).rearrange("p (c i) t -> p c t i", i=RUN))
+                                  in_=w_wide[g, q].rearrange("p t (c i) -> p c t i", i=RUN))
 
-        def interleave_w_on_gpsimd(q):
-            nc.gpsimd.tensor_scalar(out=words_of(1, q).rearrange("p (n t) -> p n t", t=PACK),
-                                    in0=w_columns(1, q * BANK, (q + 1) * BANK),
+        def interleave_w_on_gpsimd(g, q):
+            nc.gpsimd.tensor_scalar(out=words_of(g, q).rearrange("p (n t) -> p n t", t=PACK),
+                                    in0=w_wide[g, q].rearrange("p t n -> p n t"),
                                     scalar1=1.0, scalar2=0.0, op0=ALU.mult, op1=ALU.add)
 
-        def lay_w(n):
-            laid = take_bank(("w", n), [2, P * PACK], BF16)
-            for j in range(2):
-                c0 = (2 * n + j) * P
+        def lay_w(g, q, b, j0=0, j1=2):
+            if j0 == 0:
+                take_bank(("w", g, q, b), [2, P * PACK], BF16)
+            laid = held["w", g, q, b][0]
+            for j in range(j0, j1):
+                c0 = (2 * b + j) * P
                 nc.tensor.matmul(laid[:, j, :].rearrange("p (n t) -> p t n", t=PACK), lhsT=ident_bf16[:],
-                                 rhs=w_columns(0, c0, c0 + P).rearrange("p n t -> p t n"), start=True, stop=True)
+                                 rhs=w_wide[g, q][:, :, c0 : c0 + P], start=True, stop=True)
 
-        def fetch_w(n, on_vector=False):
+        def fetch_w(g, q, b, engine="scalar"):
             width = 2 * P * PACK
-            dst = words_of(0, n // 2)[:, n % 2 * width : (n % 2 + 1) * width]
-            src = empty_bank(("w", n))[:].rearrange("p j c -> p (j c)")
-            if on_vector:
-                nc.vector.tensor_copy(out=dst, in_=src)
-            else:
-                nc.scalar.copy(out=dst, in_=src)
+            copy_on(engine, words_of(g, q)[:, b * width : (b + 1) * width],
+                    empty_bank(("w", g, q, b))[:].rearrange("p j c -> p (j c)"))
 
         def quantise_w(q, g0=0, g1=2):
             c = slice(g0 * BANK, g1 * BANK)
             quantise(w_codes[q][:, c], w_scales[q][:, c], w_words[(g0, q) if q == NQ - 1 else q][:, g0 * BANK * PACK : g1 * BANK * PACK])
 
-        def interleave_pre():
+        def interleave_pre(on_scalar=1):
             dst = pre_words[:].rearrange("p (r c) t -> p c t r", r=PACK)
             src = pre_raw[:].rearrange("p t (c r) -> p c t r", r=PACK)
-            nc.vector.tensor_copy(out=dst[:, :, :, : PACK - 1], in_=src[:, :, :, : PACK - 1])
-            nc.scalar.copy(out=dst[:, :, :, PACK - 1], in_=src[:, :, :, PACK - 1])
+            cut = PACK - on_scalar
+            nc.vector.tensor_copy(out=dst[:, :, :, :cut], in_=src[:, :, :, :cut])
+            if on_scalar:
+                nc.scalar.copy(out=dst[:, :, :, cut:], in_=src[:, :, :, cut:])
 
         def quantise_pre():
             quantise(pre_codes[:], pre_scales[:], pre_words[:].rearrange("p e t -> p (e t)"))
 
-        def split_x(i):
-            dst = x_split[i][:].rearrange("p m (u c e) -> p c m u e", u=2, e=2)
-            src = x_raw[i][:].rearrange("p (c u e m) -> p c m u e", u=2, e=2, m=M1)
-            nc.vector.tensor_copy(out=dst[:, :, :2], in_=src[:, :, :2])
-            if i == 0:
-                nc.scalar.copy(out=dst[:, :, 2:], in_=src[:, :, 2:])
-            else:
-                nc.vector.tensor_copy(out=dst[:, :, 2:], in_=src[:, :, 2:])
+        def split_x(i, engine="vector"):
+            dst = x_split[i][:].rearrange("p m (u c e) -> p m c u e", u=2, e=2)
+            src = x_raw[i][:].rearrange("p (c u e m) -> p m c u e", u=2, e=2, m=M1)
+            nc.vector.tensor_copy(out=dst[:, :2], in_=src[:, :2])
+            copy_on(engine, dst[:, 2], src[:, 2])
 
-        def turn_xh(i):
-            for b in range(2):
+        def turn_xh(i, b0=0, b1=2):
+            for b in range(b0, b1):
                 turned = take_bank(("xh", i, b), [2, 2, P], F32)
                 for j in range(2):
                     m = 2 * b + j
@@ -177,34 +177,32 @@ def tile_equivariantfeedforward_pa_kernel(tc, h, x1, pre1, w1_0_bytes, w1_0_scal
                             words = h_raw[i][:].bitcast(F32)[:, u : D // 2 : 2]
                         nc.tensor.transpose(turned[:, j, u, :], words, ident_f32[:])
 
-        def fetch_xh(i):
-            for b in range(2):
+        def fetch_xh(i, b0=0, b1=2, engine="scalar"):
+            for b in range(b0, b1):
                 dst = xh_words[i][:, b * 2 * P * PACK : (b + 1) * 2 * P * PACK].bitcast(F32)
-                nc.scalar.copy(out=dst.rearrange("p (j n a u) -> p j n u a", j=2, a=2, u=2),
-                               in_=empty_bank(("xh", i, b))[:].rearrange("p j u (n a) -> p j n u a", a=2))
+                copy_on(engine, dst.rearrange("p (j n a u) -> p j n u a", j=2, a=2, u=2),
+                        empty_bank(("xh", i, b))[:].rearrange("p j u (n a) -> p j n u a", a=2))
 
         def quantise_xh(i):
             quantise(xh_codes[i][:], xh_scales[i][:], xh_words[i][:])
 
-        def xh_operand(i, m):
-            c = slice(m * P, (m + 1) * P)
-            return xh_codes[i][:, c].bitcast(FP8X4), xh_scales[i][:, c]
-
-        def project(i):
-            for m in range(M1):
+        def project(i, m0=0, m1=M1):
+            for m in range(m0, m1):
                 pm = take_bank(("pm", i, m), [BANK], F32)
-                codes, scales = xh_operand(i, m)
-                nc.tensor.matmul_mx(out=pm[:], lhsT=codes, lhsT_scale=scales, rhs=pre_codes[:].bitcast(FP8X4),
-                                    rhs_scale=pre_scales[:], start=True, stop=True)
+                c = slice(m * P, (m + 1) * P)
+                nc.tensor.matmul_mx(out=pm[:], lhsT=xh_codes[i][:, c].bitcast(FP8X4), lhsT_scale=xh_scales[i][:, c],
+                                    rhs=pre_codes[:].bitcast(FP8X4), rhs_scale=pre_scales[:], start=True, stop=True)
 
-        def square(i, components=range(M1)):
-            for m in components:
+        def square(i, m0=0, m1=M1):
+            for m in range(m0, m1):
                 nc.scalar.activation(out=squares[i, m][:].rearrange("p r c -> p (r c)"), in_=empty_bank(("pm", i, m))[:],
                                      func=ACT.Square)
 
-        def sum_squares(i):
-            total = take_bank(("sum", i), [PACK, P], F32)
-            for m in range(M1):
+        def sum_squares(i, m0=0, m1=M1):
+            if m0 == 0:
+                take_bank(("sum", i), [PACK, P], F32)
+            total = held["sum", i][0]
+            for m in range(m0, m1):
                 for r in range(PACK):
                     nc.tensor.matmul(total[:, r, :], lhsT=squares[i, m][:, r, :], rhs=ident_f32[:],
                                      start=(m, r) == (0, 0), stop=(m, r) == (M1 - 1, PACK - 1), is_transpose=True)
@@ -216,14 +214,14 @@ def tile_equivariantfeedforward_pa_kernel(tc, h, x1, pre1, w1_0_bytes, w1_0_scal
         def quantise_inv(i):
             quantise(inv_codes[i][:], inv_scales[i][:], inv_words[i][:].rearrange("p n r -> p (n r)"))
 
-        def multiply(i, q, paced=False, passes=(0, 1)):
-            if ("acc", i, q) not in held:
-                take_bank(("acc", i, q), [BANK], F32, paced)
+        def multiply(i, q, g0=0, g1=2, newest=0):
+            if g0 == 0:
+                take_bank(("acc", i, q), [BANK], F32, newest)
             acc = held["acc", i, q][0]
-            sides = [xh_operand(i, M1), (inv_codes[i][:].bitcast(FP8X4), inv_scales[i][:])]
-            for g in passes:
+            sides = [(xh_codes[i][:, M1 * P :], xh_scales[i][:, M1 * P :]), (inv_codes[i][:], inv_scales[i][:])]
+            for g in range(g0, g1):
                 c = slice(g * BANK, (g + 1) * BANK)
-                nc.tensor.matmul_mx(out=acc[:], lhsT=sides[g][0], lhsT_scale=sides[g][1],
+                nc.tensor.matmul_mx(out=acc[:], lhsT=sides[g][0].bitcast(FP8X4), lhsT_scale=sides[g][1],
                                     rhs=w_codes[q][:, c].bitcast(FP8X4), rhs_scale=w_scales[q][:, c],
                                     start=(g == 0), stop=(g == 1))
 
@@ -231,18 +229,30 @@ def tile_equivariantfeedforward_pa_kernel(tc, h, x1, pre1, w1_0_bytes, w1_0_scal
             nc.vector.tensor_tensor(out=rows[i][:, q * BANK : (q + 1) * BANK], in0=empty_bank(("acc", i, q))[:],
                                     in1=bias[:, q * BANK : (q + 1) * BANK], op=ALU.add)
 
-        def finish(i, c0, c1):
-            part = rows[i][:, c0:c1]
+        def finish(i, q0, q1):
+            part = rows[i][:, q0 * BANK : q1 * BANK]
             nc.scalar.activation(out=part, in_=part, func=ACT.Silu)
-            nc.sync.dma_start(out=out[i, :, c0:c1], in_=part)
+            nc.sync.dma_start(out=out[i, :, q0 * BANK : q1 * BANK], in_=part)
 
-        with tc.manual_schedule():
+        def set_up():
             nc.scalar.dma_start(out=w_scale[:], in_=w1_0_scale.rearrange("(g p t) o -> p g (t o)", p=P, t=PACK))
+            warm = sbuf("warm", [1], F32)
+            nc.vector.memset(warm[:], 1.0)
+            nc.scalar.activation(out=warm[:], in_=warm[:], func=ACT.Sqrt)
+            make_identity(nc, ident_bf16[:])
+            make_identity(nc, ident_f32[:])
+
+        def load_bias():
+            nc.sync.dma_start(out=bias[:], in_=b1_0.partition_broadcast(P))
+
+        V, S = "vector", "scalar"
+        with tc.manual_schedule():
+            set_up()
             load_x(0)
             load_w(0, 0, 0, 2)
             load_w(0, 0, 2, 4)
             load_h(0)
-            nc.sync.dma_start(out=pre_raw[:], in_=pre1.rearrange("(p t) e -> p t e", t=PACK))
+            load_pre()
             load_w(1, 0, 0, 2)
             load_x(1)
             load_h(1)
@@ -251,65 +261,60 @@ def tile_equivariantfeedforward_pa_kernel(tc, h, x1, pre1, w1_0_bytes, w1_0_scal
             load_w(1, 0, 2, 4)
             load_x(3)
             load_h(3)
-            load_w(0, 1, 0, PACK)
-            load_w(1, 1, 0, PACK)
-            nc.sync.dma_start(out=bias[:], in_=b1_0.partition_broadcast(P))
-            warm = sbuf("warm", [1], F32)
-            nc.vector.memset(warm[:], 1.0)
-            nc.scalar.activation(out=warm[:], in_=warm[:], func=ACT.Sqrt)
-            make_identity(nc, ident_f32[:])
-            make_identity(nc, ident_bf16[:])
-
-            split_x(0)
-            widen_on_scalar(0, 0, 2, 0)
-            for t in range(1, PACK):
-                widen_on_vector(0, 0, 2, t)
+            load_w(0, 1, 0, 4)
+            load_w(1, 1, 0, 4)
+            load_bias()
+            split_x(0, S)
+            widen(S, 0, 0, 2, 0)
+            widen(V, 0, 0, 2, 1)
+            widen(V, 0, 0, 2, 2)
+            widen(V, 0, 0, 2, 3)
             turn_xh(0)
             fetch_xh(0)
-            lay_w(0)
-            lay_w(1)
+            lay_w(0, 0, 0)
+            lay_w(0, 0, 1)
             interleave_pre()
             quantise_xh(0)
             split_x(1)
             quantise_pre()
-            widen_on_scalar(1, 0, 2, 0)
-            widen_on_scalar(1, 0, 2, 1)
-            fetch_w(0)
-            fetch_w(1)
+            widen(S, 1, 0, 2, 0)
+            widen(S, 1, 0, 2, 1)
+            fetch_w(0, 0, 0)
+            fetch_w(0, 0, 1)
             turn_xh(1)
             fetch_xh(1)
             split_x(2)
             project(0)
             square(0)
-            widen_on_vector(1, 0, 2, 2)
-            widen_on_vector(1, 0, 2, 3)
+            widen(V, 1, 0, 2, 2)
+            widen(V, 1, 0, 2, 3)
             split_x(3)
             quantise_xh(1)
-            interleave_w_on_vector(0)
+            interleave_w_on_vector(1, 0)
             turn_xh(2)
             fetch_xh(2)
-            lay_w(2)
-            fetch_w(2)
+            lay_w(0, 1, 0)
+            fetch_w(0, 1, 0)
             turn_xh(3)
             fetch_xh(3)
-            for t in range(2):
-                widen_on_vector(0, 2, 4, t)
+            widen(V, 0, 2, 4, 0)
+            widen(V, 0, 2, 4, 1)
             quantise_xh(2)
-            for t in range(2, PACK):
-                widen_on_vector(0, 2, 4, t)
+            widen(V, 0, 2, 4, 2)
+            widen(V, 0, 2, 4, 3)
             quantise_w(0)
             quantise_xh(3)
             project(1)
             square(1)
             sum_squares(0)
             root(0)
-            lay_w(3)
-            fetch_w(3)
-            interleave_w_on_vector(1)
+            lay_w(0, 1, 1)
+            fetch_w(0, 1, 1)
+            interleave_w_on_vector(1, 1)
             quantise_inv(0)
-            widen_on_vector(1, 2, 3, 0)
+            widen(V, 1, 2, 3, 0)
             quantise_w(1)
-            interleave_w_on_vector(2, 0)
+            interleave_w_on_vector(0, 2)
             project(2)
             square(2)
             sum_squares(1)
@@ -317,53 +322,71 @@ def tile_equivariantfeedforward_pa_kernel(tc, h, x1, pre1, w1_0_bytes, w1_0_scal
             project(3)
             sum_squares(2)
             quantise_inv(1)
-            for t in range(1, PACK - 1):
-                widen_on_vector(1, 2, 3, t)
-
-            last = NT - 1
-            products = [(i, q) for i in tiles for q in range(2)] + [(i, q) for q in range(2, NQ) for i in tiles]
-            multiplied = []
-
-            def multiply_up_to(n, paced=False):
-                for i, q in products[len(multiplied) : n]:
-                    multiply(i, q, paced)
-                    multiplied.append((i, q))
-
-            def add_biases(n0, n1, ready, ahead=PRODUCT_BANKS, paced=False):
-                for n in range(n0, n1):
-                    i, q = products[n]
-                    add_bias(i, q)
-                    if q >= 2 or i == 0:
-                        finish(i, q * BANK, (q + 1) * BANK)
-                    elif q == 1:
-                        finish(i, 0, HALF)
-                    multiply_up_to(min(ready, n + 1 + ahead), paced)
-
-            square(last, range(1))
-            root(last - 1)
-            multiply_up_to(2)
-            square(last, range(1, M1))
-            multiply_up_to(3)
-            sum_squares(last)
-            multiply_up_to(4)
-            for t in range(PACK - 1):
-                widen_on_scalar(1, 3, 4, t)
-            root(last)
-            widen_on_vector(1, 3, 4, PACK - 1)
-            quantise_inv(last - 1)
-            widen_on_vector(1, 2, 3, PACK - 1)
-            interleave_w_on_gpsimd(NQ - 2)
-            add_biases(0, 2, 6)
-            lay_w(6)
-            lay_w(7)
-            add_biases(2, 6, 6)
-            quantise_inv(last)
-            quantise_w(NQ - 2)
-            interleave_w_on_gpsimd(NQ - 1)
-            multiply_up_to(10)
-            fetch_w(6, on_vector=True)
-            fetch_w(7, on_vector=True)
-            add_biases(6, 10, 12, 3, True)
-            quantise_w(NQ - 1, 0, 1)
-            quantise_w(NQ - 1, 1, 2)
-            add_biases(10, 16, 16)
+            widen(V, 1, 2, 3, 1)
+            widen(V, 1, 2, 3, 2)
+            square(3, 0, 1)
+            root(2)
+            multiply(0, 0)
+            multiply(0, 1)
+            square(3, 1, 3)
+            multiply(1, 0)
+            sum_squares(3)
+            multiply(1, 1)
+            widen(S, 1, 3, 4, 0)
+            widen(S, 1, 3, 4, 1)
+            widen(S, 1, 3, 4, 2)
+            root(3)
+            widen(V, 1, 2, 3, 3)
+            quantise_inv(2)
+            interleave_w_on_gpsimd(1, 2)
+            add_bias(0, 0)
+            finish(0, 0, 1)
+            multiply(2, 0)
+            add_bias(0, 1)
+            finish(0, 1, 2)
+            multiply(2, 1)
+            lay_w(0, 3, 0)
+            lay_w(0, 3, 1)
+            add_bias(1, 0)
+            add_bias(1, 1)
+            finish(1, 0, 2)
+            add_bias(2, 0)
+            add_bias(2, 1)
+            finish(2, 0, 2)
+            widen(V, 1, 3, 4, 3)
+            quantise_w(2)
+            interleave_w_on_gpsimd(1, 3)
+            quantise_inv(3)
+            multiply(3, 0)
+            multiply(3, 1)
+            multiply(0, 2)
+            multiply(1, 2)
+            fetch_w(0, 3, 0, V)
+            fetch_w(0, 3, 1, V)
+            add_bias(3, 0)
+            add_bias(3, 1)
+            finish(3, 0, 2)
+            multiply(2, 2, 0, 2, 1)
+            add_bias(0, 2)
+            finish(0, 2, 3)
+            multiply(3, 2, 0, 2, 1)
+            add_bias(1, 2)
+            finish(1, 2, 3)
+            quantise_w(3, 0, 1)
+            quantise_w(3, 1, 2)
+            add_bias(2, 2)
+            finish(2, 2, 3)
+            multiply(0, 3)
+            multiply(1, 3)
+            multiply(2, 3)
+            add_bias(3, 2)
+            finish(3, 2, 3)
+            multiply(3, 3)
+            add_bias(0, 3)
+            finish(0, 3, 4)
+            add_bias(1, 3)
+            finish(1, 3, 4)
+            add_bias(2, 3)
+            finish(2, 3, 4)
+            add_bias(3, 3)
+            finish(3, 3, 4)

@@ -23,7 +23,8 @@ HALF = FF // 2
 NQ = FF // BANK
 UNITS = M1 + 1
 PSUM_BANKS = 8
-RUN = 4
+RUN = 8
+VECTOR, SCALAR = "vector", "scalar"
 
 FLOPS = 2 * NT * P * M1 * D * D + 2 * NT * P * 2 * D * FF
 
@@ -40,7 +41,7 @@ def tile_equivariantfeedforward_pa_kernel(tc, h, x1, pre1, w1_0_bytes, w1_0_scal
         free_banks = list(range(PSUM_BANKS))
         held = {}
 
-        def take_bank(key, shape, dtype, newest=0):
+        def take_bank(key, shape, dtype, newest=False):
             n = free_banks[-1 if newest else 0]
             free_banks.remove(n)
             held[key] = (psum.tile([P] + shape, dtype, name=f"bank{n}"), n)
@@ -62,6 +63,7 @@ def tile_equivariantfeedforward_pa_kernel(tc, h, x1, pre1, w1_0_bytes, w1_0_scal
         bias = sbuf("bias", [FF], BF16)
         ident_f32 = sbuf("ident_f32", [P], F32)
         ident_bf16 = sbuf("ident_bf16", [P], BF16)
+        w_span = {}
         w_wide = {}
         w_words = {}
         w_codes = [sbuf(f"w_codes{q}", [2 * BANK], U32) for q in range(NQ)]
@@ -79,7 +81,7 @@ def tile_equivariantfeedforward_pa_kernel(tc, h, x1, pre1, w1_0_bytes, w1_0_scal
         rows = [sbuf(f"rows{i}", [FF], F32) for i in tiles]
 
         def copy_on(engine, dst, src):
-            if engine == "vector":
+            if engine == VECTOR:
                 nc.vector.tensor_copy(out=dst, in_=src)
             else:
                 nc.scalar.copy(out=dst, in_=src)
@@ -102,24 +104,27 @@ def tile_equivariantfeedforward_pa_kernel(tc, h, x1, pre1, w1_0_bytes, w1_0_scal
         def quantise(codes, scales, words):
             nc.vector.quantize_mx(out=codes.bitcast(FP8X4), scales=scales, in_=words)
 
-        def widen(engine, g, q0, q1, t):
+        def widen(engine, g, q0, q1, planes):
             if (g, q0) not in w_wide:
-                wide = sbuf(f"w_wide{g}{q0}", [PACK, (q1 - q0) * BANK], BF16)
+                w_span[g, q0] = sbuf(f"w_wide{g}{q0}", [PACK, (q1 - q0) * BANK], BF16)
                 for q in range(q0, q1):
-                    w_wide[g, q] = wide[:, :, (q - q0) * BANK : (q - q0 + 1) * BANK]
-                w_wide[g, q0, q1] = wide
-            raw = w_bytes[g, q0 // 2, t][:, q0 % 2 * BANK : (q1 - q0 // 2 * 2) * BANK].bitcast(FP8)
-            dst, scale = w_wide[g, q0, q1][:, t, :], w_scale[:, g, t : t + 1]
-            if engine == "vector":
-                nc.vector.tensor_scalar(out=dst, in0=raw, scalar1=scale, scalar2=None, op0=ALU.mult)
-            else:
-                nc.scalar.activation(out=dst, in_=raw, func=ACT.Copy, scale=scale)
+                    w_wide[g, q] = w_span[g, q0][:, :, (q - q0) * BANK : (q - q0 + 1) * BANK]
+            for t in planes:
+                raw = w_bytes[g, q0 // 2, t][:, q0 % 2 * BANK : (q1 - q0 // 2 * 2) * BANK].bitcast(FP8)
+                dst, scale = w_span[g, q0][:, t, :], w_scale[:, g, t : t + 1]
+                if engine == VECTOR:
+                    nc.vector.tensor_scalar(out=dst, in0=raw, scalar1=scale, scalar2=None, op0=ALU.mult)
+                else:
+                    nc.scalar.activation(out=dst, in_=raw, func=ACT.Copy, scale=scale)
+
+        def words_tile(g, q):
+            key, buffer = ((g, q), q - g) if q == NQ - 1 else (q, q)
+            if key not in w_words:
+                w_words[key] = sbuf(f"w_words{buffer}", [2 * BANK * PACK], BF16)
+            return w_words[key]
 
         def words_of(g, q):
-            key = (g, q) if q == NQ - 1 else q
-            if key not in w_words:
-                w_words[key] = sbuf(f"w_words{q - g if q == NQ - 1 else q}", [2 * BANK * PACK], BF16)
-            return w_words[key][:, g * BANK * PACK : (g + 1) * BANK * PACK]
+            return words_tile(g, q)[:, g * BANK * PACK : (g + 1) * BANK * PACK]
 
         def interleave_w_on_vector(g, q):
             nc.vector.tensor_copy(out=words_of(g, q).rearrange("p (c i t) -> p c t i", i=RUN, t=PACK),
@@ -130,43 +135,39 @@ def tile_equivariantfeedforward_pa_kernel(tc, h, x1, pre1, w1_0_bytes, w1_0_scal
                                     in0=w_wide[g, q].rearrange("p t n -> p n t"),
                                     scalar1=1.0, scalar2=0.0, op0=ALU.mult, op1=ALU.add)
 
-        def lay_w(g, q, b, j0=0, j1=2):
-            if j0 == 0:
-                take_bank(("w", g, q, b), [2, P * PACK], BF16)
-            laid = held["w", g, q, b][0]
-            for j in range(j0, j1):
+        def lay_w(q, b):
+            laid = take_bank(("w", q, b), [2, P * PACK], BF16)
+            for j in range(2):
                 c0 = (2 * b + j) * P
                 nc.tensor.matmul(laid[:, j, :].rearrange("p (n t) -> p t n", t=PACK), lhsT=ident_bf16[:],
-                                 rhs=w_wide[g, q][:, :, c0 : c0 + P], start=True, stop=True)
+                                 rhs=w_wide[0, q][:, :, c0 : c0 + P], start=True, stop=True)
 
-        def fetch_w(g, q, b, engine="scalar"):
+        def fetch_w(engine, q, b):
             width = 2 * P * PACK
-            copy_on(engine, words_of(g, q)[:, b * width : (b + 1) * width],
-                    empty_bank(("w", g, q, b))[:].rearrange("p j c -> p (j c)"))
+            copy_on(engine, words_of(0, q)[:, b * width : (b + 1) * width],
+                    empty_bank(("w", q, b))[:].rearrange("p j c -> p (j c)"))
 
         def quantise_w(q, g0=0, g1=2):
             c = slice(g0 * BANK, g1 * BANK)
-            quantise(w_codes[q][:, c], w_scales[q][:, c], w_words[(g0, q) if q == NQ - 1 else q][:, g0 * BANK * PACK : g1 * BANK * PACK])
+            quantise(w_codes[q][:, c], w_scales[q][:, c], words_tile(g0, q)[:, c.start * PACK : c.stop * PACK])
 
-        def interleave_pre(on_scalar=1):
+        def interleave_pre():
             dst = pre_words[:].rearrange("p (r c) t -> p c t r", r=PACK)
             src = pre_raw[:].rearrange("p t (c r) -> p c t r", r=PACK)
-            cut = PACK - on_scalar
-            nc.vector.tensor_copy(out=dst[:, :, :, :cut], in_=src[:, :, :, :cut])
-            if on_scalar:
-                nc.scalar.copy(out=dst[:, :, :, cut:], in_=src[:, :, :, cut:])
+            nc.vector.tensor_copy(out=dst[:, :, :, : PACK - 1], in_=src[:, :, :, : PACK - 1])
+            nc.scalar.copy(out=dst[:, :, :, PACK - 1 :], in_=src[:, :, :, PACK - 1 :])
 
         def quantise_pre():
             quantise(pre_codes[:], pre_scales[:], pre_words[:].rearrange("p e t -> p (e t)"))
 
-        def split_x(i, engine="vector"):
+        def split_x(i, engine=VECTOR):
             dst = x_split[i][:].rearrange("p m (u c e) -> p m c u e", u=2, e=2)
             src = x_raw[i][:].rearrange("p (c u e m) -> p m c u e", u=2, e=2, m=M1)
             nc.vector.tensor_copy(out=dst[:, :2], in_=src[:, :2])
             copy_on(engine, dst[:, 2], src[:, 2])
 
-        def turn_xh(i, b0=0, b1=2):
-            for b in range(b0, b1):
+        def turn_xh(i):
+            for b in range(2):
                 turned = take_bank(("xh", i, b), [2, 2, P], F32)
                 for j in range(2):
                     m = 2 * b + j
@@ -177,17 +178,17 @@ def tile_equivariantfeedforward_pa_kernel(tc, h, x1, pre1, w1_0_bytes, w1_0_scal
                             words = h_raw[i][:].bitcast(F32)[:, u : D // 2 : 2]
                         nc.tensor.transpose(turned[:, j, u, :], words, ident_f32[:])
 
-        def fetch_xh(i, b0=0, b1=2, engine="scalar"):
-            for b in range(b0, b1):
+        def fetch_xh(i):
+            for b in range(2):
                 dst = xh_words[i][:, b * 2 * P * PACK : (b + 1) * 2 * P * PACK].bitcast(F32)
-                copy_on(engine, dst.rearrange("p (j n a u) -> p j n u a", j=2, a=2, u=2),
-                        empty_bank(("xh", i, b))[:].rearrange("p j u (n a) -> p j n u a", a=2))
+                nc.scalar.copy(out=dst.rearrange("p (j n a u) -> p j n u a", j=2, a=2, u=2),
+                               in_=empty_bank(("xh", i, b))[:].rearrange("p j u (n a) -> p j n u a", a=2))
 
         def quantise_xh(i):
             quantise(xh_codes[i][:], xh_scales[i][:], xh_words[i][:])
 
-        def project(i, m0=0, m1=M1):
-            for m in range(m0, m1):
+        def project(i):
+            for m in range(M1):
                 pm = take_bank(("pm", i, m), [BANK], F32)
                 c = slice(m * P, (m + 1) * P)
                 nc.tensor.matmul_mx(out=pm[:], lhsT=xh_codes[i][:, c].bitcast(FP8X4), lhsT_scale=xh_scales[i][:, c],
@@ -198,11 +199,9 @@ def tile_equivariantfeedforward_pa_kernel(tc, h, x1, pre1, w1_0_bytes, w1_0_scal
                 nc.scalar.activation(out=squares[i, m][:].rearrange("p r c -> p (r c)"), in_=empty_bank(("pm", i, m))[:],
                                      func=ACT.Square)
 
-        def sum_squares(i, m0=0, m1=M1):
-            if m0 == 0:
-                take_bank(("sum", i), [PACK, P], F32)
-            total = held["sum", i][0]
-            for m in range(m0, m1):
+        def sum_squares(i):
+            total = take_bank(("sum", i), [PACK, P], F32)
+            for m in range(M1):
                 for r in range(PACK):
                     nc.tensor.matmul(total[:, r, :], lhsT=squares[i, m][:, r, :], rhs=ident_f32[:],
                                      start=(m, r) == (0, 0), stop=(m, r) == (M1 - 1, PACK - 1), is_transpose=True)
@@ -214,12 +213,10 @@ def tile_equivariantfeedforward_pa_kernel(tc, h, x1, pre1, w1_0_bytes, w1_0_scal
         def quantise_inv(i):
             quantise(inv_codes[i][:], inv_scales[i][:], inv_words[i][:].rearrange("p n r -> p (n r)"))
 
-        def multiply(i, q, g0=0, g1=2, newest=0):
-            if g0 == 0:
-                take_bank(("acc", i, q), [BANK], F32, newest)
-            acc = held["acc", i, q][0]
+        def multiply(i, q, paced=False):
+            acc = take_bank(("acc", i, q), [BANK], F32, newest=paced)
             sides = [(xh_codes[i][:, M1 * P :], xh_scales[i][:, M1 * P :]), (inv_codes[i][:], inv_scales[i][:])]
-            for g in range(g0, g1):
+            for g in range(2):
                 c = slice(g * BANK, (g + 1) * BANK)
                 nc.tensor.matmul_mx(out=acc[:], lhsT=sides[g][0].bitcast(FP8X4), lhsT_scale=sides[g][1],
                                     rhs=w_codes[q][:, c].bitcast(FP8X4), rhs_scale=w_scales[q][:, c],
@@ -234,7 +231,8 @@ def tile_equivariantfeedforward_pa_kernel(tc, h, x1, pre1, w1_0_bytes, w1_0_scal
             nc.scalar.activation(out=part, in_=part, func=ACT.Silu)
             nc.sync.dma_start(out=out[i, :, q0 * BANK : q1 * BANK], in_=part)
 
-        def set_up():
+        last = NT - 1
+        with tc.manual_schedule():
             nc.scalar.dma_start(out=w_scale[:], in_=w1_0_scale.rearrange("(g p t) o -> p g (t o)", p=P, t=PACK))
             warm = sbuf("warm", [1], F32)
             nc.vector.memset(warm[:], 1.0)
@@ -242,151 +240,130 @@ def tile_equivariantfeedforward_pa_kernel(tc, h, x1, pre1, w1_0_bytes, w1_0_scal
             make_identity(nc, ident_bf16[:])
             make_identity(nc, ident_f32[:])
 
-        def load_bias():
-            nc.sync.dma_start(out=bias[:], in_=b1_0.partition_broadcast(P))
-
-        V, S = "vector", "scalar"
-        with tc.manual_schedule():
-            set_up()
             load_x(0)
             load_w(0, 0, 0, 2)
-            load_w(0, 0, 2, 4)
+            load_w(0, 0, 2, PACK)
             load_h(0)
             load_pre()
             load_w(1, 0, 0, 2)
-            load_x(1)
-            load_h(1)
-            load_x(2)
-            load_h(2)
-            load_w(1, 0, 2, 4)
-            load_x(3)
-            load_h(3)
-            load_w(0, 1, 0, 4)
-            load_w(1, 1, 0, 4)
-            load_bias()
-            split_x(0, S)
-            widen(S, 0, 0, 2, 0)
-            widen(V, 0, 0, 2, 1)
-            widen(V, 0, 0, 2, 2)
-            widen(V, 0, 0, 2, 3)
+            for i in range(1, last):
+                load_x(i)
+                load_h(i)
+            load_w(1, 0, 2, PACK)
+            load_x(last)
+            load_h(last)
+            for g in range(2):
+                load_w(g, 1, 0, PACK)
+            nc.sync.dma_start(out=bias[:], in_=b1_0.partition_broadcast(P))
+
+            split_x(0, SCALAR)
+            widen(SCALAR, 0, 0, 2, range(1))
+            widen(VECTOR, 0, 0, 2, range(1, PACK))
             turn_xh(0)
             fetch_xh(0)
-            lay_w(0, 0, 0)
-            lay_w(0, 0, 1)
+            for b in range(2):
+                lay_w(0, b)
             interleave_pre()
             quantise_xh(0)
             split_x(1)
             quantise_pre()
-            widen(S, 1, 0, 2, 0)
-            widen(S, 1, 0, 2, 1)
-            fetch_w(0, 0, 0)
-            fetch_w(0, 0, 1)
+            widen(SCALAR, 1, 0, 2, range(2))
+            for b in range(2):
+                fetch_w(SCALAR, 0, b)
+
             turn_xh(1)
             fetch_xh(1)
             split_x(2)
             project(0)
             square(0)
-            widen(V, 1, 0, 2, 2)
-            widen(V, 1, 0, 2, 3)
-            split_x(3)
+            widen(VECTOR, 1, 0, 2, range(2, PACK))
+            split_x(last)
             quantise_xh(1)
             interleave_w_on_vector(1, 0)
             turn_xh(2)
             fetch_xh(2)
-            lay_w(0, 1, 0)
-            fetch_w(0, 1, 0)
-            turn_xh(3)
-            fetch_xh(3)
-            widen(V, 0, 2, 4, 0)
-            widen(V, 0, 2, 4, 1)
+            lay_w(1, 0)
+            fetch_w(SCALAR, 1, 0)
+            turn_xh(last)
+            fetch_xh(last)
+            widen(VECTOR, 0, 2, NQ, range(2))
             quantise_xh(2)
-            widen(V, 0, 2, 4, 2)
-            widen(V, 0, 2, 4, 3)
+            widen(VECTOR, 0, 2, NQ, range(2, PACK))
             quantise_w(0)
-            quantise_xh(3)
+            quantise_xh(last)
+
             project(1)
             square(1)
             sum_squares(0)
             root(0)
-            lay_w(0, 1, 1)
-            fetch_w(0, 1, 1)
+            lay_w(1, 1)
+            fetch_w(SCALAR, 1, 1)
             interleave_w_on_vector(1, 1)
             quantise_inv(0)
-            widen(V, 1, 2, 3, 0)
+            widen(VECTOR, 1, 2, 3, range(1))
             quantise_w(1)
             interleave_w_on_vector(0, 2)
             project(2)
             square(2)
             sum_squares(1)
             root(1)
-            project(3)
+            project(last)
             sum_squares(2)
             quantise_inv(1)
-            widen(V, 1, 2, 3, 1)
-            widen(V, 1, 2, 3, 2)
-            square(3, 0, 1)
+            widen(VECTOR, 1, 2, 3, range(1, PACK - 1))
+
+            square(last, 0, 1)
             root(2)
             multiply(0, 0)
             multiply(0, 1)
-            square(3, 1, 3)
+            square(last, 1, M1)
             multiply(1, 0)
-            sum_squares(3)
+            sum_squares(last)
             multiply(1, 1)
-            widen(S, 1, 3, 4, 0)
-            widen(S, 1, 3, 4, 1)
-            widen(S, 1, 3, 4, 2)
-            root(3)
-            widen(V, 1, 2, 3, 3)
+            widen(SCALAR, 1, 3, NQ, range(PACK - 1))
+            root(last)
+
+            widen(VECTOR, 1, 2, 3, range(PACK - 1, PACK))
             quantise_inv(2)
             interleave_w_on_gpsimd(1, 2)
-            add_bias(0, 0)
-            finish(0, 0, 1)
-            multiply(2, 0)
-            add_bias(0, 1)
-            finish(0, 1, 2)
-            multiply(2, 1)
-            lay_w(0, 3, 0)
-            lay_w(0, 3, 1)
-            add_bias(1, 0)
-            add_bias(1, 1)
-            finish(1, 0, 2)
-            add_bias(2, 0)
-            add_bias(2, 1)
-            finish(2, 0, 2)
-            widen(V, 1, 3, 4, 3)
+            for q in range(2):
+                add_bias(0, q)
+                finish(0, q, q + 1)
+                multiply(2, q)
+            for b in range(2):
+                lay_w(3, b)
+            for i in range(1, last):
+                for q in range(2):
+                    add_bias(i, q)
+                finish(i, 0, 2)
+
+            widen(VECTOR, 1, 3, NQ, range(PACK - 1, PACK))
             quantise_w(2)
             interleave_w_on_gpsimd(1, 3)
-            quantise_inv(3)
-            multiply(3, 0)
-            multiply(3, 1)
-            multiply(0, 2)
-            multiply(1, 2)
-            fetch_w(0, 3, 0, V)
-            fetch_w(0, 3, 1, V)
-            add_bias(3, 0)
-            add_bias(3, 1)
-            finish(3, 0, 2)
-            multiply(2, 2, 0, 2, 1)
-            add_bias(0, 2)
-            finish(0, 2, 3)
-            multiply(3, 2, 0, 2, 1)
-            add_bias(1, 2)
-            finish(1, 2, 3)
-            quantise_w(3, 0, 1)
-            quantise_w(3, 1, 2)
+            quantise_inv(last)
+            for q in range(2):
+                multiply(last, q)
+            for i in range(2):
+                multiply(i, 2)
+            for b in range(2):
+                fetch_w(VECTOR, 3, b)
+            for q in range(2):
+                add_bias(last, q)
+            finish(last, 0, 2)
+            for i in range(2):
+                multiply(i + 2, 2, paced=True)
+                add_bias(i, 2)
+                finish(i, 2, 3)
+
+            for g in range(2):
+                quantise_w(3, g, g + 1)
             add_bias(2, 2)
             finish(2, 2, 3)
-            multiply(0, 3)
-            multiply(1, 3)
-            multiply(2, 3)
-            add_bias(3, 2)
-            finish(3, 2, 3)
-            multiply(3, 3)
-            add_bias(0, 3)
-            finish(0, 3, 4)
-            add_bias(1, 3)
-            finish(1, 3, 4)
-            add_bias(2, 3)
-            finish(2, 3, 4)
-            add_bias(3, 3)
-            finish(3, 3, 4)
+            for i in range(last):
+                multiply(i, 3)
+            add_bias(last, 2)
+            finish(last, 2, 3)
+            multiply(last, 3)
+            for i in tiles:
+                add_bias(i, 3)
+                finish(i, 3, NQ)

@@ -19,6 +19,7 @@ M1 = 3
 FF = 2048
 NT = 4
 BANK = 512
+PIECE = BANK // 2
 HALF = FF // 2
 NQ = FF // BANK
 UNITS = M1 + 1
@@ -66,6 +67,7 @@ def tile_equivariantfeedforward_pa_kernel(tc, h, x1, pre1, w1_0_bytes, w1_0_scal
         w_span = {}
         w_wide = {}
         w_words = {}
+        w_pairs = {}
         w_codes = [sbuf(f"w_codes{q}", [2 * BANK], U32) for q in range(NQ)]
         w_scales = [sbuf(f"w_scales{q}", [2 * BANK], U8) for q in range(NQ)]
         pre_words = sbuf("pre_words", [D, PACK], BF16)
@@ -117,53 +119,62 @@ def tile_equivariantfeedforward_pa_kernel(tc, h, x1, pre1, w1_0_bytes, w1_0_scal
                 else:
                     nc.scalar.activation(out=dst, in_=raw, func=ACT.Copy, scale=scale)
 
-        def words_tile(g, q):
-            key, buffer = ((g, q), q - g) if q == NQ - 1 else (q, q)
-            if key not in w_words:
-                w_words[key] = sbuf(f"w_words{buffer}", [2 * BANK * PACK], BF16)
-            return w_words[key]
-
         def words_of(g, q):
-            return words_tile(g, q)[:, g * BANK * PACK : (g + 1) * BANK * PACK]
+            if (g, q) not in w_words:
+                w_words[g, q] = sbuf(f"w_words{g}{q}", [BANK * PACK], BF16)
+            return w_words[g, q]
 
-        def interleave_w_on_vector(g, q):
-            nc.vector.tensor_copy(out=words_of(g, q).rearrange("p (c i t) -> p c t i", i=RUN, t=PACK),
-                                  in_=w_wide[g, q].rearrange("p t (c i) -> p c t i", i=RUN))
+        def pair_words(q):
+            both = sbuf(f"w_words{q}", [2 * BANK * PACK], BF16)
+            w_pairs[q] = both
+            for g in range(2):
+                w_words[g, q] = both[:, g * BANK * PACK : (g + 1) * BANK * PACK]
 
-        def interleave_w_on_gpsimd(g, q):
-            nc.gpsimd.tensor_scalar(out=words_of(g, q).rearrange("p (n t) -> p n t", t=PACK),
-                                    in0=w_wide[g, q].rearrange("p t n -> p n t"),
+        def interleave_w_on_vector(g, q, b0=0, b1=2):
+            c0, c1 = b0 * 2 * P, b1 * 2 * P
+            nc.vector.tensor_copy(out=words_of(g, q)[:, c0 * PACK : c1 * PACK].rearrange("p (c i t) -> p c t i", i=RUN, t=PACK),
+                                  in_=w_wide[g, q][:, :, c0:c1].rearrange("p t (c i) -> p c t i", i=RUN))
+
+        def interleave_w_on_gpsimd(g, q, b0=0, b1=2):
+            c0, c1 = b0 * 2 * P, b1 * 2 * P
+            nc.gpsimd.tensor_scalar(out=words_of(g, q)[:, c0 * PACK : c1 * PACK].rearrange("p (n t) -> p n t", t=PACK),
+                                    in0=w_wide[g, q][:, :, c0:c1].rearrange("p t n -> p n t"),
                                     scalar1=1.0, scalar2=0.0, op0=ALU.mult, op1=ALU.add)
 
-        def lay_w(q, b):
-            laid = take_bank(("w", q, b), [2, P * PACK], BF16)
+        def lay_w(g, q, b):
+            laid = take_bank(("w", g, q, b), [2, P * PACK], BF16)
             for j in range(2):
                 c0 = (2 * b + j) * P
                 nc.tensor.matmul(laid[:, j, :].rearrange("p (n t) -> p t n", t=PACK), lhsT=ident_bf16[:],
-                                 rhs=w_wide[0, q][:, :, c0 : c0 + P], start=True, stop=True)
+                                 rhs=w_wide[g, q][:, :, c0 : c0 + P], start=True, stop=True)
 
-        def fetch_w(engine, q, b):
+        def fetch_w(engine, g, q, b):
             width = 2 * P * PACK
-            copy_on(engine, words_of(0, q)[:, b * width : (b + 1) * width],
-                    empty_bank(("w", q, b))[:].rearrange("p j c -> p (j c)"))
+            copy_on(engine, words_of(g, q)[:, b * width : (b + 1) * width],
+                    empty_bank(("w", g, q, b))[:].rearrange("p j c -> p (j c)"))
 
-        def quantise_w(q, g0=0, g1=2):
-            c = slice(g0 * BANK, g1 * BANK)
-            quantise(w_codes[q][:, c], w_scales[q][:, c], words_tile(g0, q)[:, c.start * PACK : c.stop * PACK])
+        def quantise_w(q, g=None, b0=0, b1=2):
+            if g is None:
+                quantise(w_codes[q][:], w_scales[q][:], w_pairs[q][:])
+            else:
+                c = slice(g * BANK + b0 * PIECE, g * BANK + b1 * PIECE)
+                quantise(w_codes[q][:, c], w_scales[q][:, c], words_of(g, q)[:, b0 * PIECE * PACK : b1 * PIECE * PACK])
 
         def interleave_pre():
             dst = pre_words[:].rearrange("p (r c) t -> p c t r", r=PACK)
             src = pre_raw[:].rearrange("p t (c r) -> p c t r", r=PACK)
-            nc.vector.tensor_copy(out=dst[:, :, :, : PACK - 1], in_=src[:, :, :, : PACK - 1])
-            nc.scalar.copy(out=dst[:, :, :, PACK - 1 :], in_=src[:, :, :, PACK - 1 :])
+            nc.vector.tensor_copy(out=dst[:, :, :, :2], in_=src[:, :, :, :2])
+            nc.scalar.copy(out=dst[:, :, :, 2:], in_=src[:, :, :, 2:])
 
         def quantise_pre():
             quantise(pre_codes[:], pre_scales[:], pre_words[:].rearrange("p e t -> p (e t)"))
 
-        def split_x(i, engine=VECTOR):
+        def split_x(i, engine=VECTOR, between=None):
             dst = x_split[i][:].rearrange("p m (u c e) -> p m c u e", u=2, e=2)
             src = x_raw[i][:].rearrange("p (c u e m) -> p m c u e", u=2, e=2, m=M1)
             nc.vector.tensor_copy(out=dst[:, :2], in_=src[:, :2])
+            if between:
+                between()
             copy_on(engine, dst[:, 2], src[:, 2])
 
         def turn_xh(i):
@@ -213,23 +224,24 @@ def tile_equivariantfeedforward_pa_kernel(tc, h, x1, pre1, w1_0_bytes, w1_0_scal
         def quantise_inv(i):
             quantise(inv_codes[i][:], inv_scales[i][:], inv_words[i][:].rearrange("p n r -> p (n r)"))
 
-        def multiply(i, q, paced=False):
-            acc = take_bank(("acc", i, q), [BANK], F32, newest=paced)
+        def multiply(i, c0, width=BANK, passes=range(2), paced=False):
             sides = [(xh_codes[i][:, M1 * P :], xh_scales[i][:, M1 * P :]), (inv_codes[i][:], inv_scales[i][:])]
-            for g in range(2):
-                c = slice(g * BANK, (g + 1) * BANK)
+            q, first = divmod(c0, BANK)
+            for g in passes:
+                acc = take_bank(("acc", i, c0), [width], F32, newest=paced) if g == 0 else held["acc", i, c0][0]
+                c = slice(g * BANK + first, g * BANK + first + width)
                 nc.tensor.matmul_mx(out=acc[:], lhsT=sides[g][0].bitcast(FP8X4), lhsT_scale=sides[g][1],
                                     rhs=w_codes[q][:, c].bitcast(FP8X4), rhs_scale=w_scales[q][:, c],
                                     start=(g == 0), stop=(g == 1))
 
-        def add_bias(i, q):
-            nc.vector.tensor_tensor(out=rows[i][:, q * BANK : (q + 1) * BANK], in0=empty_bank(("acc", i, q))[:],
-                                    in1=bias[:, q * BANK : (q + 1) * BANK], op=ALU.add)
+        def add_bias(i, c0, width=BANK):
+            c = slice(c0, c0 + width)
+            nc.vector.tensor_tensor(out=rows[i][:, c], in0=empty_bank(("acc", i, c0))[:], in1=bias[:, c], op=ALU.add)
 
-        def finish(i, q0, q1):
-            part = rows[i][:, q0 * BANK : q1 * BANK]
+        def finish(i, c0, width=BANK):
+            part = rows[i][:, c0 : c0 + width]
             nc.scalar.activation(out=part, in_=part, func=ACT.Silu)
-            nc.sync.dma_start(out=out[i, :, q0 * BANK : q1 * BANK], in_=part)
+            nc.sync.dma_start(out=out[i, :, c0 : c0 + width], in_=part)
 
         last = NT - 1
         with tc.manual_schedule():
@@ -245,125 +257,125 @@ def tile_equivariantfeedforward_pa_kernel(tc, h, x1, pre1, w1_0_bytes, w1_0_scal
             load_w(0, 0, 2, PACK)
             load_h(0)
             load_pre()
+            load_x(1)
+            load_h(1)
             load_w(1, 0, 0, 2)
-            for i in range(1, last):
+            for i in range(2, NT):
                 load_x(i)
                 load_h(i)
             load_w(1, 0, 2, PACK)
-            load_x(last)
-            load_h(last)
             for g in range(2):
                 load_w(g, 1, 0, PACK)
             nc.sync.dma_start(out=bias[:], in_=b1_0.partition_broadcast(P))
+            for q in range(2):
+                pair_words(q)
 
             split_x(0, SCALAR)
             widen(SCALAR, 0, 0, 2, range(1))
             widen(VECTOR, 0, 0, 2, range(1, PACK))
             turn_xh(0)
             fetch_xh(0)
-            for b in range(2):
-                lay_w(0, b)
+            lay_w(0, 0, 0)
+            lay_w(0, 0, 1)
+            lay_w(0, 1, 0)
             interleave_pre()
             quantise_xh(0)
-            split_x(1)
-            quantise_pre()
-            widen(SCALAR, 1, 0, 2, range(2))
-            for b in range(2):
-                fetch_w(SCALAR, 0, b)
-
+            split_x(1, between=quantise_pre)
+            fetch_w(SCALAR, 0, 0, 0)
+            fetch_w(SCALAR, 0, 0, 1)
             turn_xh(1)
+            project(0)
+            widen(SCALAR, 1, 0, 2, range(1))
             fetch_xh(1)
             split_x(2)
-            project(0)
-            square(0)
-            widen(VECTOR, 1, 0, 2, range(2, PACK))
-            split_x(last)
-            quantise_xh(1)
-            interleave_w_on_vector(1, 0)
             turn_xh(2)
-            fetch_xh(2)
-            lay_w(1, 0)
-            fetch_w(SCALAR, 1, 0)
+            square(0)
+            widen(VECTOR, 1, 0, 2, range(1, 2))
+            split_x(last)
+            widen(VECTOR, 1, 0, 2, range(2, PACK))
+            quantise_xh(1)
             turn_xh(last)
-            fetch_xh(last)
-            widen(VECTOR, 0, 2, NQ, range(2))
-            quantise_xh(2)
-            widen(VECTOR, 0, 2, NQ, range(2, PACK))
-            quantise_w(0)
-            quantise_xh(last)
-
+            lay_w(0, 1, 1)
+            fetch_xh(2)
+            fetch_w(SCALAR, 0, 1, 0)
             project(1)
-            square(1)
+            fetch_xh(last)
             sum_squares(0)
-            root(0)
-            lay_w(1, 1)
-            fetch_w(SCALAR, 1, 1)
-            interleave_w_on_vector(1, 1)
-            quantise_inv(0)
-            widen(VECTOR, 1, 2, 3, range(1))
-            quantise_w(1)
-            interleave_w_on_vector(0, 2)
+            interleave_w_on_vector(1, 0)
+            quantise_xh(2)
+            square(1)
             project(2)
-            square(2)
+            widen(VECTOR, 0, 2, NQ, range(2))
+            quantise_xh(last)
+            fetch_w(SCALAR, 0, 1, 1)
             sum_squares(1)
-            root(1)
+            quantise_w(0)
+            square(2)
             project(last)
+            widen(VECTOR, 0, 2, NQ, range(2, PACK))
+            interleave_w_on_vector(1, 1)
+            root(0)
             sum_squares(2)
-            quantise_inv(1)
-            widen(VECTOR, 1, 2, 3, range(1, PACK - 1))
-
-            square(last, 0, 1)
-            root(2)
-            multiply(0, 0)
-            multiply(0, 1)
-            square(last, 1, M1)
-            multiply(1, 0)
+            square(last)
+            root(1)
+            for i in range(2):
+                multiply(i, 0, passes=range(1))
+            lay_w(0, 3, 0)
+            widen(VECTOR, 1, 2, 3, range(2))
+            quantise_inv(0)
+            quantise_w(1)
             sum_squares(last)
-            multiply(1, 1)
-            widen(SCALAR, 1, 3, NQ, range(PACK - 1))
+            multiply(0, 0, passes=range(1, 2))
+            root(2)
+            widen(SCALAR, 1, 3, NQ, range(2))
             root(last)
-
-            widen(VECTOR, 1, 2, 3, range(PACK - 1, PACK))
+            quantise_inv(1)
+            interleave_w_on_vector(0, 2)
+            widen(VECTOR, 1, 2, 3, range(2, PACK))
             quantise_inv(2)
             interleave_w_on_gpsimd(1, 2)
+            multiply(1, 0, passes=range(1, 2))
+            for i in range(2):
+                multiply(i, BANK)
+            for i in range(2):
+                add_bias(i, 0)
+                finish(i, 0)
+                multiply(2, i * BANK)
+            for i in range(2):
+                add_bias(i, BANK)
+            lay_w(0, 3, 1)
             for q in range(2):
-                add_bias(0, q)
-                finish(0, q, q + 1)
-                multiply(2, q)
-            for b in range(2):
-                lay_w(3, b)
-            for i in range(1, last):
-                for q in range(2):
-                    add_bias(i, q)
-                finish(i, 0, 2)
-
-            widen(VECTOR, 1, 3, NQ, range(PACK - 1, PACK))
-            quantise_w(2)
-            interleave_w_on_gpsimd(1, 3)
+                add_bias(2, q * BANK)
             quantise_inv(last)
             for q in range(2):
-                multiply(last, q)
+                multiply(last, q * BANK)
             for i in range(2):
-                multiply(i, 2)
+                finish(i, BANK)
+            widen(SCALAR, 1, 3, NQ, range(2, 3))
+            finish(2, 0, HALF)
             for b in range(2):
-                fetch_w(VECTOR, 3, b)
-            for q in range(2):
-                add_bias(last, q)
-            finish(last, 0, 2)
+                fetch_w(SCALAR, 0, 3, b)
+            quantise_w(2, 0)
+            quantise_w(2, 1, 0, 1)
+            widen(VECTOR, 1, 3, NQ, range(PACK - 1, PACK))
+            quantise_w(2, 1, 1, 2)
+            interleave_w_on_gpsimd(1, 3)
             for i in range(2):
-                multiply(i + 2, 2, paced=True)
-                add_bias(i, 2)
-                finish(i, 2, 3)
-
-            for g in range(2):
-                quantise_w(3, g, g + 1)
-            add_bias(2, 2)
-            finish(2, 2, 3)
-            for i in range(last):
-                multiply(i, 3)
-            add_bias(last, 2)
-            finish(last, 2, 3)
-            multiply(last, 3)
+                multiply(i, HALF)
+            for q in range(2):
+                add_bias(last, q * BANK)
+                finish(last, q * BANK)
             for i in tiles:
-                add_bias(i, 3)
-                finish(i, 3, NQ)
+                if i < 2:
+                    multiply(i + 2, HALF, paced=True)
+                add_bias(i, HALF)
+                finish(i, HALF)
+            for b in range(2):
+                for g in range(2):
+                    quantise_w(3, g, b, b + 1)
+            pieces = [(i, FF - BANK + b * PIECE) for b in range(2) for i in tiles]
+            for i, c0 in pieces:
+                multiply(i, c0, PIECE)
+            for i, c0 in pieces:
+                add_bias(i, c0, PIECE)
+                finish(i, c0, PIECE)

@@ -107,17 +107,20 @@ def tile_equivariantfeedforward_pa_kernel(tc, h, x1, pre1, w1_0_bytes, w1_0_scal
             nc.vector.quantize_mx(out=codes.bitcast(FP8X4), scales=scales, in_=words)
 
         def widen(engine, g, q0, q1, planes):
-            if (g, q0) not in w_wide:
-                w_span[g, q0] = sbuf(f"w_wide{g}{q0}", [PACK, (q1 - q0) * BANK], BF16)
-                for q in range(q0, q1):
-                    w_wide[g, q] = w_span[g, q0][:, :, (q - q0) * BANK : (q - q0 + 1) * BANK]
             for t in planes:
                 raw = w_bytes[g, q0 // 2, t][:, q0 % 2 * BANK : (q1 - q0 // 2 * 2) * BANK].bitcast(FP8)
-                dst, scale = w_span[g, q0][:, t, :], w_scale[:, g, t : t + 1]
+                span, first = w_span[g, q0]
+                dst, scale = span[:, t, first : first + (q1 - q0) * BANK], w_scale[:, g, t : t + 1]
                 if engine == VECTOR:
                     nc.vector.tensor_scalar(out=dst, in0=raw, scalar1=scale, scalar2=None, op0=ALU.mult)
                 else:
                     nc.scalar.activation(out=dst, in_=raw, func=ACT.Copy, scale=scale)
+
+        def wide_tile(g, q0, q1):
+            span = sbuf(f"w_wide{g}{q0}", [PACK, (q1 - q0) * BANK], BF16)
+            for q in range(q0, q1):
+                w_span[g, q] = (span, (q - q0) * BANK)
+                w_wide[g, q] = span[:, :, (q - q0) * BANK : (q - q0 + 1) * BANK]
 
         def words_of(g, q):
             if (g, q) not in w_words:
@@ -163,8 +166,8 @@ def tile_equivariantfeedforward_pa_kernel(tc, h, x1, pre1, w1_0_bytes, w1_0_scal
         def interleave_pre():
             dst = pre_words[:].rearrange("p (r c) t -> p c t r", r=PACK)
             src = pre_raw[:].rearrange("p t (c r) -> p c t r", r=PACK)
-            nc.vector.tensor_copy(out=dst[:, :, :, :2], in_=src[:, :, :, :2])
-            nc.scalar.copy(out=dst[:, :, :, 2:], in_=src[:, :, :, 2:])
+            nc.vector.tensor_copy(out=dst[:, :, :, : PACK - 1], in_=src[:, :, :, : PACK - 1])
+            nc.scalar.copy(out=dst[:, :, :, PACK - 1 :], in_=src[:, :, :, PACK - 1 :])
 
         def quantise_pre():
             quantise(pre_codes[:], pre_scales[:], pre_words[:].rearrange("p e t -> p (e t)"))
@@ -189,17 +192,17 @@ def tile_equivariantfeedforward_pa_kernel(tc, h, x1, pre1, w1_0_bytes, w1_0_scal
                             words = h_raw[i][:].bitcast(F32)[:, u : D // 2 : 2]
                         nc.tensor.transpose(turned[:, j, u, :], words, ident_f32[:])
 
-        def fetch_xh(i):
+        def fetch_xh(i, engines=(SCALAR, SCALAR)):
             for b in range(2):
                 dst = xh_words[i][:, b * 2 * P * PACK : (b + 1) * 2 * P * PACK].bitcast(F32)
-                nc.scalar.copy(out=dst.rearrange("p (j n a u) -> p j n u a", j=2, a=2, u=2),
-                               in_=empty_bank(("xh", i, b))[:].rearrange("p j u (n a) -> p j n u a", a=2))
+                copy_on(engines[b], dst.rearrange("p (j n a u) -> p j n u a", j=2, a=2, u=2),
+                        empty_bank(("xh", i, b))[:].rearrange("p j u (n a) -> p j n u a", a=2))
 
         def quantise_xh(i):
             quantise(xh_codes[i][:], xh_scales[i][:], xh_words[i][:])
 
-        def project(i):
-            for m in range(M1):
+        def project(i, m0=0, m1=M1):
+            for m in range(m0, m1):
                 pm = take_bank(("pm", i, m), [BANK], F32)
                 c = slice(m * P, (m + 1) * P)
                 nc.tensor.matmul_mx(out=pm[:], lhsT=xh_codes[i][:, c].bitcast(FP8X4), lhsT_scale=xh_scales[i][:, c],
@@ -267,94 +270,110 @@ def tile_equivariantfeedforward_pa_kernel(tc, h, x1, pre1, w1_0_bytes, w1_0_scal
             for g in range(2):
                 load_w(g, 1, 0, PACK)
             nc.sync.dma_start(out=bias[:], in_=b1_0.partition_broadcast(P))
-            for q in range(2):
-                pair_words(q)
+            for g, q0, q1 in ((0, 0, 2), (1, 0, 2), (0, 2, NQ), (1, 2, 3), (1, 3, NQ)):
+                wide_tile(g, q0, q1)
+            pair_words(1)
 
             split_x(0, SCALAR)
-            widen(SCALAR, 0, 0, 2, range(1))
-            widen(VECTOR, 0, 0, 2, range(1, PACK))
+            widen(VECTOR, 0, 0, 2, range(1))
+            widen(SCALAR, 0, 0, 2, range(1, 2))
+            widen(VECTOR, 0, 0, 1, range(2, PACK))
+            widen(SCALAR, 0, 1, 2, range(2, 3))
+            widen(VECTOR, 0, 1, 2, range(3, PACK))
             turn_xh(0)
             fetch_xh(0)
-            lay_w(0, 0, 0)
-            lay_w(0, 0, 1)
-            lay_w(0, 1, 0)
+            for q in range(2):
+                lay_w(0, q, 0)
+            interleave_w_on_vector(0, 0, 1, 2)
             interleave_pre()
+            split_x(1, SCALAR)
             quantise_xh(0)
-            split_x(1, between=quantise_pre)
+            quantise_pre()
             fetch_w(SCALAR, 0, 0, 0)
-            fetch_w(SCALAR, 0, 0, 1)
+            widen(SCALAR, 1, 0, 1, range(1))
+            fetch_w(SCALAR, 0, 1, 0)
             turn_xh(1)
-            project(0)
-            widen(SCALAR, 1, 0, 2, range(1))
+            project(0, 0, 1)
+            lay_w(0, 1, 1)
+            project(0, 1, M1)
             fetch_xh(1)
+            widen(VECTOR, 1, 1, 2, range(1))
+            widen(VECTOR, 1, 0, 2, range(1, 2))
             split_x(2)
             turn_xh(2)
-            square(0)
-            widen(VECTOR, 1, 0, 2, range(1, 2))
-            split_x(last)
-            widen(VECTOR, 1, 0, 2, range(2, PACK))
-            quantise_xh(1)
-            turn_xh(last)
-            lay_w(0, 1, 1)
-            fetch_xh(2)
-            fetch_w(SCALAR, 0, 1, 0)
-            project(1)
-            fetch_xh(last)
-            sum_squares(0)
-            interleave_w_on_vector(1, 0)
-            quantise_xh(2)
-            square(1)
-            project(2)
-            widen(VECTOR, 0, 2, NQ, range(2))
-            quantise_xh(last)
+            square(0, 0, 1)
             fetch_w(SCALAR, 0, 1, 1)
-            sum_squares(1)
-            quantise_w(0)
-            square(2)
-            project(last)
-            widen(VECTOR, 0, 2, NQ, range(2, PACK))
+            square(0, 1, 2)
+            fetch_xh(2)
+            square(0, 2, M1)
+            quantise_w(0, 0)
+            split_x(last, between=lambda: quantise_xh(1))
+            project(1, 0, 2)
+            turn_xh(last)
+            project(1, 2, M1)
+            widen(VECTOR, 1, 0, 2, range(2, PACK))
+            square(1, 0, 1)
+            fetch_xh(last)
+            quantise_xh(2)
+            interleave_w_on_vector(1, 0, 0, 1)
+            widen(VECTOR, 0, 2, NQ, range(1))
+            sum_squares(0)
+            square(1, 1, M1)
+            project(2, 0, 2)
+            lay_w(1, 0, 1)
+            project(2, 2, M1)
             interleave_w_on_vector(1, 1)
+            quantise_xh(last)
+            widen(SCALAR, 1, 3, NQ, range(1))
+            sum_squares(1)
             root(0)
+            project(last)
+            square(2)
+            quantise_w(1)
+            widen(VECTOR, 0, 2, NQ, range(1, 3))
+            fetch_w(VECTOR, 1, 0, 1)
+            quantise_inv(0)
+            widen(VECTOR, 0, 2, NQ, range(3, PACK))
+            quantise_w(0, 1)
             sum_squares(2)
-            square(last)
             root(1)
             for i in range(2):
                 multiply(i, 0, passes=range(1))
-            lay_w(0, 3, 0)
-            widen(VECTOR, 1, 2, 3, range(2))
-            quantise_inv(0)
-            quantise_w(1)
-            sum_squares(last)
+            square(last)
             multiply(0, 0, passes=range(1, 2))
             root(2)
-            widen(SCALAR, 1, 3, NQ, range(2))
+            sum_squares(last)
+            widen(SCALAR, 1, 3, NQ, range(1, 3))
             root(last)
+            widen(VECTOR, 1, 2, 3, range(PACK - 1))
             quantise_inv(1)
-            interleave_w_on_vector(0, 2)
-            widen(VECTOR, 1, 2, 3, range(2, PACK))
+            interleave_w_on_vector(0, 2, 0, 1)
             quantise_inv(2)
+            widen(VECTOR, 1, 2, 3, range(PACK - 1, PACK))
+            interleave_w_on_vector(0, 2, 1, 2)
             interleave_w_on_gpsimd(1, 2)
             multiply(1, 0, passes=range(1, 2))
             for i in range(2):
                 multiply(i, BANK)
-            for i in range(2):
-                add_bias(i, 0)
-                finish(i, 0)
-                multiply(2, i * BANK)
+            add_bias(0, 0)
+            finish(0, 0)
+            multiply(2, 0)
+            lay_w(0, 3, 1)
+            add_bias(1, 0)
+            finish(1, 0)
             for i in range(2):
                 add_bias(i, BANK)
-            lay_w(0, 3, 1)
-            for q in range(2):
-                add_bias(2, q * BANK)
+            finish(0, BANK)
+            finish(1, BANK)
+            multiply(2, BANK)
+            lay_w(0, 3, 0)
+            add_bias(2, 0)
+            finish(2, 0)
+            fetch_w(VECTOR, 0, 3, 1)
             quantise_inv(last)
             for q in range(2):
                 multiply(last, q * BANK)
-            for i in range(2):
-                finish(i, BANK)
-            widen(SCALAR, 1, 3, NQ, range(2, 3))
-            finish(2, 0, HALF)
-            for b in range(2):
-                fetch_w(SCALAR, 0, 3, b)
+            fetch_w(SCALAR, 0, 3, 0)
             quantise_w(2, 0)
             quantise_w(2, 1, 0, 1)
             widen(VECTOR, 1, 3, NQ, range(PACK - 1, PACK))
@@ -362,20 +381,27 @@ def tile_equivariantfeedforward_pa_kernel(tc, h, x1, pre1, w1_0_bytes, w1_0_scal
             interleave_w_on_gpsimd(1, 3)
             for i in range(2):
                 multiply(i, HALF)
-            for q in range(2):
-                add_bias(last, q * BANK)
-                finish(last, q * BANK)
-            for i in tiles:
+            for i, c0 in ((2, BANK), (last, 0), (last, BANK)):
+                add_bias(i, c0)
+                finish(i, c0)
+            for i in range(last):
                 if i < 2:
                     multiply(i + 2, HALF, paced=True)
                 add_bias(i, HALF)
                 finish(i, HALF)
-            for b in range(2):
-                for g in range(2):
-                    quantise_w(3, g, b, b + 1)
             pieces = [(i, FF - BANK + b * PIECE) for b in range(2) for i in tiles]
-            for i, c0 in pieces:
+            for g in range(2):
+                quantise_w(3, g, 0, 1)
+            add_bias(last, HALF)
+            finish(last, HALF)
+            quantise_w(3, 0, 1, 2)
+            for i, c0 in pieces[:NT]:
                 multiply(i, c0, PIECE)
-            for i, c0 in pieces:
+            add_bias(*pieces[0], PIECE)
+            finish(*pieces[0], PIECE)
+            quantise_w(3, 1, 1, 2)
+            for i, c0 in pieces[NT:]:
+                multiply(i, c0, PIECE)
+            for i, c0 in pieces[1:]:
                 add_bias(i, c0, PIECE)
                 finish(i, c0, PIECE)

@@ -67,6 +67,7 @@ def tile_equivariantfeedforward_pa_kernel(tc, h, x1, pre1, w1_0_bytes, w1_0_scal
         w_span = {}
         w_wide = {}
         w_words = {}
+        piece_words = {}
         w_pairs = {}
         w_codes = [sbuf(f"w_codes{q}", [2 * BANK], U32) for q in range(NQ)]
         w_scales = [sbuf(f"w_scales{q}", [2 * BANK], U8) for q in range(NQ)]
@@ -77,9 +78,9 @@ def tile_equivariantfeedforward_pa_kernel(tc, h, x1, pre1, w1_0_bytes, w1_0_scal
         xh_codes = [sbuf(f"xh_codes{i}", [UNITS * P], U32) for i in tiles]
         xh_scales = [sbuf(f"xh_scales{i}", [UNITS * P], U8) for i in tiles]
         squares = {(i, m): sbuf(f"squares{i}{m}", [PACK, P], F32) for i in tiles for m in range(M1)}
-        inv_words = [sbuf(f"inv_words{i}", [P, PACK], BF16) for i in tiles]
-        inv_codes = [sbuf(f"inv_codes{i}", [P], U32) for i in tiles]
-        inv_scales = [sbuf(f"inv_scales{i}", [P], U8) for i in tiles]
+        inv_words = sbuf("inv_words", [NT * P * PACK], BF16)
+        inv_codes = sbuf("inv_codes", [NT * P], U32)
+        inv_scales = sbuf("inv_scales", [NT * P], U8)
         rows = [sbuf(f"rows{i}", [FF], F32) for i in tiles]
 
         def copy_on(engine, dst, src):
@@ -122,6 +123,14 @@ def tile_equivariantfeedforward_pa_kernel(tc, h, x1, pre1, w1_0_bytes, w1_0_scal
                 w_span[g, q] = (span, (q - q0) * BANK)
                 w_wide[g, q] = span[:, :, (q - q0) * BANK : (q - q0 + 1) * BANK]
 
+        def wide_late():
+            span = sbuf("w_wide_late", [PACK, 2, HALF], BF16)
+            for g in range(2):
+                for q in range(2, NQ):
+                    w_span[g, q] = (span[:, :, g, :], (q - 2) * BANK)
+                    w_wide[g, q] = span[:, :, g, (q - 2) * BANK : (q - 1) * BANK]
+            return span
+
         def words_of(g, q):
             if (g, q) not in w_words:
                 w_words[g, q] = sbuf(f"w_words{g}{q}", [BANK * PACK], BF16)
@@ -153,7 +162,8 @@ def tile_equivariantfeedforward_pa_kernel(tc, h, x1, pre1, w1_0_bytes, w1_0_scal
 
         def fetch_w(engine, g, q, b):
             width = 2 * P * PACK
-            copy_on(engine, words_of(g, q)[:, b * width : (b + 1) * width],
+            dst = piece_words[b][:, g * width : (g + 1) * width] if q == NQ - 1 else words_of(g, q)[:, b * width : (b + 1) * width]
+            copy_on(engine, dst,
                     empty_bank(("w", g, q, b))[:].rearrange("p j c -> p (j c)"))
 
         def quantise_w(q, g=None, b0=0, b1=2):
@@ -162,6 +172,15 @@ def tile_equivariantfeedforward_pa_kernel(tc, h, x1, pre1, w1_0_bytes, w1_0_scal
             else:
                 c = slice(g * BANK + b0 * PIECE, g * BANK + b1 * PIECE)
                 quantise(w_codes[q][:, c], w_scales[q][:, c], words_of(g, q)[:, b0 * PIECE * PACK : b1 * PIECE * PACK])
+
+        def quantise_piece(b):
+            c = slice(b * BANK, (b + 1) * BANK)
+            quantise(w_codes[NQ - 1][:, c], w_scales[NQ - 1][:, c], piece_words[b][:])
+
+        def interleave_last_piece(span):
+            nc.gpsimd.tensor_scalar(out=piece_words[1][:].rearrange("p (g n t) -> p g n t", g=2, t=PACK),
+                                    in0=span[:, :, :, HALF - PIECE :].rearrange("p t g n -> p g n t"),
+                                    scalar1=1.0, scalar2=0.0, op0=ALU.mult, op1=ALU.add)
 
         def interleave_pre():
             dst = pre_words[:].rearrange("p (r c) t -> p c t r", r=PACK)
@@ -221,18 +240,20 @@ def tile_equivariantfeedforward_pa_kernel(tc, h, x1, pre1, w1_0_bytes, w1_0_scal
                                      start=(m, r) == (0, 0), stop=(m, r) == (M1 - 1, PACK - 1), is_transpose=True)
 
         def root(i):
-            nc.scalar.activation(out=inv_words[i][:].rearrange("p (n a) r -> p n r a", a=2),
+            nc.scalar.activation(out=inv_words[:, i * D : (i + 1) * D].rearrange("p (n a r) -> p n r a", a=2, r=PACK),
                                  in_=empty_bank(("sum", i))[:].rearrange("p r (n a) -> p n r a", a=2), func=ACT.Sqrt)
 
-        def quantise_inv(i):
-            quantise(inv_codes[i][:], inv_scales[i][:], inv_words[i][:].rearrange("p n r -> p (n r)"))
+        def quantise_inv(i, count=1):
+            c = slice(i * P, (i + count) * P)
+            quantise(inv_codes[:, c], inv_scales[:, c], inv_words[:, i * D : (i + count) * D])
 
         def multiply(i, c0, width=BANK, passes=range(2), paced=False):
-            sides = [(xh_codes[i][:, M1 * P :], xh_scales[i][:, M1 * P :]), (inv_codes[i][:], inv_scales[i][:])]
+            sides = [(xh_codes[i][:, M1 * P :], xh_scales[i][:, M1 * P :]), (inv_codes[:, i * P : (i + 1) * P], inv_scales[:, i * P : (i + 1) * P])]
             q, first = divmod(c0, BANK)
             for g in passes:
                 acc = take_bank(("acc", i, c0), [width], F32, newest=paced) if g == 0 else held["acc", i, c0][0]
-                c = slice(g * BANK + first, g * BANK + first + width)
+                start = 2 * first + g * width if width == PIECE else g * BANK
+                c = slice(start, start + width)
                 nc.tensor.matmul_mx(out=acc[:], lhsT=sides[g][0].bitcast(FP8X4), lhsT_scale=sides[g][1],
                                     rhs=w_codes[q][:, c].bitcast(FP8X4), rhs_scale=w_scales[q][:, c],
                                     start=(g == 0), stop=(g == 1))
@@ -270,8 +291,10 @@ def tile_equivariantfeedforward_pa_kernel(tc, h, x1, pre1, w1_0_bytes, w1_0_scal
             for g in range(2):
                 load_w(g, 1, 0, PACK)
             nc.sync.dma_start(out=bias[:], in_=b1_0.partition_broadcast(P))
-            for g, q0, q1 in ((0, 0, 2), (1, 0, 2), (0, 2, NQ), (1, 2, 3), (1, 3, NQ)):
-                wide_tile(g, q0, q1)
+            for g in range(2):
+                wide_tile(g, 0, 2)
+            late = wide_late()
+            piece_words[0] = sbuf("piece_words", [BANK * PACK], BF16)
             pair_words(1)
 
             split_x(0, SCALAR)
@@ -324,15 +347,13 @@ def tile_equivariantfeedforward_pa_kernel(tc, h, x1, pre1, w1_0_bytes, w1_0_scal
             project(2, 2, M1)
             interleave_w_on_vector(1, 1)
             quantise_xh(last)
-            widen(SCALAR, 1, 3, NQ, range(1))
             sum_squares(1)
             root(0)
             project(last)
             square(2)
             quantise_w(1)
             widen(VECTOR, 0, 2, NQ, range(1, 3))
-            fetch_w(VECTOR, 1, 0, 1)
-            quantise_inv(0)
+            fetch_w(SCALAR, 1, 0, 1)
             widen(VECTOR, 0, 2, NQ, range(3, PACK))
             quantise_w(0, 1)
             sum_squares(2)
@@ -340,16 +361,18 @@ def tile_equivariantfeedforward_pa_kernel(tc, h, x1, pre1, w1_0_bytes, w1_0_scal
             for i in range(2):
                 multiply(i, 0, passes=range(1))
             square(last)
+            quantise_inv(0, 2)
             multiply(0, 0, passes=range(1, 2))
             root(2)
             sum_squares(last)
             widen(SCALAR, 1, 3, NQ, range(1, 3))
             root(last)
-            widen(VECTOR, 1, 2, 3, range(PACK - 1))
-            quantise_inv(1)
+            widen(VECTOR, 1, 2, NQ, range(1))
+            widen(VECTOR, 1, 2, 3, range(1, PACK - 1))
+
             interleave_w_on_vector(0, 2, 0, 1)
             quantise_inv(2)
-            widen(VECTOR, 1, 2, 3, range(PACK - 1, PACK))
+            widen(VECTOR, 1, 2, NQ, range(PACK - 1, PACK))
             interleave_w_on_vector(0, 2, 1, 2)
             interleave_w_on_gpsimd(1, 2)
             multiply(1, 0, passes=range(1, 2))
@@ -358,7 +381,7 @@ def tile_equivariantfeedforward_pa_kernel(tc, h, x1, pre1, w1_0_bytes, w1_0_scal
             add_bias(0, 0)
             finish(0, 0)
             multiply(2, 0)
-            lay_w(0, 3, 1)
+            lay_w(0, 3, 0)
             add_bias(1, 0)
             finish(1, 0)
             for i in range(2):
@@ -366,19 +389,18 @@ def tile_equivariantfeedforward_pa_kernel(tc, h, x1, pre1, w1_0_bytes, w1_0_scal
             finish(0, BANK)
             finish(1, BANK)
             multiply(2, BANK)
-            lay_w(0, 3, 0)
+            lay_w(1, 3, 0)
             add_bias(2, 0)
             finish(2, 0)
-            fetch_w(VECTOR, 0, 3, 1)
+            fetch_w(VECTOR, 0, 3, 0)
             quantise_inv(last)
             for q in range(2):
                 multiply(last, q * BANK)
-            fetch_w(SCALAR, 0, 3, 0)
+            fetch_w(SCALAR, 1, 3, 0)
             quantise_w(2, 0)
-            quantise_w(2, 1, 0, 1)
-            widen(VECTOR, 1, 3, NQ, range(PACK - 1, PACK))
-            quantise_w(2, 1, 1, 2)
-            interleave_w_on_gpsimd(1, 3)
+            quantise_w(2, 1)
+            piece_words[1] = sbuf("w_words02", [BANK * PACK], BF16)
+            interleave_last_piece(late)
             for i in range(2):
                 multiply(i, HALF)
             for i, c0 in ((2, BANK), (last, 0), (last, BANK)):
@@ -390,18 +412,12 @@ def tile_equivariantfeedforward_pa_kernel(tc, h, x1, pre1, w1_0_bytes, w1_0_scal
                 add_bias(i, HALF)
                 finish(i, HALF)
             pieces = [(i, FF - BANK + b * PIECE) for b in range(2) for i in tiles]
-            for g in range(2):
-                quantise_w(3, g, 0, 1)
+            quantise_piece(0)
             add_bias(last, HALF)
             finish(last, HALF)
-            quantise_w(3, 0, 1, 2)
-            for i, c0 in pieces[:NT]:
+            quantise_piece(1)
+            for i, c0 in pieces:
                 multiply(i, c0, PIECE)
-            add_bias(*pieces[0], PIECE)
-            finish(*pieces[0], PIECE)
-            quantise_w(3, 1, 1, 2)
-            for i, c0 in pieces[NT:]:
-                multiply(i, c0, PIECE)
-            for i, c0 in pieces[1:]:
+            for i, c0 in pieces:
                 add_bias(i, c0, PIECE)
                 finish(i, c0, PIECE)

@@ -163,8 +163,7 @@ def tile_equivariantfeedforward_pa_kernel(tc, h, x1, pre1, w1_0_bytes, w1_0_scal
         def fetch_w(engine, g, q, b):
             width = 2 * P * PACK
             dst = piece_words[b][:, g * width : (g + 1) * width] if q == NQ - 1 else words_of(g, q)[:, b * width : (b + 1) * width]
-            copy_on(engine, dst,
-                    empty_bank(("w", g, q, b))[:].rearrange("p j c -> p (j c)"))
+            copy_on(engine, dst.bitcast(F32), empty_bank(("w", g, q, b))[:].rearrange("p j c -> p (j c)").bitcast(F32))
 
         def quantise_w(q, g=None, b0=0, b1=2):
             if g is None:
@@ -173,9 +172,9 @@ def tile_equivariantfeedforward_pa_kernel(tc, h, x1, pre1, w1_0_bytes, w1_0_scal
                 c = slice(g * BANK + b0 * PIECE, g * BANK + b1 * PIECE)
                 quantise(w_codes[q][:, c], w_scales[q][:, c], words_of(g, q)[:, b0 * PIECE * PACK : b1 * PIECE * PACK])
 
-        def quantise_piece(b):
-            c = slice(b * BANK, (b + 1) * BANK)
-            quantise(w_codes[NQ - 1][:, c], w_scales[NQ - 1][:, c], piece_words[b][:])
+        def quantise_piece(b, g0=0, g1=2):
+            c = slice(b * BANK + g0 * PIECE, b * BANK + g1 * PIECE)
+            quantise(w_codes[NQ - 1][:, c], w_scales[NQ - 1][:, c], piece_words[b][:, g0 * PIECE * PACK : g1 * PIECE * PACK])
 
         def interleave_last_piece(span):
             nc.gpsimd.tensor_scalar(out=piece_words[1][:].rearrange("p (g n t) -> p g n t", g=2, t=PACK),
@@ -286,6 +285,7 @@ def tile_equivariantfeedforward_pa_kernel(tc, h, x1, pre1, w1_0_bytes, w1_0_scal
             load_w(1, 0, 0, 2)
             for i in range(2, NT):
                 load_x(i)
+            for i in range(2, NT):
                 load_h(i)
             load_w(1, 0, 2, PACK)
             for g in range(2):
@@ -293,9 +293,9 @@ def tile_equivariantfeedforward_pa_kernel(tc, h, x1, pre1, w1_0_bytes, w1_0_scal
             nc.sync.dma_start(out=bias[:], in_=b1_0.partition_broadcast(P))
             for g in range(2):
                 wide_tile(g, 0, 2)
+                pair_words(g)
             late = wide_late()
             piece_words[0] = sbuf("piece_words", [BANK * PACK], BF16)
-            pair_words(1)
 
             split_x(0, SCALAR)
             widen(VECTOR, 0, 0, 2, range(1))
@@ -318,105 +318,111 @@ def tile_equivariantfeedforward_pa_kernel(tc, h, x1, pre1, w1_0_bytes, w1_0_scal
             turn_xh(1)
             project(0, 0, 1)
             lay_w(0, 1, 1)
-            project(0, 1, M1)
+            project(0, 1, 2)
             fetch_xh(1)
-            widen(VECTOR, 1, 1, 2, range(1))
-            widen(VECTOR, 1, 0, 2, range(1, 2))
             split_x(2)
+            split_x(last)
+            widen(VECTOR, 1, 0, 2, range(1, 2))
+            widen(VECTOR, 1, 1, 2, range(1))
             turn_xh(2)
+            project(0, 2, M1)
             square(0, 0, 1)
             fetch_w(SCALAR, 0, 1, 1)
             square(0, 1, 2)
             fetch_xh(2)
-            square(0, 2, M1)
-            quantise_w(0, 0)
-            split_x(last, between=lambda: quantise_xh(1))
-            project(1, 0, 2)
+            quantise_xh(1)
             turn_xh(last)
-            project(1, 2, M1)
             widen(VECTOR, 1, 0, 2, range(2, PACK))
-            square(1, 0, 1)
+            project(1, 0, 1)
             fetch_xh(last)
-            quantise_xh(2)
-            interleave_w_on_vector(1, 0, 0, 1)
+            square(0, 2, M1)
+            lay_w(1, 0, 1)
+            project(1, 1, M1)
             widen(VECTOR, 0, 2, NQ, range(1))
+            interleave_w_on_vector(1, 0, 0, 1)
+            quantise_xh(2)
+            square(1, 0, 1)
+            fetch_w(SCALAR, 1, 0, 1)
             sum_squares(0)
             square(1, 1, M1)
-            project(2, 0, 2)
-            lay_w(1, 0, 1)
-            project(2, 2, M1)
+            project(2)
             interleave_w_on_vector(1, 1)
             quantise_xh(last)
             sum_squares(1)
-            root(0)
             project(last)
             square(2)
-            quantise_w(1)
-            widen(VECTOR, 0, 2, NQ, range(1, 3))
-            fetch_w(SCALAR, 1, 0, 1)
+            widen(VECTOR, 0, 2, NQ, range(1, 2))
+            quantise_w(0)
             widen(VECTOR, 0, 2, NQ, range(3, PACK))
-            quantise_w(0, 1)
+            quantise_w(1)
+            widen(VECTOR, 0, 2, NQ, range(2, 3))
+            widen(VECTOR, 1, 2, 3, range(2, 3))
+            widen(VECTOR, 1, 2, NQ, range(3, PACK))
             sum_squares(2)
+            root(0)
+            square(last, 0, 1)
             root(1)
             for i in range(2):
                 multiply(i, 0, passes=range(1))
-            square(last)
-            quantise_inv(0, 2)
-            multiply(0, 0, passes=range(1, 2))
+            square(last, 1, M1)
+            for i in range(2):
+                multiply(i, BANK, passes=range(1))
             root(2)
             sum_squares(last)
-            widen(SCALAR, 1, 3, NQ, range(1, 3))
+            quantise_inv(0, 2)
+            widen(SCALAR, 1, 2, NQ, range(1, 2))
+            widen(SCALAR, 1, 3, NQ, range(2, 3))
             root(last)
+            interleave_w_on_vector(0, 2)
             widen(VECTOR, 1, 2, NQ, range(1))
-            widen(VECTOR, 1, 2, 3, range(1, PACK - 1))
-
-            interleave_w_on_vector(0, 2, 0, 1)
             quantise_inv(2)
-            widen(VECTOR, 1, 2, NQ, range(PACK - 1, PACK))
-            interleave_w_on_vector(0, 2, 1, 2)
             interleave_w_on_gpsimd(1, 2)
-            multiply(1, 0, passes=range(1, 2))
             for i in range(2):
-                multiply(i, BANK)
-            add_bias(0, 0)
-            finish(0, 0)
+                for q in range(2):
+                    multiply(i, q * BANK, passes=range(1, 2))
             multiply(2, 0)
+            add_bias(0, 0)
             lay_w(0, 3, 0)
-            add_bias(1, 0)
-            finish(1, 0)
-            for i in range(2):
-                add_bias(i, BANK)
-            finish(0, BANK)
-            finish(1, BANK)
-            multiply(2, BANK)
+            add_bias(0, BANK)
+            finish(0, 0, HALF)
+            for q in range(2):
+                add_bias(1, q * BANK)
+            finish(1, 0, HALF)
             lay_w(1, 3, 0)
             add_bias(2, 0)
             finish(2, 0)
+            multiply(2, BANK)
             fetch_w(VECTOR, 0, 3, 0)
             quantise_inv(last)
             for q in range(2):
                 multiply(last, q * BANK)
             fetch_w(SCALAR, 1, 3, 0)
+            quantise_piece(0, 0, 1)
             quantise_w(2, 0)
             quantise_w(2, 1)
             piece_words[1] = sbuf("w_words02", [BANK * PACK], BF16)
             interleave_last_piece(late)
+            pieces = [(i, FF - BANK + b * PIECE) for b in range(2) for i in tiles]
             for i in range(2):
                 multiply(i, HALF)
-            for i, c0 in ((2, BANK), (last, 0), (last, BANK)):
-                add_bias(i, c0)
-                finish(i, c0)
+            add_bias(2, BANK)
+            finish(2, BANK)
+            for q in range(2):
+                add_bias(last, q * BANK)
+                finish(last, q * BANK)
+            for i in range(2, NT):
+                multiply(i, HALF)
             for i in range(last):
-                if i < 2:
-                    multiply(i + 2, HALF, paced=True)
                 add_bias(i, HALF)
                 finish(i, HALF)
-            pieces = [(i, FF - BANK + b * PIECE) for b in range(2) for i in tiles]
-            quantise_piece(0)
+                multiply(*pieces[i], PIECE, passes=range(1), paced=True)
+            quantise_piece(0, 1, 2)
             add_bias(last, HALF)
             finish(last, HALF)
             quantise_piece(1)
-            for i, c0 in pieces:
+            for i, c0 in pieces[:last]:
+                multiply(i, c0, PIECE, passes=range(1, 2))
+            for i, c0 in pieces[last:]:
                 multiply(i, c0, PIECE)
             for i, c0 in pieces:
                 add_bias(i, c0, PIECE)

@@ -24,6 +24,7 @@ HALF = FF // 2
 NQ = FF // BANK
 UNITS = M1 + 1
 PSUM_BANKS = 8
+DMA_ALIGN = 256
 RUN = 8
 VECTOR, SCALAR = "vector", "scalar"
 
@@ -36,8 +37,11 @@ def tile_equivariantfeedforward_pa_kernel(tc, h, x1, pre1, w1_0_bytes, w1_0_scal
         keep = ctx.enter_context(tc.tile_pool(name="keep", bufs=1))
         psum = ctx.enter_context(tc.psum_pool(name="psum", bufs=1))
 
-        def sbuf(name, shape, dtype):
-            return keep.tile([P] + shape, dtype, name=name, align_bytes=64)
+        def sbuf(name, shape, dtype, align=64):
+            return keep.tile([P] + shape, dtype, name=name, align_bytes=align)
+
+        def dma_tile(name, shape, dtype):
+            return sbuf(name, shape, dtype, DMA_ALIGN)
 
         free_banks = list(range(PSUM_BANKS))
         held = {}
@@ -56,12 +60,12 @@ def tile_equivariantfeedforward_pa_kernel(tc, h, x1, pre1, w1_0_bytes, w1_0_scal
         tiles = range(NT)
         w_rows = w1_0_bytes.rearrange("(g p t) n -> g p t n", p=P, t=PACK)
         w_bytes = {}
-        x_raw = [sbuf(f"x_raw{i}", [D * M1], BF16) for i in tiles]
-        h_raw = [sbuf(f"h_raw{i}", [D], BF16) for i in tiles]
+        x_raw = [dma_tile(f"x_raw{i}", [D * M1], BF16) for i in tiles]
+        h_raw = [dma_tile(f"h_raw{i}", [D], BF16) for i in tiles]
         x_split = [sbuf(f"x_split{i}", [M1, D], BF16) for i in tiles]
-        pre_raw = sbuf("pre_raw", [PACK, D], BF16)
+        pre_raw = dma_tile("pre_raw", [PACK, D], BF16)
         w_scale = sbuf("w_scale", [2, PACK], F32)
-        bias = sbuf("bias", [FF], BF16)
+        bias = dma_tile("bias", [FF], BF16)
         ident_f32 = sbuf("ident_f32", [P], F32)
         ident_bf16 = sbuf("ident_bf16", [P], BF16)
         w_span = {}
@@ -81,7 +85,7 @@ def tile_equivariantfeedforward_pa_kernel(tc, h, x1, pre1, w1_0_bytes, w1_0_scal
         inv_words = sbuf("inv_words", [NT * P * PACK], BF16)
         inv_codes = sbuf("inv_codes", [NT * P], U32)
         inv_scales = sbuf("inv_scales", [NT * P], U8)
-        rows = [sbuf(f"rows{i}", [FF], F32) for i in tiles]
+        rows = [dma_tile(f"rows{i}", [FF], F32) for i in tiles]
 
         def copy_on(engine, dst, src):
             if engine == VECTOR:
@@ -90,7 +94,7 @@ def tile_equivariantfeedforward_pa_kernel(tc, h, x1, pre1, w1_0_bytes, w1_0_scal
                 nc.scalar.copy(out=dst, in_=src)
 
         def load_w(g, half, t0, t1):
-            raw = sbuf(f"w_bytes{g}{half}{t0}", [t1 - t0, HALF], U8)
+            raw = dma_tile(f"w_bytes{g}{half}{t0}", [t1 - t0, HALF], U8)
             nc.sync.dma_start(out=raw[:], in_=w_rows[g][:, t0:t1, half * HALF : (half + 1) * HALF])
             for t in range(t0, t1):
                 w_bytes[g, half, t] = raw[:, t - t0, :]
@@ -108,6 +112,10 @@ def tile_equivariantfeedforward_pa_kernel(tc, h, x1, pre1, w1_0_bytes, w1_0_scal
             nc.vector.quantize_mx(out=codes.bitcast(FP8X4), scales=scales, in_=words)
 
         def widen(engine, g, q0, q1, planes):
+            if (q0, q1) == (2, NQ):
+                widen(engine, g, 2, 3, planes)
+                widen(engine, g, 3, NQ, planes)
+                return
             for t in planes:
                 raw = w_bytes[g, q0 // 2, t][:, q0 % 2 * BANK : (q1 - q0 // 2 * 2) * BANK].bitcast(FP8)
                 span, first = w_span[g, q0]
@@ -124,11 +132,11 @@ def tile_equivariantfeedforward_pa_kernel(tc, h, x1, pre1, w1_0_bytes, w1_0_scal
                 w_wide[g, q] = span[:, :, (q - q0) * BANK : (q - q0 + 1) * BANK]
 
         def wide_late():
-            span = sbuf("w_wide_late", [PACK, 2, HALF], BF16)
+            span = sbuf("w_wide_late", [PACK, 2, BANK], BF16)
             for g in range(2):
-                for q in range(2, NQ):
-                    w_span[g, q] = (span[:, :, g, :], (q - 2) * BANK)
-                    w_wide[g, q] = span[:, :, g, (q - 2) * BANK : (q - 1) * BANK]
+                wide_tile(g, 2, 3)
+                w_span[g, 3] = (span[:, :, g, :], 0)
+                w_wide[g, 3] = span[:, :, g, :]
             return span
 
         def words_of(g, q):
@@ -178,7 +186,7 @@ def tile_equivariantfeedforward_pa_kernel(tc, h, x1, pre1, w1_0_bytes, w1_0_scal
 
         def interleave_last_piece(span):
             nc.gpsimd.tensor_scalar(out=piece_words[1][:].rearrange("p (g n t) -> p g n t", g=2, t=PACK),
-                                    in0=span[:, :, :, HALF - PIECE :].rearrange("p t g n -> p g n t"),
+                                    in0=span[:, :, :, PIECE:].rearrange("p t g n -> p g n t"),
                                     scalar1=1.0, scalar2=0.0, op0=ALU.mult, op1=ALU.add)
 
         def interleave_pre():

@@ -64,14 +64,13 @@ def tile_equivariantfeedforward_pa_kernel(tc, h, x1, pre1, w1_0_bytes, w1_0_scal
         h_raw = [dma_tile(f"h_raw{i}", [D], BF16) for i in tiles]
         x_split = [sbuf(f"x_split{i}", [M1, D], BF16) for i in tiles]
         pre_raw = dma_tile("pre_raw", [PACK, D], BF16)
-        w_scale = sbuf("w_scale", [2, PACK], F32)
+        w_scale = sbuf("w_scale", [2, 2 * PACK], F32)
         bias = dma_tile("bias", [FF], BF16)
         ident_f32 = sbuf("ident_f32", [P], F32)
         ident_bf16 = sbuf("ident_bf16", [P], BF16)
         w_span = {}
         w_wide = {}
         w_words = {}
-        piece_words = {}
         w_pairs = {}
         w_codes = [sbuf(f"w_codes{q}", [2 * BANK], U32) for q in range(NQ)]
         w_scales = [sbuf(f"w_scales{q}", [2 * BANK], U8) for q in range(NQ)]
@@ -85,7 +84,7 @@ def tile_equivariantfeedforward_pa_kernel(tc, h, x1, pre1, w1_0_bytes, w1_0_scal
         inv_words = sbuf("inv_words", [NT * P * PACK], BF16)
         inv_codes = sbuf("inv_codes", [NT * P], U32)
         inv_scales = sbuf("inv_scales", [NT * P], U8)
-        rows = [dma_tile(f"rows{i}", [FF], F32) for i in tiles]
+        rows = dma_tile("rows", [NT, FF], F32)
 
         def copy_on(engine, dst, src):
             if engine == VECTOR:
@@ -112,10 +111,6 @@ def tile_equivariantfeedforward_pa_kernel(tc, h, x1, pre1, w1_0_bytes, w1_0_scal
             nc.vector.quantize_mx(out=codes.bitcast(FP8X4), scales=scales, in_=words)
 
         def widen(engine, g, q0, q1, planes):
-            if (q0, q1) == (2, NQ):
-                widen(engine, g, 2, 3, planes)
-                widen(engine, g, 3, NQ, planes)
-                return
             for t in planes:
                 raw = w_bytes[g, q0 // 2, t][:, q0 % 2 * BANK : (q1 - q0 // 2 * 2) * BANK].bitcast(FP8)
                 span, first = w_span[g, q0]
@@ -130,14 +125,6 @@ def tile_equivariantfeedforward_pa_kernel(tc, h, x1, pre1, w1_0_bytes, w1_0_scal
             for q in range(q0, q1):
                 w_span[g, q] = (span, (q - q0) * BANK)
                 w_wide[g, q] = span[:, :, (q - q0) * BANK : (q - q0 + 1) * BANK]
-
-        def wide_late():
-            span = sbuf("w_wide_late", [PACK, 2, BANK], BF16)
-            for g in range(2):
-                wide_tile(g, 2, 3)
-                w_span[g, 3] = (span[:, :, g, :], 0)
-                w_wide[g, 3] = span[:, :, g, :]
-            return span
 
         def words_of(g, q):
             if (g, q) not in w_words:
@@ -170,7 +157,7 @@ def tile_equivariantfeedforward_pa_kernel(tc, h, x1, pre1, w1_0_bytes, w1_0_scal
 
         def fetch_w(engine, g, q, b):
             width = 2 * P * PACK
-            dst = piece_words[b][:, g * width : (g + 1) * width] if q == NQ - 1 else words_of(g, q)[:, b * width : (b + 1) * width]
+            dst = words_of(g, q)[:, b * width : (b + 1) * width]
             copy_on(engine, dst.bitcast(F32), empty_bank(("w", g, q, b))[:].rearrange("p j c -> p (j c)").bitcast(F32))
 
         def quantise_w(q, g=None, b0=0, b1=2):
@@ -179,15 +166,6 @@ def tile_equivariantfeedforward_pa_kernel(tc, h, x1, pre1, w1_0_bytes, w1_0_scal
             else:
                 c = slice(g * BANK + b0 * PIECE, g * BANK + b1 * PIECE)
                 quantise(w_codes[q][:, c], w_scales[q][:, c], words_of(g, q)[:, b0 * PIECE * PACK : b1 * PIECE * PACK])
-
-        def quantise_piece(b, g0=0, g1=2):
-            c = slice(b * BANK + g0 * PIECE, b * BANK + g1 * PIECE)
-            quantise(w_codes[NQ - 1][:, c], w_scales[NQ - 1][:, c], piece_words[b][:, g0 * PIECE * PACK : g1 * PIECE * PACK])
-
-        def interleave_last_piece(span):
-            nc.gpsimd.tensor_scalar(out=piece_words[1][:].rearrange("p (g n t) -> p g n t", g=2, t=PACK),
-                                    in0=span[:, :, :, PIECE:].rearrange("p t g n -> p g n t"),
-                                    scalar1=1.0, scalar2=0.0, op0=ALU.mult, op1=ALU.add)
 
         def interleave_pre():
             dst = pre_words[:].rearrange("p (r c) t -> p c t r", r=PACK)
@@ -239,9 +217,9 @@ def tile_equivariantfeedforward_pa_kernel(tc, h, x1, pre1, w1_0_bytes, w1_0_scal
                 nc.scalar.activation(out=squares[i, m][:].rearrange("p r c -> p (r c)"), in_=empty_bank(("pm", i, m))[:],
                                      func=ACT.Square)
 
-        def sum_squares(i):
-            total = take_bank(("sum", i), [PACK, P], F32)
-            for m in range(M1):
+        def sum_squares(i, m0=0, m1=M1):
+            total = take_bank(("sum", i), [PACK, P], F32) if m0 == 0 else held["sum", i][0]
+            for m in range(m0, m1):
                 for r in range(PACK):
                     nc.tensor.matmul(total[:, r, :], lhsT=squares[i, m][:, r, :], rhs=ident_f32[:],
                                      start=(m, r) == (0, 0), stop=(m, r) == (M1 - 1, PACK - 1), is_transpose=True)
@@ -259,24 +237,30 @@ def tile_equivariantfeedforward_pa_kernel(tc, h, x1, pre1, w1_0_bytes, w1_0_scal
             q, first = divmod(c0, BANK)
             for g in passes:
                 acc = take_bank(("acc", i, c0), [width], F32, newest=paced) if g == 0 else held["acc", i, c0][0]
-                start = 2 * first + g * width if width == PIECE else g * BANK
-                c = slice(start, start + width)
+                c = slice(g * BANK + first, g * BANK + first + width)
                 nc.tensor.matmul_mx(out=acc[:], lhsT=sides[g][0].bitcast(FP8X4), lhsT_scale=sides[g][1],
                                     rhs=w_codes[q][:, c].bitcast(FP8X4), rhs_scale=w_scales[q][:, c],
                                     start=(g == 0), stop=(g == 1))
 
         def add_bias(i, c0, width=BANK):
             c = slice(c0, c0 + width)
-            nc.vector.tensor_tensor(out=rows[i][:, c], in0=empty_bank(("acc", i, c0))[:], in1=bias[:, c], op=ALU.add)
+            nc.vector.tensor_tensor(out=rows[:, i, c], in0=empty_bank(("acc", i, c0))[:], in1=bias[:, c], op=ALU.add)
 
-        def finish(i, c0, width=BANK):
-            part = rows[i][:, c0 : c0 + width]
+        def silu(i, c0, width=BANK, count=1):
+            part = rows[:, i : i + count, c0 : c0 + width]
             nc.scalar.activation(out=part, in_=part, func=ACT.Silu)
-            nc.sync.dma_start(out=out[i, :, c0 : c0 + width], in_=part)
+
+        def store(i, c0, width=BANK, count=1):
+            nc.sync.dma_start(out=out[i : i + count, :, c0 : c0 + width].rearrange("i p c -> p i c"),
+                              in_=rows[:, i : i + count, c0 : c0 + width])
+
+        def finish(i, c0, width=BANK, count=1):
+            silu(i, c0, width, count)
+            store(i, c0, width, count)
 
         last = NT - 1
         with tc.manual_schedule():
-            nc.scalar.dma_start(out=w_scale[:], in_=w1_0_scale.rearrange("(g p t) o -> p g (t o)", p=P, t=PACK))
+            nc.scalar.dma_start(out=w_scale[:, :, :PACK], in_=w1_0_scale.rearrange("(g p t) o -> p g (t o)", p=P, t=PACK))
             warm = sbuf("warm", [1], F32)
             nc.vector.memset(warm[:], 1.0)
             nc.scalar.activation(out=warm[:], in_=warm[:], func=ACT.Sqrt)
@@ -301,9 +285,8 @@ def tile_equivariantfeedforward_pa_kernel(tc, h, x1, pre1, w1_0_bytes, w1_0_scal
             nc.sync.dma_start(out=bias[:], in_=b1_0.partition_broadcast(P))
             for g in range(2):
                 wide_tile(g, 0, 2)
+                wide_tile(g, 2, NQ)
                 pair_words(g)
-            late = wide_late()
-            piece_words[0] = sbuf("piece_words", [BANK * PACK], BF16)
 
             split_x(0, SCALAR)
             widen(VECTOR, 0, 0, 2, range(1))
@@ -364,8 +347,8 @@ def tile_equivariantfeedforward_pa_kernel(tc, h, x1, pre1, w1_0_bytes, w1_0_scal
             widen(VECTOR, 0, 2, NQ, range(3, PACK))
             quantise_w(1)
             widen(VECTOR, 0, 2, NQ, range(2, 3))
-            widen(VECTOR, 1, 2, 3, range(2, 3))
-            widen(VECTOR, 1, 2, NQ, range(3, PACK))
+            widen(VECTOR, 1, 2, NQ, range(2, PACK))
+            widen(VECTOR, 1, 3, NQ, range(1, 2))
             sum_squares(2)
             root(0)
             square(last, 0, 1)
@@ -378,8 +361,7 @@ def tile_equivariantfeedforward_pa_kernel(tc, h, x1, pre1, w1_0_bytes, w1_0_scal
             root(2)
             sum_squares(last)
             quantise_inv(0, 2)
-            widen(SCALAR, 1, 2, NQ, range(1, 2))
-            widen(SCALAR, 1, 3, NQ, range(2, 3))
+            widen(SCALAR, 1, 2, 3, range(1, 2))
             root(last)
             interleave_w_on_vector(0, 2)
             widen(VECTOR, 1, 2, NQ, range(1))
@@ -388,49 +370,46 @@ def tile_equivariantfeedforward_pa_kernel(tc, h, x1, pre1, w1_0_bytes, w1_0_scal
             for i in range(2):
                 for q in range(2):
                     multiply(i, q * BANK, passes=range(1, 2))
-            multiply(2, 0)
-            add_bias(0, 0)
-            lay_w(0, 3, 0)
-            add_bias(0, BANK)
-            finish(0, 0, HALF)
+            for i in range(2, NT):
+                for q in range(2):
+                    multiply(i, q * BANK, passes=range(1))
             for q in range(2):
-                add_bias(1, q * BANK)
-            finish(1, 0, HALF)
-            lay_w(1, 3, 0)
-            add_bias(2, 0)
-            finish(2, 0)
-            multiply(2, BANK)
-            fetch_w(VECTOR, 0, 3, 0)
+                multiply(2, q * BANK, passes=range(1, 2))
+            for i in range(last):
+                for q in range(2):
+                    add_bias(i, q * BANK)
+                    finish(i, q * BANK)
             quantise_inv(last)
+            for b in range(2):
+                lay_w(0, 3, b)
             for q in range(2):
-                multiply(last, q * BANK)
-            fetch_w(SCALAR, 1, 3, 0)
-            quantise_piece(0, 0, 1)
+                multiply(last, q * BANK, passes=range(1, 2))
             quantise_w(2, 0)
             quantise_w(2, 1)
-            piece_words[1] = sbuf("w_words02", [BANK * PACK], BF16)
-            interleave_last_piece(late)
+            for b in range(2):
+                fetch_w(SCALAR, 0, 3, b)
+            w_words[1, 3] = sbuf("w_words02", [BANK * PACK], BF16)
+            interleave_w_on_gpsimd(1, 3)
             pieces = [(i, FF - BANK + b * PIECE) for b in range(2) for i in tiles]
-            for i in range(2):
+            for i in range(3):
                 multiply(i, HALF)
-            add_bias(2, BANK)
-            finish(2, BANK)
             for q in range(2):
                 add_bias(last, q * BANK)
                 finish(last, q * BANK)
-            for i in range(2, NT):
-                multiply(i, HALF)
             for i in range(last):
                 add_bias(i, HALF)
                 finish(i, HALF)
-                multiply(*pieces[i], PIECE, passes=range(1), paced=True)
-            quantise_piece(0, 1, 2)
+                if i == 0:
+                    multiply(last, HALF, paced=True)
+            quantise_w(3, 0, 0, 1)
+            quantise_w(3, 1, 0, 1)
+            for i, c0 in pieces[:NT]:
+                multiply(i, c0, PIECE)
             add_bias(last, HALF)
             finish(last, HALF)
-            quantise_piece(1)
-            for i, c0 in pieces[:last]:
-                multiply(i, c0, PIECE, passes=range(1, 2))
-            for i, c0 in pieces[last:]:
+            quantise_w(3, 0, 1, 2)
+            quantise_w(3, 1, 1, 2)
+            for i, c0 in pieces[NT:]:
                 multiply(i, c0, PIECE)
             for i, c0 in pieces:
                 add_bias(i, c0, PIECE)

@@ -24,7 +24,8 @@ HALF = FF // 2
 NQ = FF // BANK
 UNITS = M1 + 1
 PSUM_BANKS = 8
-DMA_ALIGN = 256
+DMA_ALIGN = 512
+MX_ALIGN = 256
 RUN = 8
 VECTOR, SCALAR = "vector", "scalar"
 
@@ -72,18 +73,18 @@ def tile_equivariantfeedforward_pa_kernel(tc, h, x1, pre1, w1_0_bytes, w1_0_scal
         w_wide = {}
         w_words = {}
         w_pairs = {}
-        w_codes = [sbuf(f"w_codes{q}", [2 * BANK], U32) for q in range(NQ)]
-        w_scales = [sbuf(f"w_scales{q}", [2 * BANK], U8) for q in range(NQ)]
+        w_codes = [sbuf(f"w_codes{q}", [2 * BANK], U32, MX_ALIGN) for q in range(NQ)]
+        w_scales = [sbuf(f"w_scales{q}", [2 * BANK], U8, MX_ALIGN) for q in range(NQ)]
         pre_words = sbuf("pre_words", [D, PACK], BF16)
-        pre_codes = sbuf("pre_codes", [D], U32)
-        pre_scales = sbuf("pre_scales", [D], U8)
+        pre_codes = sbuf("pre_codes", [D], U32, MX_ALIGN)
+        pre_scales = sbuf("pre_scales", [D], U8, MX_ALIGN)
         xh_words = [sbuf(f"xh_words{i}", [UNITS * P * PACK], BF16) for i in tiles]
-        xh_codes = [sbuf(f"xh_codes{i}", [UNITS * P], U32) for i in tiles]
-        xh_scales = [sbuf(f"xh_scales{i}", [UNITS * P], U8) for i in tiles]
-        squares = {(i, m): sbuf(f"squares{i}{m}", [PACK, P], F32) for i in tiles for m in range(M1)}
+        xh_codes = [sbuf(f"xh_codes{i}", [UNITS * P], U32, MX_ALIGN) for i in tiles]
+        xh_scales = [sbuf(f"xh_scales{i}", [UNITS * P], U8, MX_ALIGN) for i in tiles]
+        squares = {}
         inv_words = sbuf("inv_words", [NT * P * PACK], BF16)
-        inv_codes = sbuf("inv_codes", [NT * P], U32)
-        inv_scales = sbuf("inv_scales", [NT * P], U8)
+        inv_codes = sbuf("inv_codes", [NT * P], U32, MX_ALIGN)
+        inv_scales = sbuf("inv_scales", [NT * P], U8, MX_ALIGN)
         rows = dma_tile("rows", [NT, FF], F32)
 
         def copy_on(engine, dst, src):
@@ -214,6 +215,7 @@ def tile_equivariantfeedforward_pa_kernel(tc, h, x1, pre1, w1_0_bytes, w1_0_scal
 
         def square(i, m0=0, m1=M1):
             for m in range(m0, m1):
+                squares[i, m] = sbuf(f"squares{i % 3}{m}", [PACK, P], F32)
                 nc.scalar.activation(out=squares[i, m][:].rearrange("p r c -> p (r c)"), in_=empty_bank(("pm", i, m))[:],
                                      func=ACT.Square)
 
@@ -264,8 +266,8 @@ def tile_equivariantfeedforward_pa_kernel(tc, h, x1, pre1, w1_0_bytes, w1_0_scal
             warm = sbuf("warm", [1], F32)
             nc.vector.memset(warm[:], 1.0)
             nc.scalar.activation(out=warm[:], in_=warm[:], func=ACT.Sqrt)
-            make_identity(nc, ident_bf16[:])
             make_identity(nc, ident_f32[:])
+            nc.vector.tensor_copy(out=ident_bf16[:], in_=ident_f32[:])
 
             load_x(0)
             load_w(0, 0, 0, 2)

@@ -149,9 +149,9 @@ def tile_equivariantfeedforward_pa_kernel(tc, h, x1, pre1, w1_0_bytes, w1_0_scal
                                     in0=w_wide[g, q][:, :, c0:c1].rearrange("p t n -> p n t"),
                                     scalar1=1.0, scalar2=0.0, op0=ALU.mult, op1=ALU.add)
 
-        def lay_w(g, q, b):
-            laid = take_bank(("w", g, q, b), [2, P * PACK], BF16)
-            for j in range(2):
+        def lay_w(g, q, b, j0=0, j1=2):
+            laid = take_bank(("w", g, q, b), [2, P * PACK], BF16) if j0 == 0 else held["w", g, q, b][0]
+            for j in range(j0, j1):
                 c0 = (2 * b + j) * P
                 nc.tensor.matmul(laid[:, j, :].rearrange("p (n t) -> p t n", t=PACK), lhsT=ident_bf16[:],
                                  rhs=w_wide[g, q][:, :, c0 : c0 + P], start=True, stop=True)
@@ -244,9 +244,11 @@ def tile_equivariantfeedforward_pa_kernel(tc, h, x1, pre1, w1_0_bytes, w1_0_scal
                                     rhs=w_codes[q][:, c].bitcast(FP8X4), rhs_scale=w_scales[q][:, c],
                                     start=(g == 0), stop=(g == 1))
 
-        def add_bias(i, c0, width=BANK):
-            c = slice(c0, c0 + width)
-            nc.vector.tensor_tensor(out=rows[:, i, c], in0=empty_bank(("acc", i, c0))[:], in1=bias[:, c], op=ALU.add)
+        def add_bias(i, c0, width=BANK, first=0, end=None):
+            end = end or width
+            acc = empty_bank(("acc", i, c0)) if end == width else held["acc", i, c0][0]
+            c = slice(c0 + first, c0 + end)
+            nc.vector.tensor_tensor(out=rows[:, i, c], in0=acc[:, first:end], in1=bias[:, c], op=ALU.add)
 
         def silu(i, c0, width=BANK, count=1):
             part = rows[:, i : i + count, c0 : c0 + width]
@@ -382,18 +384,20 @@ def tile_equivariantfeedforward_pa_kernel(tc, h, x1, pre1, w1_0_bytes, w1_0_scal
                     add_bias(i, q * BANK)
                     finish(i, q * BANK)
             quantise_inv(last)
-            for b in range(2):
-                lay_w(0, 3, b)
+            lay_w(0, 3, 0)
+            lay_w(0, 3, 1, 0, 1)
             for q in range(2):
                 multiply(last, q * BANK, passes=range(1, 2))
             quantise_w(2, 0)
             quantise_w(2, 1)
-            for b in range(2):
-                fetch_w(SCALAR, 0, 3, b)
+            fetch_w(SCALAR, 0, 3, 0)
             w_words[1, 3] = sbuf("w_words02", [BANK * PACK], BF16)
             interleave_w_on_gpsimd(1, 3)
             pieces = [(i, FF - BANK + b * PIECE) for b in range(2) for i in tiles]
-            for i in range(3):
+            for i in range(4):
+                multiply(i, HALF)
+            lay_w(0, 3, 1, 1, 2)
+            for i in range(4, NT):
                 multiply(i, HALF)
             for q in range(2):
                 add_bias(last, q * BANK)
@@ -401,16 +405,17 @@ def tile_equivariantfeedforward_pa_kernel(tc, h, x1, pre1, w1_0_bytes, w1_0_scal
             for i in range(last):
                 add_bias(i, HALF)
                 finish(i, HALF)
-                if i == 0:
-                    multiply(last, HALF, paced=True)
+                if i == 1:
+                    fetch_w(SCALAR, 0, 3, 1)
+            add_bias(last, HALF, end=PIECE)
             quantise_w(3, 0, 0, 1)
             quantise_w(3, 1, 0, 1)
             for i, c0 in pieces[:NT]:
                 multiply(i, c0, PIECE)
-            add_bias(last, HALF)
+            add_bias(last, HALF, first=PIECE)
             finish(last, HALF)
-            quantise_w(3, 0, 1, 2)
             quantise_w(3, 1, 1, 2)
+            quantise_w(3, 0, 1, 2)
             for i, c0 in pieces[NT:]:
                 multiply(i, c0, PIECE)
             for i, c0 in pieces:

from contextlib import ExitStack

import concourse.mybir as mybir
from concourse.masks import make_identity

F32 = mybir.dt.float32
BF16 = mybir.dt.bfloat16
U8 = mybir.dt.uint8
U32 = mybir.dt.uint32
FP8 = mybir.dt.float8_e4m3fn
FP8X4 = mybir.dt.float8_e4m3fn_x4
ACT = mybir.ActivationFunctionType
ALU = mybir.AluOpType

P = 128
PACK = 4
D = 512
M1 = 3
FF = 2048
NT = 4
BANK = 512
PIECE = BANK // 2
HALF = FF // 2
NQ = FF // BANK
UNITS = M1 + 1
PSUM_BANKS = 8
DMA_ALIGN = 512
MX_ALIGN = 256
RUN = 8
VECTOR, SCALAR = "vector", "scalar"

FLOPS = 2 * NT * P * M1 * D * D + 2 * NT * P * 2 * D * FF


def tile_equivariantfeedforward_pa_kernel(tc, h, x1, pre1, w1_0_bytes, w1_0_scale, b1_0, out):
    nc = tc.nc
    with ExitStack() as ctx:
        keep = ctx.enter_context(tc.tile_pool(name="keep", bufs=1))
        psum = ctx.enter_context(tc.psum_pool(name="psum", bufs=1))

        def sbuf(name, shape, dtype, align=64):
            return keep.tile([P] + shape, dtype, name=name, align_bytes=align)

        def dma_tile(name, shape, dtype):
            return sbuf(name, shape, dtype, DMA_ALIGN)

        free_banks = list(range(PSUM_BANKS))
        held = {}

        def take_bank(key, shape, dtype, newest=False):
            n = free_banks[-1 if newest else 0]
            free_banks.remove(n)
            held[key] = (psum.tile([P] + shape, dtype, name=f"bank{n}"), n)
            return held[key][0]

        def empty_bank(key):
            tile, n = held[key]
            free_banks.append(n)
            return tile

        tiles = range(NT)
        w_rows = w1_0_bytes.rearrange("(g p t) n -> g p t n", p=P, t=PACK)
        w_bytes = {}
        x_raw = [dma_tile(f"x_raw{i}", [D * M1], BF16) for i in tiles]
        h_raw = [dma_tile(f"h_raw{i}", [D], BF16) for i in tiles]
        x_split = [sbuf(f"x_split{i}", [M1, D], BF16) for i in tiles]
        pre_raw = dma_tile("pre_raw", [PACK, D], BF16)
        w_scale = sbuf("w_scale", [2, 2 * PACK], F32)
        bias = dma_tile("bias", [FF], BF16)
        ident_f32 = sbuf("ident_f32", [P], F32)
        ident_bf16 = sbuf("ident_bf16", [P], BF16)
        w_span = {}
        w_wide = {}
        w_words = {}
        w_pairs = {}
        w_codes = [sbuf(f"w_codes{q}", [2 * BANK], U32, MX_ALIGN) for q in range(NQ)]
        w_scales = [sbuf(f"w_scales{q}", [2 * BANK], U8, MX_ALIGN) for q in range(NQ)]
        pre_words = sbuf("pre_words", [D, PACK], BF16)
        pre_codes = sbuf("pre_codes", [D], U32, MX_ALIGN)
        pre_scales = sbuf("pre_scales", [D], U8, MX_ALIGN)
        xh_words = [sbuf(f"xh_words{i}", [UNITS * P * PACK], BF16) for i in tiles]
        xh_codes = [sbuf(f"xh_codes{i}", [UNITS * P], U32, MX_ALIGN) for i in tiles]
        xh_scales = [sbuf(f"xh_scales{i}", [UNITS * P], U8, MX_ALIGN) for i in tiles]
        squares = {}
        inv_words = sbuf("inv_words", [NT * P * PACK], BF16)
        inv_codes = sbuf("inv_codes", [NT * P], U32, MX_ALIGN)
        inv_scales = sbuf("inv_scales", [NT * P], U8, MX_ALIGN)
        rows = dma_tile("rows", [NT, FF], F32)

        def copy_on(engine, dst, src):
            if engine == VECTOR:
                nc.vector.tensor_copy(out=dst, in_=src)
            else:
                nc.scalar.copy(out=dst, in_=src)

        def load_w(g, half, t0, t1):
            raw = dma_tile(f"w_bytes{g}{half}{t0}", [t1 - t0, HALF], U8)
            nc.sync.dma_start(out=raw[:], in_=w_rows[g][:, t0:t1, half * HALF : (half + 1) * HALF])
            for t in range(t0, t1):
                w_bytes[g, half, t] = raw[:, t - t0, :]

        def load_x(i):
            nc.sync.dma_start(out=x_raw[i][:], in_=x1[i].rearrange("n d m -> n (d m)"))

        def load_h(i):
            nc.sync.dma_start(out=h_raw[i][:], in_=h[i])

        def load_pre():
            nc.sync.dma_start(out=pre_raw[:], in_=pre1.rearrange("(p t) e -> p t e", t=PACK))

        def quantise(codes, scales, words):
            nc.vector.quantize_mx(out=codes.bitcast(FP8X4), scales=scales, in_=words)

        def widen(engine, g, q0, q1, planes):
            for t in planes:
                raw = w_bytes[g, q0 // 2, t][:, q0 % 2 * BANK : (q1 - q0 // 2 * 2) * BANK].bitcast(FP8)
                span, first = w_span[g, q0]
                dst, scale = span[:, t, first : first + (q1 - q0) * BANK], w_scale[:, g, t : t + 1]
                if engine == VECTOR:
                    nc.vector.tensor_scalar(out=dst, in0=raw, scalar1=scale, scalar2=None, op0=ALU.mult)
                else:
                    nc.scalar.activation(out=dst, in_=raw, func=ACT.Copy, scale=scale)

        def wide_tile(g, q0, q1):
            span = sbuf(f"w_wide{g}{q0}", [PACK, (q1 - q0) * BANK], BF16)
            for q in range(q0, q1):
                w_span[g, q] = (span, (q - q0) * BANK)
                w_wide[g, q] = span[:, :, (q - q0) * BANK : (q - q0 + 1) * BANK]

        def words_of(g, q):
            if (g, q) not in w_words:
                w_words[g, q] = sbuf(f"w_words{g}{q}", [BANK * PACK], BF16)
            return w_words[g, q]

        def pair_words(q):
            both = sbuf(f"w_words{q}", [2 * BANK * PACK], BF16)
            w_pairs[q] = both
            for g in range(2):
                w_words[g, q] = both[:, g * BANK * PACK : (g + 1) * BANK * PACK]

        def interleave_w_on_vector(g, q, b0=0, b1=2):
            c0, c1 = b0 * 2 * P, b1 * 2 * P
            nc.vector.tensor_copy(out=words_of(g, q)[:, c0 * PACK : c1 * PACK].rearrange("p (c i t) -> p c t i", i=RUN, t=PACK),
                                  in_=w_wide[g, q][:, :, c0:c1].rearrange("p t (c i) -> p c t i", i=RUN))

        def interleave_w_on_gpsimd(g, q, b0=0, b1=2):
            c0, c1 = b0 * 2 * P, b1 * 2 * P
            nc.gpsimd.tensor_scalar(out=words_of(g, q)[:, c0 * PACK : c1 * PACK].rearrange("p (n t) -> p n t", t=PACK),
                                    in0=w_wide[g, q][:, :, c0:c1].rearrange("p t n -> p n t"),
                                    scalar1=1.0, scalar2=0.0, op0=ALU.mult, op1=ALU.add)

        def lay_w(g, q, b, j0=0, j1=2):
            laid = take_bank(("w", g, q, b), [2, P * PACK], BF16) if j0 == 0 else held["w", g, q, b][0]
            for j in range(j0, j1):
                c0 = (2 * b + j) * P
                nc.tensor.matmul(laid[:, j, :].rearrange("p (n t) -> p t n", t=PACK), lhsT=ident_bf16[:],
                                 rhs=w_wide[g, q][:, :, c0 : c0 + P], start=True, stop=True)

        def fetch_w(engine, g, q, b):
            width = 2 * P * PACK
            dst = words_of(g, q)[:, b * width : (b + 1) * width]
            copy_on(engine, dst.bitcast(F32), empty_bank(("w", g, q, b))[:].rearrange("p j c -> p (j c)").bitcast(F32))

        def quantise_w(q, g=None, b0=0, b1=2):
            if g is None:
                quantise(w_codes[q][:], w_scales[q][:], w_pairs[q][:])
            else:
                c = slice(g * BANK + b0 * PIECE, g * BANK + b1 * PIECE)
                quantise(w_codes[q][:, c], w_scales[q][:, c], words_of(g, q)[:, b0 * PIECE * PACK : b1 * PIECE * PACK])

        def interleave_pre():
            dst = pre_words[:].rearrange("p (r c) t -> p c t r", r=PACK)
            src = pre_raw[:].rearrange("p t (c r) -> p c t r", r=PACK)
            nc.vector.tensor_copy(out=dst[:, :, :, : PACK - 1], in_=src[:, :, :, : PACK - 1])
            nc.scalar.copy(out=dst[:, :, :, PACK - 1 :], in_=src[:, :, :, PACK - 1 :])

        def quantise_pre():
            quantise(pre_codes[:], pre_scales[:], pre_words[:].rearrange("p e t -> p (e t)"))

        def split_x(i, engine=VECTOR, between=None):
            dst = x_split[i][:].rearrange("p m (u c e) -> p m c u e", u=2, e=2)
            src = x_raw[i][:].rearrange("p (c u e m) -> p m c u e", u=2, e=2, m=M1)
            nc.vector.tensor_copy(out=dst[:, :2], in_=src[:, :2])
            if between:
                between()
            copy_on(engine, dst[:, 2], src[:, 2])

        def turn_xh(i):
            for b in range(2):
                turned = take_bank(("xh", i, b), [2, 2, P], F32)
                for j in range(2):
                    m = 2 * b + j
                    for u in range(2):
                        if m < M1:
                            words = x_split[i][:, m, :].bitcast(F32)[:, u * P : (u + 1) * P]
                        else:
                            words = h_raw[i][:].bitcast(F32)[:, u : D // 2 : 2]
                        nc.tensor.transpose(turned[:, j, u, :], words, ident_f32[:])

        def fetch_xh(i, engines=(SCALAR, SCALAR)):
            for b in range(2):
                dst = xh_words[i][:, b * 2 * P * PACK : (b + 1) * 2 * P * PACK].bitcast(F32)
                copy_on(engines[b], dst.rearrange("p (j n a u) -> p j n u a", j=2, a=2, u=2),
                        empty_bank(("xh", i, b))[:].rearrange("p j u (n a) -> p j n u a", a=2))

        def quantise_xh(i):
            quantise(xh_codes[i][:], xh_scales[i][:], xh_words[i][:])

        def project(i, m0=0, m1=M1):
            for m in range(m0, m1):
                pm = take_bank(("pm", i, m), [BANK], F32)
                c = slice(m * P, (m + 1) * P)
                nc.tensor.matmul_mx(out=pm[:], lhsT=xh_codes[i][:, c].bitcast(FP8X4), lhsT_scale=xh_scales[i][:, c],
                                    rhs=pre_codes[:].bitcast(FP8X4), rhs_scale=pre_scales[:], start=True, stop=True)

        def square(i, m0=0, m1=M1):
            for m in range(m0, m1):
                squares[i, m] = sbuf(f"squares{i % 3}{m}", [PACK, P], F32)
                nc.scalar.activation(out=squares[i, m][:].rearrange("p r c -> p (r c)"), in_=empty_bank(("pm", i, m))[:],
                                     func=ACT.Square)

        def sum_squares(i, m0=0, m1=M1):
            total = take_bank(("sum", i), [PACK, P], F32) if m0 == 0 else held["sum", i][0]
            for m in range(m0, m1):
                for r in range(PACK):
                    nc.tensor.matmul(total[:, r, :], lhsT=squares[i, m][:, r, :], rhs=ident_f32[:],
                                     start=(m, r) == (0, 0), stop=(m, r) == (M1 - 1, PACK - 1), is_transpose=True)

        def root(i):
            nc.scalar.activation(out=inv_words[:, i * D : (i + 1) * D].rearrange("p (n a r) -> p n r a", a=2, r=PACK),
                                 in_=empty_bank(("sum", i))[:].rearrange("p r (n a) -> p n r a", a=2), func=ACT.Sqrt)

        def quantise_inv(i, count=1):
            c = slice(i * P, (i + count) * P)
            quantise(inv_codes[:, c], inv_scales[:, c], inv_words[:, i * D : (i + count) * D])

        def multiply(i, c0, width=BANK, passes=range(2), paced=False):
            sides = [(xh_codes[i][:, M1 * P :], xh_scales[i][:, M1 * P :]), (inv_codes[:, i * P : (i + 1) * P], inv_scales[:, i * P : (i + 1) * P])]
            q, first = divmod(c0, BANK)
            for g in passes:
                acc = take_bank(("acc", i, c0), [width], F32, newest=paced) if g == 0 else held["acc", i, c0][0]
                c = slice(g * BANK + first, g * BANK + first + width)
                nc.tensor.matmul_mx(out=acc[:], lhsT=sides[g][0].bitcast(FP8X4), lhsT_scale=sides[g][1],
                                    rhs=w_codes[q][:, c].bitcast(FP8X4), rhs_scale=w_scales[q][:, c],
                                    start=(g == 0), stop=(g == 1))

        def add_bias(i, c0, width=BANK, first=0, end=None):
            end = end or width
            acc = empty_bank(("acc", i, c0)) if end == width else held["acc", i, c0][0]
            c = slice(c0 + first, c0 + end)
            nc.vector.tensor_tensor(out=rows[:, i, c], in0=acc[:, first:end], in1=bias[:, c], op=ALU.add)

        def silu(i, c0, width=BANK, count=1):
            part = rows[:, i : i + count, c0 : c0 + width]
            nc.scalar.activation(out=part, in_=part, func=ACT.Silu)

        def store(i, c0, width=BANK, count=1):
            nc.sync.dma_start(out=out[i : i + count, :, c0 : c0 + width].rearrange("i p c -> p i c"),
                              in_=rows[:, i : i + count, c0 : c0 + width])

        def finish(i, c0, width=BANK, count=1):
            silu(i, c0, width, count)
            store(i, c0, width, count)

        last = NT - 1
        with tc.manual_schedule():
            nc.scalar.dma_start(out=w_scale[:, :, :PACK], in_=w1_0_scale.rearrange("(g p t) o -> p g (t o)", p=P, t=PACK))
            warm = sbuf("warm", [1], F32)
            nc.vector.memset(warm[:], 1.0)
            nc.scalar.activation(out=warm[:], in_=warm[:], func=ACT.Sqrt)
            make_identity(nc, ident_f32[:])
            nc.vector.tensor_copy(out=ident_bf16[:], in_=ident_f32[:])

            load_x(0)
            load_w(0, 0, 0, 2)
            load_w(0, 0, 2, PACK)
            load_h(0)
            load_pre()
            load_x(1)
            load_h(1)
            load_w(1, 0, 0, 2)
            for i in range(2, NT):
                load_x(i)
            for i in range(2, NT):
                load_h(i)
            load_w(1, 0, 2, PACK)
            for g in range(2):
                load_w(g, 1, 0, PACK)
            nc.sync.dma_start(out=bias[:], in_=b1_0.partition_broadcast(P))
            for g in range(2):
                wide_tile(g, 0, 2)
                wide_tile(g, 2, NQ)
                pair_words(g)

            split_x(0, SCALAR)
            widen(VECTOR, 0, 0, 2, range(1))
            widen(SCALAR, 0, 0, 2, range(1, 2))
            widen(VECTOR, 0, 0, 1, range(2, PACK))
            widen(SCALAR, 0, 1, 2, range(2, 3))
            widen(VECTOR, 0, 1, 2, range(3, PACK))
            turn_xh(0)
            fetch_xh(0)
            for q in range(2):
                lay_w(0, q, 0)
            interleave_w_on_vector(0, 0, 1, 2)
            interleave_pre()
            split_x(1, SCALAR)
            quantise_xh(0)
            quantise_pre()
            fetch_w(SCALAR, 0, 0, 0)
            widen(SCALAR, 1, 0, 1, range(1))
            fetch_w(SCALAR, 0, 1, 0)
            turn_xh(1)
            project(0, 0, 1)
            lay_w(0, 1, 1)
            project(0, 1, 2)
            fetch_xh(1)
            split_x(2)
            split_x(last)
            widen(VECTOR, 1, 0, 2, range(1, 2))
            widen(VECTOR, 1, 1, 2, range(1))
            turn_xh(2)
            project(0, 2, M1)
            square(0, 0, 1)
            fetch_w(SCALAR, 0, 1, 1)
            square(0, 1, 2)
            fetch_xh(2)
            quantise_xh(1)
            turn_xh(last)
            widen(VECTOR, 1, 0, 2, range(2, PACK))
            project(1, 0, 1)
            fetch_xh(last)
            square(0, 2, M1)
            lay_w(1, 0, 1)
            project(1, 1, M1)
            widen(VECTOR, 0, 2, NQ, range(1))
            interleave_w_on_vector(1, 0, 0, 1)
            quantise_xh(2)
            square(1, 0, 1)
            fetch_w(SCALAR, 1, 0, 1)
            sum_squares(0)
            square(1, 1, M1)
            project(2)
            interleave_w_on_vector(1, 1)
            quantise_xh(last)
            sum_squares(1)
            project(last)
            square(2)
            widen(VECTOR, 0, 2, NQ, range(1, 2))
            quantise_w(0)
            widen(VECTOR, 0, 2, NQ, range(3, PACK))
            quantise_w(1)
            widen(VECTOR, 0, 2, NQ, range(2, 3))
            widen(VECTOR, 1, 2, NQ, range(2, PACK))
            widen(VECTOR, 1, 3, NQ, range(1, 2))
            sum_squares(2)
            root(0)
            square(last, 0, 1)
            root(1)
            for i in range(2):
                multiply(i, 0, passes=range(1))
            square(last, 1, M1)
            for i in range(2):
                multiply(i, BANK, passes=range(1))
            root(2)
            sum_squares(last)
            quantise_inv(0, 2)
            widen(SCALAR, 1, 2, 3, range(1, 2))
            root(last)
            interleave_w_on_vector(0, 2)
            widen(VECTOR, 1, 2, NQ, range(1))
            quantise_inv(2)
            interleave_w_on_gpsimd(1, 2)
            for i in range(2):
                for q in range(2):
                    multiply(i, q * BANK, passes=range(1, 2))
            for i in range(2, NT):
                for q in range(2):
                    multiply(i, q * BANK, passes=range(1))
            for q in range(2):
                multiply(2, q * BANK, passes=range(1, 2))
            for i in range(last):
                for q in range(2):
                    add_bias(i, q * BANK)
                    finish(i, q * BANK)
            quantise_inv(last)
            lay_w(0, 3, 0)
            lay_w(0, 3, 1, 0, 1)
            for q in range(2):
                multiply(last, q * BANK, passes=range(1, 2))
            quantise_w(2, 0)
            quantise_w(2, 1)
            fetch_w(SCALAR, 0, 3, 0)
            w_words[1, 3] = sbuf("w_words02", [BANK * PACK], BF16)
            interleave_w_on_gpsimd(1, 3)
            pieces = [(i, FF - BANK + b * PIECE) for b in range(2) for i in tiles]
            for i in range(4):
                multiply(i, HALF)
            lay_w(0, 3, 1, 1, 2)
            for i in range(4, NT):
                multiply(i, HALF)
            for q in range(2):
                add_bias(last, q * BANK)
                finish(last, q * BANK)
            for i in range(last):
                add_bias(i, HALF)
                finish(i, HALF)
                if i == 1:
                    fetch_w(SCALAR, 0, 3, 1)
            add_bias(last, HALF, end=PIECE)
            quantise_w(3, 0, 0, 1)
            quantise_w(3, 1, 0, 1)
            for i, c0 in pieces[:NT]:
                multiply(i, c0, PIECE)
            add_bias(last, HALF, first=PIECE)
            finish(last, HALF)
            quantise_w(3, 1, 1, 2)
            quantise_w(3, 0, 1, 2)
            for i, c0 in pieces[NT:]:
                multiply(i, c0, PIECE)
            for i, c0 in pieces:
                add_bias(i, c0, PIECE)
                finish(i, c0, PIECE)
